import numpy as np
import ml_dtypes


def mxq(x, axis, fmt="e4m3"):
    dtype, down = {"e4m3": (ml_dtypes.float8_e4m3fn, 7), "e5m2": (ml_dtypes.float8_e5m2, 14)}[fmt]
    v = np.moveaxis(np.asarray(x, np.float32).astype(ml_dtypes.bfloat16).astype(np.float64), axis, -1)
    blocks = v.reshape(v.shape[:-1] + (-1, 32))
    amax = np.abs(blocks).max(-1, keepdims=True)
    byte = np.maximum(np.where(amax > 0, np.frexp(amax)[1] - 1 + 127, 0) - down, 1)
    scale = np.exp2(byte - 127.0)
    codes = (blocks / scale).astype(np.float32).astype(dtype).astype(np.float64)
    return np.moveaxis((codes * scale).reshape(v.shape), -1, axis)


WIDE = False


def mx_kscale(k):
    if not WIDE:
        return np.ones(k)
    levels = np.array([18, -18])
    if k % 512:
        return np.exp2(np.random.permutation(np.resize(levels, k // 32))).repeat(32)
    a = np.empty((k // 512, 16))
    for p in range(k // 512):
        a[p, :8] = np.random.permutation(np.resize(levels, 8))
        for g in range(8):
            far = levels[np.abs(levels - a[p, g]) >= 10]
            a[p, g + 8] = far[np.random.randint(len(far))]
    return np.exp2(a.ravel()).repeat(32)


BF16 = ml_dtypes.bfloat16


def bf(x):
    return np.asarray(x, np.float32).astype(BF16)


def f64(x):
    return np.asarray(x).astype(np.float64)


B, S, DIM, H, NOPE, ROPE, VHD, KV_RANK = 2, 256, 2048, 16, 128, 64, 128, 512
QKHD = NOPE + ROPE
HALF = ROPE // 2
EPS = 1e-5
T = B * S
HN, HR, HV = H * NOPE, H * ROPE, H * VHD


def rope(u, cos, sin):
    ur = u.reshape(u.shape[:-1] + (HALF, 2))
    a, b = ur[..., 0], ur[..., 1]
    c = cos[None, :, None, :]
    s = sin[None, :, None, :]
    return np.stack([a * c - b * s, a * s + b * c], axis=-1).reshape(u.shape)


def rope_back(g, cos, sin):
    gr = g.reshape(g.shape[:-1] + (HALF, 2))
    p, q = gr[..., 0], gr[..., 1]
    c = cos[None, :, None, :]
    s = sin[None, :, None, :]
    return np.stack([p * c + q * s, q * c - p * s], axis=-1).reshape(g.shape)


def setup_inputs():
    s = mx_kscale(T).reshape(B, S, 1)
    u = mx_kscale(HN + HV)
    v = mx_kscale(HR + KV_RANK)
    vr = v[:HR] / np.max(v[:HR])
    vc = v[HR:] / np.min(v[HR:])
    vw = np.concatenate([vr, vc])
    f0 = np.concatenate([u[:HN], vr]).reshape(H, QKHD)
    f1 = u[HN:].reshape(H, VHD)
    inv_freq = 1.0 / 10000.0 ** (np.arange(0, ROPE, 2) / ROPE)
    ang = np.arange(S)[:, None] * inv_freq[None, :]
    x0 = bf(np.random.standard_normal((B, S, DIM)))
    wa0 = bf(np.random.standard_normal((DIM, KV_RANK + HR)) / np.sqrt(DIM))
    ba = bf(np.random.standard_normal(KV_RANK + HR) * 0.2)
    kvn_g = bf(1.0 + 0.1 * np.random.standard_normal(KV_RANK))
    kvn_b = bf(0.1 * np.random.standard_normal(KV_RANK))
    wk0 = bf(np.random.standard_normal((KV_RANK, HN)) / np.sqrt(KV_RANK))
    wk_b = bf(np.random.standard_normal(HN) * 0.2)
    wv0 = bf(np.random.standard_normal((KV_RANK, HV)) / np.sqrt(KV_RANK))
    wv_b = bf(np.random.standard_normal(HV) * 0.2)
    g0 = np.random.standard_normal((B, S, H, QKHD)) * np.exp2(np.random.randint(-6, 1, (B, S, 1, 1)))
    g1 = np.random.standard_normal((B, S, H, VHD)) * np.exp2(np.random.randint(-6, 1, (B, S, 1, 1)))
    c = (f64(x0) @ f64(wa0) + f64(ba))[..., HR:]
    mu = c.mean(-1, keepdims=True)
    rstd = 1.0 / np.sqrt(np.square(c - mu).mean(-1, keepdims=True) + EPS)
    return {"x": bf(f64(x0) * s),
            "wkv_a_w": bf(f64(wa0) / vw),
            "wkv_a_b": ba,
            "kvn_g": kvn_g,
            "kvn_b": kvn_b,
            "wk_w": bf(f64(wk0) / u[:HN]),
            "wk_b": wk_b,
            "wv_w": bf(f64(wv0) / u[HN:]),
            "wv_b": wv_b,
            "cos": bf(np.cos(ang)), "sin": bf(np.sin(ang)),
            "c_lat": np.asarray(c, np.float32),
            "mu": np.asarray(mu, np.float32),
            "rstd": np.asarray(rstd, np.float32),
            "grad_0": bf(g0 * f0 / s[..., None]),
            "grad_1": bf(g1 * f1 / s[..., None])}


def reference(x, wkv_a_w, wkv_a_b, kvn_g, kvn_b, wk_w, wk_b, wv_w, wv_b, cos, sin, c_lat, mu, rstd, grad_0, grad_1):
    g0 = f64(grad_0)
    dk = np.concatenate([g0[..., :NOPE], rope_back(g0[..., NOPE:], f64(cos), f64(sin))], axis=-1).reshape(T, H * QKHD)
    dk_rope = dk[:, HN:]
    dz2 = np.concatenate([dk[:, :HN], f64(grad_1).reshape(T, HV)], axis=1)
    w2 = np.concatenate([f64(wk_w), f64(wv_w)], axis=1)
    dcn = mxq(dz2, 1, "e5m2") @ mxq(w2, 1, "e4m3").T
    r = f64(rstd).reshape(T, 1)
    xhat = (f64(c_lat).reshape(T, KV_RANK) - f64(mu).reshape(T, 1)) * r
    e = dcn * f64(kvn_g)
    dc = r * (e - e.mean(-1, keepdims=True) - xhat * (e * xhat).mean(-1, keepdims=True))
    dz1 = np.concatenate([dk_rope, dc], axis=1)
    dx = mxq(dz1, 1, "e5m2") @ mxq(f64(wkv_a_w), 1, "e4m3").T
    dw = mxq(f64(x).reshape(T, DIM), 0, "e4m3").T @ mxq(dz1, 0, "e5m2")
    return dx.reshape(B, S, DIM), dw

@@ -1,0 +1,403 @@
+from contextlib import ExitStack
+
+import concourse.mybir as mybir
+from concourse.masks import make_identity
+
+F32 = mybir.dt.float32
+BF16 = mybir.dt.bfloat16
+U32 = mybir.dt.uint32
+U8 = mybir.dt.uint8
+E4M3 = mybir.dt.float8_e4m3fn_x4
+E5M2 = mybir.dt.float8_e5m2_x4
+MULT = mybir.AluOpType.mult
+ADD = mybir.AluOpType.add
+SUB = mybir.AluOpType.subtract
+
+TOKENS, DIM, RANK, HEADS, HEAD = 512, 2048, 512, 16, 192
+NOPE, ROPE = 2048, 1024
+FEATURES = 4096
+WIDTH = ROPE + RANK
+FLOPS = 2 * (TOKENS * FEATURES * RANK + 2 * TOKENS * WIDTH * DIM)
+BYTES = (
+    2 * (TOKENS * DIM + DIM * WIDTH + RANK * FEATURES + TOKENS * (FEATURES + ROPE) + 256 * 64 + RANK)
+    + 4 * (TOKENS * RANK + 2 * TOKENS)
+    + 4 * (TOKENS * DIM + DIM * WIDTH)
+)
+
+INPUT_BUFS = 10
+OUT_BUFS = 6
+SPLIT_BUFS = 3
+DZ2_BUFS = 3
+TURNED_BUFS = 3
+TURN_BANKS = 4
+PRODUCT_BANKS = 3
+
+LOADS = [
+    "t", "g 0", "w 4", "g 2", "w 5", "w 6", "w 7", "g 1", "w 0", "k 5", "s", "x 0", "g 3", "w 1",
+    "w 2", "w 3", "a 0", "x 1", "k 12", "a 2", "k 2", "c", "a 1", "x 3", "a 3", "k 1", "x 2", "k 0",
+    "k 3", "k 7", "k 10", "k 6", "k 4", "k 15", "k 13", "k 14", "k 11", "k 8", "k 9",
+]
+
+STEPS = [
+    ("W 4", "SS", ["tables", "turn 0", "sum 0", "turn 2", "sum 2"], []),
+    ("W 5", "SS", ["turn 1"], []),
+    ("Z 2 0", "SS", [], []),
+    ("W 6", "SS", [], ["gain S"]),
+    ("W 7", "SS", ["sum 1", "xlay 0 S"], []),
+    ("Z 0 0", "VS", ["turn 3"], []),
+    ("F 0", "SS", ["xquant 0"], []),
+    ("W 0", "SS", [], []),
+    ("W 1", "SS", ["sum 3"], []),
+    ("W 2", "SS", [], []),
+    ("Z 0 1", "SS", [], []),
+    ("W 3", "SS", ["xlay 1 V"], []),
+    ("Z 2 1", "SS", ["xhat 0", "split 5 V"], []),
+    ("Z 1 0", "SS", ["zlay 1 S", "xquant 1", "xhat 2", "norm1 0"], ["dh 0"]),
+    ("Z 1 1", "SV", ["split 12 V", "zquant 1", "zlay 0 S"], []),
+    ("Z 3 0", "SS", ["zquant 0", "norm1 2", "norm2 0", "norm2 2", "norm3 0", "xlay 2 S", "norm3 2"], ["dh 2"]),
+    ("", "", ["xquant 2", "xlay 3 V"], []),
+    ("K 0 0", "SS", [], ["A 4 S S", "dh 1"]),
+    ("Z 3 1", "SS", ["xquant 3", "xhat 1", "norm1 1", "norm4 0"], ["A 5 S S"]),
+    ("K 0 1", "SS", [], []),
+    ("K 0 2", "SS", ["norm2 1"], ["A 8 S S"]),
+    ("", "", ["norm1 3"], ["dh 3", "A 0 S S"]),
+    ("K 1 0", "SS", ["xhat 3", "norm4 2", "norm2 3"], ["A 6 S V", "A 12 V S"]),
+    ("K 1 1", "VS", ["norm3 1"], ["A 7 V S", "A 13 S S"]),
+    ("K 2 0", "VS", ["norm3 3"], ["A 1 V S", "A 9 S S"]),
+    ("F 1", "SS", ["norm4 1"], ["A 2 V V", "A 10 S V"]),
+    ("K 3 0", "SS", ["norm4 3"], []),
+    ("K 2 1", "VS", ["zlay 2 V"], ["A 3 S S", "A 11 S S"]),
+    ("D", "VS", ["zquant 2"], ["A 14 S V", "A 15 V S"]),
+    ("K 2 2", "SS", [], []),
+    ("K 1 2", "SV", [], ["l 0 S", "l 1 S", "l 2 V"]),
+    ("K 3 1", "SV", [], ["l 3 S", "l 4 S", "l 5 V"]),
+    ("K 3 2", "SS", [], ["l 6 S", "l 7 V"]),
+    ("", "", [], ["o 0 3 S", "o 1 3 S", "l 8 V", "l 9 V", "o 1 1 S", "l 10 V", "o 0 1 S", "l 11 V", "o 2 3 S", "l 12 V", "l 13 S", "o 3 3 V", "o 0 2 V", "o 1 2 S", "o 2 1 V", "l 14 V", "l 15 S", "o 1 0 V", "o 0 0 S", "o 2 0 V", "o 3 0 S", "o 3 1 S", "o 3 2 S", "o 2 2 S"]),
+    ("", "", [], []),
+]
+
+
+def tile_mla_pa_v_kernel(
+    tc, x, wkv_a_w, wkv_a_b, kvn_g, kvn_b, wk_w, wk_b, wv_w, wv_b, cos, sin, c_lat, mu, rstd, grad_0, grad_1, out_0, out_1
+):
+    nc = tc.nc
+    x_rows = x.flatten_outer_dims().rearrange("(p j) w -> p j w", j=4)
+    grad_0_rows = grad_0.rearrange("b s h d -> (b s) (h d)").rearrange("(p j) w -> p j w", j=4)
+    grad_1_rows = grad_1.rearrange("b s h d -> (b s) (h d)").rearrange("(p j) w -> p j w", j=4)
+    c_lat_rows = c_lat.flatten_outer_dims().rearrange("(p j) w -> p j w", j=4)
+    mu_rows = mu.flatten_outer_dims().rearrange("(p j) o -> p (j o)", j=4)
+    rstd_rows = rstd.flatten_outer_dims().rearrange("(p j) o -> p (j o)", j=4)
+    out_0_rows = out_0.flatten_outer_dims().rearrange("(p j) w -> p j w", j=4)
+    out_1_rows = out_1.rearrange("(m p) w -> p m w", p=128)
+    cos_rows = cos.rearrange("(q j) w -> q j w", j=4)
+    sin_rows = sin.rearrange("(q j) w -> q j w", j=4)
+
+    with ExitStack() as ctx:
+        keep = ctx.enter_context(tc.tile_pool(name="keep", bufs=1))
+        inputs = ctx.enter_context(tc.tile_pool(name="inputs", bufs=INPUT_BUFS))
+        outputs = ctx.enter_context(tc.tile_pool(name="outputs", bufs=OUT_BUFS))
+        turned = ctx.enter_context(tc.tile_pool(name="turned", bufs=TURNED_BUFS))
+        work = ctx.enter_context(tc.tile_pool(name="work", bufs=2))
+        psum = ctx.enter_context(tc.psum_pool(name="psum", bufs=1))
+
+        def kept(name, shape, dtype):
+            return keep.tile(shape, dtype, name=name, align_bytes=64)
+
+        identity = kept("identity", [128, 128], F32)
+        make_identity(nc, identity[:])
+        ones = kept("ones", [128, 128], BF16)
+        nc.gpsimd.memset(ones[:], 1.0)
+        gain_row = kept("gain_row", [128, RANK], BF16)
+        nc.gpsimd.memset(gain_row[:], 0.0)
+        cos_in = kept("cos_in", [128, 4, 32], BF16)
+        sin_in = kept("sin_in", [128, 4, 32], BF16)
+        mu_col = kept("mu_col", [128, 4], F32)
+        rstd_col = kept("rstd_col", [128, 4], F32)
+        rstd_mean_col = kept("rstd_mean_col", [128, 4], F32)
+        w2_codes = kept("w2_codes", [128, 8, RANK], U32)
+        w2_scales = kept("w2_scales", [128, 8, RANK], U8)
+        x_codes = kept("x_codes", [128, DIM], U32)
+        x_scales = kept("x_scales", [128, DIM], U8)
+        wkv_codes = kept("wkv_codes", [128, 3, DIM], U32)
+        wkv_scales = kept("wkv_scales", [128, 3, DIM], U8)
+        dz1_token_codes = kept("dz1_token_codes", [128, WIDTH], U32)
+        dz1_token_scales = kept("dz1_token_scales", [128, WIDTH], U8)
+        rope_codes = kept("rope_codes", [128, 4, 2, 128], U32)
+        rope_scales = kept("rope_scales", [128, 4, 2, 128], U8)
+        latent_codes = kept("latent_codes", [128, 4, 128], U32)
+        latent_scales = kept("latent_scales", [128, 4, 128], U8)
+        g0 = kept("g0", [128, 4, HEADS * HEAD], BF16)
+        xhat = kept("xhat", [128, 4, RANK], F32)
+        dc = kept("dc", [128, 4, RANK], BF16)
+        gain = kept("gain", [128, RANK], F32)
+        cos_pairs = kept("cos_pairs", [128, 4, 32, 2], BF16)
+        sin_pairs = kept("sin_pairs", [128, 4, 32, 2], BF16)
+        means = kept("means", [128, 4, 2], F32)
+
+        def copy(engine, out, in_):
+            if engine == "V":
+                nc.vector.tensor_copy(out=out, in_=in_)
+            else:
+                nc.scalar.copy(out=out, in_=in_)
+
+        loaded = {}
+
+        def load(name):
+            k, *rest = name.split()
+            i = int(rest[0]) if rest else 0
+            if k == "x":
+                t = outputs.tile([128, 4, 512], BF16, name="out", align_bytes=64)
+                loaded[name] = t
+                nc.sync.dma_start(out=t[:], in_=x_rows[:, :, 512 * i : 512 * i + 512])
+            elif k in "wak":
+                t = inputs.tile([128, 2048], BF16, name="input", align_bytes=64)
+                loaded[name] = t
+                if k == "k":
+                    nc.sync.dma_start(out=t[:, 0:WIDTH], in_=wkv_a_w[128 * i : 128 * i + 128, :])
+                elif k == "a":
+                    nc.sync.dma_start(out=t[:], in_=grad_1_rows[:, i, :])
+                else:
+                    w = wk_w if i < 4 else wv_w
+                    nc.sync.dma_start(out=t[:], in_=w[128 * (i % 4) : 128 * (i % 4) + 128, :])
+            elif k == "g":
+                nc.sync.dma_start(out=g0[:, i, :], in_=grad_0_rows[:, i, :])
+            elif k == "c":
+                nc.sync.dma_start(out=xhat[:], in_=c_lat_rows)
+            elif k == "t":
+                for half in (slice(0, 64), slice(64, 128)):
+                    nc.sync.dma_start(out=cos_in[half], in_=cos_rows)
+                    nc.sync.dma_start(out=sin_in[half], in_=sin_rows)
+            elif k == "s":
+                nc.sync.dma_start(out=mu_col[:], in_=mu_rows)
+                nc.sync.dma_start(out=rstd_col[:], in_=rstd_rows)
+                nc.sync.dma_start(out=gain_row[0:1, :], in_=kvn_g.rearrange("(o w) -> o w", o=1))
+
+        def buffered(name):
+            return name[0] in "wak"
+
+        dz2, split = {}, {}
+
+        def run_inputs(run):
+            k, *a = run.split()
+            if k == "W":
+                first = 4 * (int(a[0]) // 4)
+                return ["w %d" % (first + i) for i in range(4)]
+            if k == "K":
+                return ["k %d" % (4 * int(a[0]) + i) for i in range(4)]
+            return ["a " + a[0]] if k == "Z" and a[1] == "1" else []
+
+        def words(rows, g):
+            return rows.bitcast(F32)[:, 256 * g : 256 * g + 256].rearrange("p (w u) -> p u w", u=2)
+
+        def run_blocks(run):
+            k, *a = run.split()
+            a = [int(z) for z in a]
+            if k == "W":
+                return [words(loaded[name][:], a[0] % 4) for name in run_inputs(run)]
+            if k == "K":
+                return [split[name][:, a[1], :, :] if name in split else words(loaded[name][:], a[1]) for name in run_inputs(run)]
+            if k == "Z":
+                rows = loaded["a %d" % a[0]][:] if a[1] else g0[:, a[0], 0:NOPE]
+                return [words(rows, g) for g in range(4)]
+            if k == "F":
+                return [words(g0[:, 2 * a[0] + i, NOPE : NOPE + ROPE], g) for i in range(2) for g in range(2)]
+            return [words(dc[:, j, :], 0) for j in range(4)]
+
+        def run_operand(run):
+            k, *a = run.split()
+            a = [int(z) for z in a]
+            if k == "W":
+                return w2_codes[:, a[0], :], w2_scales[:, a[0], :], E4M3
+            if k == "K":
+                cols = slice(512 * a[0], 512 * a[0] + 512)
+                return wkv_codes[:, a[1], cols], wkv_scales[:, a[1], cols], E4M3
+            if k == "Z":
+                j, h = a
+                if j not in dz2:
+                    codes = work.tile([128, 8, 128], U32, name="dz2_codes", bufs=DZ2_BUFS, align_bytes=64)
+                    scales = work.tile([128, 8, 128], U8, name="dz2_scales", bufs=DZ2_BUFS, align_bytes=64)
+                    dz2[j] = (codes, scales)
+                codes, scales = [t[:, 4 * h : 4 * h + 4, :].rearrange("p g n -> p (g n)") for t in dz2[j]]
+                return codes, scales, E5M2
+            if k == "F":
+                tiles = slice(2 * a[0], 2 * a[0] + 2)
+                codes, scales = [t[:, tiles, :, :].rearrange("p j g n -> p (j g n)") for t in (rope_codes, rope_scales)]
+                return codes, scales, E5M2
+            codes, scales = [t[:].rearrange("p j n -> p (j n)") for t in (latent_codes, latent_scales)]
+            return codes, scales, E5M2
+
+        def transpose_run(run):
+            blocks = run_blocks(run)
+            banks = []
+            for b in range(2):
+                bank = psum.tile([128, 2, 2, 128], F32, name="turn", bufs=TURN_BANKS)
+                banks.append(bank)
+                for a in range(2):
+                    for u in range(2):
+                        nc.tensor.transpose(bank[:, a, u, :], blocks[2 * b + a][:, u, :], identity[:])
+            return banks
+
+        def copy_run(banks, engines):
+            rows = turned.tile([128, 4, 128, 4], BF16, name="rows", align_bytes=64)
+            for b in range(2):
+                copy(engines[b], rows[:, 2 * b : 2 * b + 2, :, :].bitcast(F32), banks[b][:].rearrange("p a u n -> p a n u"))
+            return rows
+
+        def quantize_run(run, rows):
+            codes, scales, fmt = run_operand(run)
+            nc.vector.quantize_mx(out=codes.bitcast(fmt), scales=scales, in_=rows[:].rearrange("p a n t -> p (a n t)"))
+
+        dh, beside, halves, norm = {}, {}, {}, {}
+
+        def task(name):
+            k, *a = name.split()
+            i = int(a[0]) if a else 0
+            if k == "tables":
+                for e in range(2):
+                    nc.vector.tensor_copy(out=cos_pairs[:, :, :, e], in_=cos_in[:])
+                nc.vector.tensor_scalar(out=sin_pairs[:, :, :, 0], in0=sin_in[:], scalar1=-1.0, scalar2=None, op0=MULT)
+                nc.vector.tensor_copy(out=sin_pairs[:, :, :, 1], in_=sin_in[:])
+            elif k == "turn":
+                pairs = g0[:, i, :].rearrange("p (h w) -> p h w", w=HEAD)[:, :, 128:HEAD]
+                halves[i] = []
+                for table in (cos_pairs, sin_pairs):
+                    half = work.tile([128, HEADS, 64], F32, name="half", tag="f32", bufs=3)
+                    halves[i].append(half)
+                    row = table[:, i, :, :].rearrange("p w e -> p (w e)")
+                    nc.vector.tensor_tensor(out=half[:], in0=pairs, in1=row.unsqueeze(1).to_broadcast([128, HEADS, 64]), op=MULT)
+            elif k == "sum":
+                by_cos, by_sin = [half[:].rearrange("p h (w e) -> p h w e", e=2) for half in halves[i]]
+                pairs = g0[:, i, :].rearrange("p (h w) -> p h w", w=HEAD)[:, :, 128:HEAD]
+                nc.vector.tensor_tensor(out=pairs.rearrange("p h (w e) -> p h w e", e=2), in0=by_cos, in1=by_sin[:, :, :, ::-1], op=ADD)
+            elif k in ("xlay", "zlay"):
+                if k == "xlay":
+                    cols = loaded["x %d" % i][:]
+                else:
+                    cols = g0[:, :, NOPE + 512 * i : NOPE + 512 * i + 512] if i < 2 else dc[:]
+                tokens = work.tile([128, 512, 4], BF16, name="tokens", align_bytes=64)
+                beside[(k[0], i)] = tokens
+                copy(a[1], tokens[:].rearrange("p (c i) j -> p c j i", i=4), cols.rearrange("p j (c i) -> p c j i", i=4))
+            elif k in ("xquant", "zquant"):
+                codes, scales, fmt = (x_codes, x_scales, E4M3) if k == "xquant" else (dz1_token_codes, dz1_token_scales, E5M2)
+                cols = slice(512 * i, 512 * i + 512)
+                nc.vector.quantize_mx(out=codes[:, cols].bitcast(fmt), scales=scales[:, cols], in_=beside[(k[0], i)][:].rearrange("p c j -> p (c j)"))
+            elif k == "split":
+                t = inputs.tile([128, 3, 2, 128], F32, name="split", bufs=SPLIT_BUFS, align_bytes=64)
+                split["k %d" % i] = t
+                copy(a[1], t[:], loaded["k %d" % i][:].bitcast(F32)[:, 0 : WIDTH // 2].rearrange("p (g w u) -> p g u w", g=3, u=2))
+            elif k == "xhat":
+                if i == 0:
+                    nc.vector.tensor_scalar(out=rstd_mean_col[:], in0=rstd_col[:], scalar1=1.0 / RANK, scalar2=None, op0=MULT)
+                nc.vector.tensor_scalar(out=xhat[:, i, :], in0=xhat[:, i, :], scalar1=mu_col[:, i : i + 1], scalar2=rstd_col[:, i : i + 1], op0=SUB, op1=MULT)
+            elif k == "norm1":
+                t = work.tile([128, 2, RANK], F32, name="norm", tag="f32", bufs=3)
+                norm[i] = (t[:, 0, :], t[:, 1, :])
+                nc.vector.scalar_tensor_tensor(out=norm[i][0], in0=dh[i][:], scalar=rstd_mean_col[:, i : i + 1], in1=gain[:], op0=MULT, op1=MULT, accum_out=means[:, i, 0:1])
+                if len(norm) == 4:
+                    dh_done.append(True)
+            elif k == "norm2":
+                nc.vector.scalar_tensor_tensor(out=norm[i][1], in0=norm[i][0], scalar=1.0, in1=xhat[:, i, :], op0=MULT, op1=MULT, accum_out=means[:, i, 1:2])
+            elif k == "norm3":
+                nc.vector.tensor_scalar(out=norm[i][1], in0=xhat[:, i, :], scalar1=means[:, i, 1:2], scalar2=means[:, i, 0:1], op0=MULT, op1=ADD)
+            elif k == "norm4":
+                nc.vector.scalar_tensor_tensor(out=dc[:, i, :], in0=norm[i][0], scalar=float(RANK), in1=norm[i][1], op0=MULT, op1=SUB)
+
+        full, dh_done, staged = [], [], {}
+        late_banks = [0]
+
+        def matmul_mx(out, left, right, start, stop):
+            (l, l_scales, l_fmt), (r, r_scales, r_fmt) = left, right
+            nc.tensor.matmul_mx(out=out, lhsT=l.bitcast(l_fmt), lhsT_scale=l_scales, rhs=r.bitcast(r_fmt), rhs_scale=r_scales, start=start, stop=stop)
+
+        def product_bank():
+            if len(full) == PRODUCT_BANKS + len(dh_done):
+                empty(*full.pop(0))
+            if dh_done:
+                late_banks[0] += 1
+            if late_banks[0] % (PRODUCT_BANKS + 1) == PRODUCT_BANKS:
+                bank = psum.tile([128, 512], F32, name="dh")
+            else:
+                bank = psum.tile([128, 512], F32, name="product", bufs=PRODUCT_BANKS)
+            return bank
+
+        def product(name):
+            k, *a = name.split()
+            engines = [z for z in a if z in "VS"]
+            a = [int(z) for z in a if z not in "VS"]
+            if k == "gain":
+                bank = product_bank()
+                nc.tensor.matmul(bank[:], ones[:], gain_row[:], start=True, stop=True)
+                full.append((bank, None, engines[0]))
+            elif k == "dh":
+                bank = psum.tile([128, 512], F32, name="dh")
+                dh[a[0]] = bank
+                codes, scales = dz2[a[0]]
+                for g in range(8):
+                    matmul_mx(bank[:], (codes[:, g, :], scales[:, g, :], E5M2), (w2_codes[:, g, :], w2_scales[:, g, :], E4M3), g == 0, g == 7)
+            elif k in "Al":
+                rows = slice(128 * a[0], 128 * a[0] + 128)
+                for n in (0, 1) if k == "A" else (2,):
+                    bank = product_bank()
+                    cols = slice(512 * n, 512 * n + 512)
+                    matmul_mx(bank[:], (x_codes[:, rows], x_scales[:, rows], E4M3), (dz1_token_codes[:, cols], dz1_token_scales[:, cols], E5M2), True, True)
+                    full.append((bank, (k, a[0], n), engines[n % 2]))
+            elif k == "o":
+                n, j = a
+                bank = product_bank()
+                cols = slice(512 * n, 512 * n + 512)
+                for g in range(3):
+                    left = (rope_codes[:, j, g, :], rope_scales[:, j, g, :], E5M2) if g < 2 else (latent_codes[:, j, :], latent_scales[:, j, :], E5M2)
+                    matmul_mx(bank[:], left, (wkv_codes[:, g, cols], wkv_scales[:, g, cols], E4M3), g == 0, g == 2)
+                full.append((bank, (k, j, n), engines[0]))
+
+        def empty(bank, place, engine):
+            if place is None:
+                copy(engine, gain[:], bank[:])
+                return
+            k, i, n = place
+            pair, side = {"A": ((k, i), n), "l": ((k, i // 2), i % 2), "o": ((k, i, n // 2), n % 2)}[k]
+            if pair not in staged:
+                t = outputs.tile([128, 2, 512], F32, name="out", align_bytes=64)
+                staged[pair] = [t]
+            t = staged[pair][0]
+            copy(engine, t[:, side, :], bank[:])
+            staged[pair].append(side)
+            if len(staged[pair]) == 3:
+                if k == "A":
+                    nc.sync.dma_start(out=out_1_rows[:, i, 0:ROPE], in_=t[:].rearrange("p a w -> p (a w)"))
+                elif k == "l":
+                    nc.sync.dma_start(out=out_1_rows[:, i // 2 * 2 : i // 2 * 2 + 2, ROPE:WIDTH], in_=t[:])
+                else:
+                    nc.sync.dma_start(out=out_0_rows[:, i, 1024 * (n // 2) : 1024 * (n // 2) + 1024], in_=t[:].rearrange("p a w -> p (a w)"))
+
+        ctx.enter_context(tc.manual_schedule())
+
+        split_names = ["k " + name.split()[1] for step in STEPS for name in step[2] if name.startswith("split")]
+        last_use = {}
+        for s, (run, engines, tasks, products) in enumerate(STEPS):
+            for name in run_inputs(run) if run else []:
+                if name not in split_names:
+                    last_use[name] = s
+            for name in tasks:
+                if name.startswith("split"):
+                    last_use["k " + name.split()[1]] = s
+
+        waiting, issued = list(LOADS), []
+        before = None
+        for s, (run, engines, tasks, products) in enumerate(STEPS):
+            while waiting:
+                if buffered(waiting[0]):
+                    if len(issued) >= INPUT_BUFS and last_use[issued[-INPUT_BUFS]] >= s:
+                        break
+                    issued.append(waiting[0])
+                load(waiting.pop(0))
+            banks = transpose_run(run) if run else None
+            while full:
+                empty(*full.pop(0))
+            if before:
+                quantize_run(*before)
+            before = (run, copy_run(banks, engines)) if run else None
+            for name in products:
+                product(name)
+            for name in tasks:
+                task(name)

@@ -15,6 +15,7 @@ SUB = mybir.AluOpType.subtract
 
 TOKENS, DIM, RANK, HEADS, HEAD = 512, 2048, 512, 16, 192
 NOPE, ROPE = 2048, 1024
+DK = NOPE + ROPE
 FEATURES = 4096
 WIDTH = ROPE + RANK
 FLOPS = 2 * (TOKENS * FEATURES * RANK + 2 * TOKENS * WIDTH * DIM)
@@ -24,57 +25,12 @@ BYTES = (
     + 4 * (TOKENS * DIM + DIM * WIDTH)
 )
 
-INPUT_BUFS = 10
-OUT_BUFS = 6
-SPLIT_BUFS = 3
-DZ2_BUFS = 3
-TURNED_BUFS = 3
-TURN_BANKS = 4
-PRODUCT_BANKS = 3
-
-LOADS = [
-    "t", "g 0", "w 4", "g 2", "w 5", "w 6", "w 7", "g 1", "w 0", "k 5", "s", "x 0", "g 3", "w 1",
-    "w 2", "w 3", "a 0", "x 1", "k 12", "a 2", "k 2", "c", "a 1", "x 3", "a 3", "k 1", "x 2", "k 0",
-    "k 3", "k 7", "k 10", "k 6", "k 4", "k 15", "k 13", "k 14", "k 11", "k 8", "k 9",
-]
-
-STEPS = [
-    ("W 4", "SS", ["tables", "turn 0", "sum 0", "turn 2", "sum 2"], []),
-    ("W 5", "SS", ["turn 1"], []),
-    ("Z 2 0", "SS", [], []),
-    ("W 6", "SS", [], ["gain S"]),
-    ("W 7", "SS", ["sum 1", "xlay 0 S"], []),
-    ("Z 0 0", "VS", ["turn 3"], []),
-    ("F 0", "SS", ["xquant 0"], []),
-    ("W 0", "SS", [], []),
-    ("W 1", "SS", ["sum 3"], []),
-    ("W 2", "SS", [], []),
-    ("Z 0 1", "SS", [], []),
-    ("W 3", "SS", ["xlay 1 V"], []),
-    ("Z 2 1", "SS", ["xhat 0", "split 5 V"], []),
-    ("Z 1 0", "SS", ["zlay 1 S", "xquant 1", "xhat 2", "norm1 0"], ["dh 0"]),
-    ("Z 1 1", "SV", ["split 12 V", "zquant 1", "zlay 0 S"], []),
-    ("Z 3 0", "SS", ["zquant 0", "norm1 2", "norm2 0", "norm2 2", "norm3 0", "xlay 2 S", "norm3 2"], ["dh 2"]),
-    ("", "", ["xquant 2", "xlay 3 V"], []),
-    ("K 0 0", "SS", [], ["A 4 S S", "dh 1"]),
-    ("Z 3 1", "SS", ["xquant 3", "xhat 1", "norm1 1", "norm4 0"], ["A 5 S S"]),
-    ("K 0 1", "SS", [], []),
-    ("K 0 2", "SS", ["norm2 1"], ["A 8 S S"]),
-    ("", "", ["norm1 3"], ["dh 3", "A 0 S S"]),
-    ("K 1 0", "SS", ["xhat 3", "norm4 2", "norm2 3"], ["A 6 S V", "A 12 V S"]),
-    ("K 1 1", "VS", ["norm3 1"], ["A 7 V S", "A 13 S S"]),
-    ("K 2 0", "VS", ["norm3 3"], ["A 1 V S", "A 9 S S"]),
-    ("F 1", "SS", ["norm4 1"], ["A 2 V V", "A 10 S V"]),
-    ("K 3 0", "SS", ["norm4 3"], []),
-    ("K 2 1", "VS", ["zlay 2 V"], ["A 3 S S", "A 11 S S"]),
-    ("D", "VS", ["zquant 2"], ["A 14 S V", "A 15 V S"]),
-    ("K 2 2", "SS", [], []),
-    ("K 1 2", "SV", [], ["l 0 S", "l 1 S", "l 2 V"]),
-    ("K 3 1", "SV", [], ["l 3 S", "l 4 S", "l 5 V"]),
-    ("K 3 2", "SS", [], ["l 6 S", "l 7 V"]),
-    ("", "", [], ["o 0 3 S", "o 1 3 S", "l 8 V", "l 9 V", "o 1 1 S", "l 10 V", "o 0 1 S", "l 11 V", "o 2 3 S", "l 12 V", "l 13 S", "o 3 3 V", "o 0 2 V", "o 1 2 S", "o 2 1 V", "l 14 V", "l 15 S", "o 1 0 V", "o 0 0 S", "o 2 0 V", "o 3 0 S", "o 3 1 S", "o 3 2 S", "o 2 2 S"]),
-    ("", "", [], []),
-]
+KIB = 1024
+STAGE_BUFS = 9
+ROW_BUFS = 6
+PAIR_BUFS = 6
+SPLIT_FROM = 6
+VECTOR_EVERY = 3
 
 
 def tile_mla_pa_v_kernel(
@@ -84,24 +40,25 @@ def tile_mla_pa_v_kernel(
     x_rows = x.flatten_outer_dims().rearrange("(p j) w -> p j w", j=4)
     grad_0_rows = grad_0.rearrange("b s h d -> (b s) (h d)").rearrange("(p j) w -> p j w", j=4)
     grad_1_rows = grad_1.rearrange("b s h d -> (b s) (h d)").rearrange("(p j) w -> p j w", j=4)
-    c_lat_rows = c_lat.flatten_outer_dims().rearrange("(p j) w -> p j w", j=4)
+    c_lat_rows = c_lat.flatten_outer_dims().rearrange("(p j) w -> p (j w)", j=4)
     mu_rows = mu.flatten_outer_dims().rearrange("(p j) o -> p (j o)", j=4)
     rstd_rows = rstd.flatten_outer_dims().rearrange("(p j) o -> p (j o)", j=4)
+    wkv_rows = wkv_a_w.rearrange("(n p j) w -> n p (j w)", p=128, j=4)
     out_0_rows = out_0.flatten_outer_dims().rearrange("(p j) w -> p j w", j=4)
     out_1_rows = out_1.rearrange("(m p) w -> p m w", p=128)
-    cos_rows = cos.rearrange("(q j) w -> q j w", j=4)
-    sin_rows = sin.rearrange("(q j) w -> q j w", j=4)
+    cos_rows = cos.rearrange("(q j) w -> q (j w)", j=4)
+    sin_rows = sin.rearrange("(q j) w -> q (j w)", j=4)
 
     with ExitStack() as ctx:
         keep = ctx.enter_context(tc.tile_pool(name="keep", bufs=1))
-        inputs = ctx.enter_context(tc.tile_pool(name="inputs", bufs=INPUT_BUFS))
-        outputs = ctx.enter_context(tc.tile_pool(name="outputs", bufs=OUT_BUFS))
-        turned = ctx.enter_context(tc.tile_pool(name="turned", bufs=TURNED_BUFS))
-        work = ctx.enter_context(tc.tile_pool(name="work", bufs=2))
-        psum = ctx.enter_context(tc.psum_pool(name="psum", bufs=1))
+        shared = ctx.enter_context(tc.tile_pool(name="shared", bufs=1))
+        psum = ctx.enter_context(tc.psum_pool(name="psum", bufs=8))
 
         def kept(name, shape, dtype):
             return keep.tile(shape, dtype, name=name, align_bytes=64)
+
+        def placed(name, shape, dtype, kib, bufs=1):
+            return shared.tile(shape, dtype, name=name, bufs=bufs, align_bytes=64, offset=kib * KIB)
 
         identity = kept("identity", [128, 128], F32)
         make_identity(nc, identity[:])
@@ -109,30 +66,36 @@ def tile_mla_pa_v_kernel(
         nc.gpsimd.memset(ones[:], 1.0)
         gain_row = kept("gain_row", [128, RANK], BF16)
         nc.gpsimd.memset(gain_row[:], 0.0)
-        cos_in = kept("cos_in", [128, 4, 32], BF16)
-        sin_in = kept("sin_in", [128, 4, 32], BF16)
+        gain = kept("gain", [128, RANK], F32)
+        cos_in = kept("cos_in", [128, 128], BF16)
+        sin_in = kept("sin_in", [128, 128], BF16)
+        cos_pairs = kept("cos_pairs", [128, 128, 2], BF16)
+        sin_pairs = kept("sin_pairs", [128, 128, 2], BF16)
         mu_col = kept("mu_col", [128, 4], F32)
         rstd_col = kept("rstd_col", [128, 4], F32)
-        rstd_mean_col = kept("rstd_mean_col", [128, 4], F32)
-        w2_codes = kept("w2_codes", [128, 8, RANK], U32)
-        w2_scales = kept("w2_scales", [128, 8, RANK], U8)
-        x_codes = kept("x_codes", [128, DIM], U32)
-        x_scales = kept("x_scales", [128, DIM], U8)
-        wkv_codes = kept("wkv_codes", [128, 3, DIM], U32)
-        wkv_scales = kept("wkv_scales", [128, 3, DIM], U8)
-        dz1_token_codes = kept("dz1_token_codes", [128, WIDTH], U32)
-        dz1_token_scales = kept("dz1_token_scales", [128, WIDTH], U8)
-        rope_codes = kept("rope_codes", [128, 4, 2, 128], U32)
-        rope_scales = kept("rope_scales", [128, 4, 2, 128], U8)
-        latent_codes = kept("latent_codes", [128, 4, 128], U32)
-        latent_scales = kept("latent_scales", [128, 4, 128], U8)
-        g0 = kept("g0", [128, 4, HEADS * HEAD], BF16)
-        xhat = kept("xhat", [128, 4, RANK], F32)
-        dc = kept("dc", [128, 4, RANK], BF16)
-        gain = kept("gain", [128, RANK], F32)
-        cos_pairs = kept("cos_pairs", [128, 4, 32, 2], BF16)
-        sin_pairs = kept("sin_pairs", [128, 4, 32, 2], BF16)
+        factors = kept("factors", [128, 4, 2], F32)
+        sums = kept("sums", [128, 4, 2], F32)
         means = kept("means", [128, 4, 2], F32)
+        x_in = [kept("x_in%d" % h, [128, 4, 1024], BF16) for h in range(2)]
+        dc = kept("dc", [128, 4 * RANK], BF16)
+
+        def operand(name, width, kib=None):
+            if kib is None:
+                return kept(name + "_codes", [128, width], U32), kept(name + "_scales", [128, width], U8)
+            return placed(name + "_codes", [128, width], U32, kib), placed(name + "_scales", [128, width], U8, kib + width // 256)
+
+        wkv_mx = {}
+        token_mx = operand("dz1_token", WIDTH)
+        rope_mx = operand("rope", 4 * 2 * 128)
+        latent_mx = operand("latent", 4 * 128)
+        dk = placed("dk", [128, 4 * DK], BF16, 0)
+        w2_mx = operand("w2", 8 * RANK, 24)
+        dz2_mx = operand("dz2", 4 * 8 * 128, 44)
+        c_in = placed("c_in", [128, 4 * RANK], F32, 64)
+        RAW = 88
+
+        def cols(mx, start, width):
+            return mx[0][:, start : start + width], mx[1][:, start : start + width]
 
         def copy(engine, out, in_):
             if engine == "V":
@@ -140,264 +103,361 @@ def tile_mla_pa_v_kernel(
             else:
                 nc.scalar.copy(out=out, in_=in_)
 
-        loaded = {}
+        def stage_tile(name):
+            return keep.tile([128, 1024], F32, name=name, tag="stage", bufs=STAGE_BUFS, align_bytes=64)
 
-        def load(name):
-            k, *rest = name.split()
-            i = int(rest[0]) if rest else 0
-            if k == "x":
-                t = outputs.tile([128, 4, 512], BF16, name="out", align_bytes=64)
-                loaded[name] = t
-                nc.sync.dma_start(out=t[:], in_=x_rows[:, :, 512 * i : 512 * i + 512])
-            elif k in "wak":
-                t = inputs.tile([128, 2048], BF16, name="input", align_bytes=64)
-                loaded[name] = t
-                if k == "k":
-                    nc.sync.dma_start(out=t[:, 0:WIDTH], in_=wkv_a_w[128 * i : 128 * i + 128, :])
-                elif k == "a":
-                    nc.sync.dma_start(out=t[:], in_=grad_1_rows[:, i, :])
-                else:
-                    w = wk_w if i < 4 else wv_w
-                    nc.sync.dma_start(out=t[:], in_=w[128 * (i % 4) : 128 * (i % 4) + 128, :])
-            elif k == "g":
-                nc.sync.dma_start(out=g0[:, i, :], in_=grad_0_rows[:, i, :])
-            elif k == "c":
-                nc.sync.dma_start(out=xhat[:], in_=c_lat_rows)
-            elif k == "t":
-                for half in (slice(0, 64), slice(64, 128)):
-                    nc.sync.dma_start(out=cos_in[half], in_=cos_rows)
-                    nc.sync.dma_start(out=sin_in[half], in_=sin_rows)
-            elif k == "s":
-                nc.sync.dma_start(out=mu_col[:], in_=mu_rows)
-                nc.sync.dma_start(out=rstd_col[:], in_=rstd_rows)
-                nc.sync.dma_start(out=gain_row[0:1, :], in_=kvn_g.rearrange("(o w) -> o w", o=1))
+        def bank_tile(name):
+            return psum.tile([128, 512], F32, name=name, tag="bank")
 
-        def buffered(name):
-            return name[0] in "wak"
+        def quantize(mx, fmt, in_):
+            nc.vector.quantize_mx(out=mx[0].bitcast(fmt), scales=mx[1], in_=in_.bitcast(BF16))
 
-        dz2, split = {}, {}
+        def matmul_mx(out, left, left_fmt, right, right_fmt, start, stop):
+            nc.tensor.matmul_mx(out=out, lhsT=left[0].bitcast(left_fmt), lhsT_scale=left[1], rhs=right[0].bitcast(right_fmt), rhs_scale=right[1], start=start, stop=stop)
 
-        def run_inputs(run):
-            k, *a = run.split()
-            if k == "W":
-                first = 4 * (int(a[0]) // 4)
-                return ["w %d" % (first + i) for i in range(4)]
-            if k == "K":
-                return ["k %d" % (4 * int(a[0]) + i) for i in range(4)]
-            return ["a " + a[0]] if k == "Z" and a[1] == "1" else []
+        def words(rows, start):
+            return rows.bitcast(F32)[:, start // 2 : start // 2 + 256].rearrange("p (w u) -> p u w", u=2)
 
-        def words(rows, g):
-            return rows.bitcast(F32)[:, 256 * g : 256 * g + 256].rearrange("p (w u) -> p u w", u=2)
-
-        def run_blocks(run):
-            k, *a = run.split()
-            a = [int(z) for z in a]
-            if k == "W":
-                return [words(loaded[name][:], a[0] % 4) for name in run_inputs(run)]
-            if k == "K":
-                return [split[name][:, a[1], :, :] if name in split else words(loaded[name][:], a[1]) for name in run_inputs(run)]
-            if k == "Z":
-                rows = loaded["a %d" % a[0]][:] if a[1] else g0[:, a[0], 0:NOPE]
-                return [words(rows, g) for g in range(4)]
-            if k == "F":
-                return [words(g0[:, 2 * a[0] + i, NOPE : NOPE + ROPE], g) for i in range(2) for g in range(2)]
-            return [words(dc[:, j, :], 0) for j in range(4)]
-
-        def run_operand(run):
-            k, *a = run.split()
-            a = [int(z) for z in a]
-            if k == "W":
-                return w2_codes[:, a[0], :], w2_scales[:, a[0], :], E4M3
-            if k == "K":
-                cols = slice(512 * a[0], 512 * a[0] + 512)
-                return wkv_codes[:, a[1], cols], wkv_scales[:, a[1], cols], E4M3
-            if k == "Z":
-                j, h = a
-                if j not in dz2:
-                    codes = work.tile([128, 8, 128], U32, name="dz2_codes", bufs=DZ2_BUFS, align_bytes=64)
-                    scales = work.tile([128, 8, 128], U8, name="dz2_scales", bufs=DZ2_BUFS, align_bytes=64)
-                    dz2[j] = (codes, scales)
-                codes, scales = [t[:, 4 * h : 4 * h + 4, :].rearrange("p g n -> p (g n)") for t in dz2[j]]
-                return codes, scales, E5M2
-            if k == "F":
-                tiles = slice(2 * a[0], 2 * a[0] + 2)
-                codes, scales = [t[:, tiles, :, :].rearrange("p j g n -> p (j g n)") for t in (rope_codes, rope_scales)]
-                return codes, scales, E5M2
-            codes, scales = [t[:].rearrange("p j n -> p (j n)") for t in (latent_codes, latent_scales)]
-            return codes, scales, E5M2
-
-        def transpose_run(run):
-            blocks = run_blocks(run)
+        def turn(name, blocks, places):
             banks = []
             for b in range(2):
-                bank = psum.tile([128, 2, 2, 128], F32, name="turn", bufs=TURN_BANKS)
-                banks.append(bank)
+                bank = bank_tile(name)
+                banks.append(bank[:].rearrange("p (a u n) -> p a u n", a=2, u=2))
                 for a in range(2):
                     for u in range(2):
-                        nc.tensor.transpose(bank[:, a, u, :], blocks[2 * b + a][:, u, :], identity[:])
-            return banks
-
-        def copy_run(banks, engines):
-            rows = turned.tile([128, 4, 128, 4], BF16, name="rows", align_bytes=64)
+                        nc.tensor.transpose(banks[b][:, a, u, :], blocks[2 * b + a][:, u, :], identity[:])
             for b in range(2):
-                copy(engines[b], rows[:, 2 * b : 2 * b + 2, :, :].bitcast(F32), banks[b][:].rearrange("p a u n -> p a n u"))
-            return rows
+                copy("S", places[b], banks[b].rearrange("p a u n -> p a n u"))
 
-        def quantize_run(run, rows):
-            codes, scales, fmt = run_operand(run)
-            nc.vector.quantize_mx(out=codes.bitcast(fmt), scales=scales, in_=rows[:].rearrange("p a n t -> p (a n t)"))
+        def plain_run(name, blocks, mx, fmt):
+            stage = stage_tile(name)
+            halves = stage[:].rearrange("p (b a n u) -> p b a n u", b=2, a=2, u=2)
+            turn(name, blocks, [halves[:, b] for b in range(2)])
+            return lambda: quantize(mx, fmt, stage[:])
 
-        dh, beside, halves, norm = {}, {}, {}, {}
+        raw = {}
 
-        def task(name):
-            k, *a = name.split()
-            i = int(a[0]) if a else 0
-            if k == "tables":
-                for e in range(2):
-                    nc.vector.tensor_copy(out=cos_pairs[:, :, :, e], in_=cos_in[:])
-                nc.vector.tensor_scalar(out=sin_pairs[:, :, :, 0], in0=sin_in[:], scalar1=-1.0, scalar2=None, op0=MULT)
-                nc.vector.tensor_copy(out=sin_pairs[:, :, :, 1], in_=sin_in[:])
-            elif k == "turn":
-                pairs = g0[:, i, :].rearrange("p (h w) -> p h w", w=HEAD)[:, :, 128:HEAD]
-                halves[i] = []
-                for table in (cos_pairs, sin_pairs):
-                    half = work.tile([128, HEADS, 64], F32, name="half", tag="f32", bufs=3)
-                    halves[i].append(half)
-                    row = table[:, i, :, :].rearrange("p w e -> p (w e)")
-                    nc.vector.tensor_tensor(out=half[:], in0=pairs, in1=row.unsqueeze(1).to_broadcast([128, HEADS, 64]), op=MULT)
-            elif k == "sum":
-                by_cos, by_sin = [half[:].rearrange("p h (w e) -> p h w e", e=2) for half in halves[i]]
-                pairs = g0[:, i, :].rearrange("p (h w) -> p h w", w=HEAD)[:, :, 128:HEAD]
-                nc.vector.tensor_tensor(out=pairs.rearrange("p h (w e) -> p h w e", e=2), in0=by_cos, in1=by_sin[:, :, :, ::-1], op=ADD)
-            elif k in ("xlay", "zlay"):
-                if k == "xlay":
-                    cols = loaded["x %d" % i][:]
-                else:
-                    cols = g0[:, :, NOPE + 512 * i : NOPE + 512 * i + 512] if i < 2 else dc[:]
-                tokens = work.tile([128, 512, 4], BF16, name="tokens", align_bytes=64)
-                beside[(k[0], i)] = tokens
-                copy(a[1], tokens[:].rearrange("p (c i) j -> p c j i", i=4), cols.rearrange("p j (c i) -> p c j i", i=4))
-            elif k in ("xquant", "zquant"):
-                codes, scales, fmt = (x_codes, x_scales, E4M3) if k == "xquant" else (dz1_token_codes, dz1_token_scales, E5M2)
-                cols = slice(512 * i, 512 * i + 512)
-                nc.vector.quantize_mx(out=codes[:, cols].bitcast(fmt), scales=scales[:, cols], in_=beside[(k[0], i)][:].rearrange("p c j -> p (c j)"))
-            elif k == "split":
-                t = inputs.tile([128, 3, 2, 128], F32, name="split", bufs=SPLIT_BUFS, align_bytes=64)
-                split["k %d" % i] = t
-                copy(a[1], t[:], loaded["k %d" % i][:].bitcast(F32)[:, 0 : WIDTH // 2].rearrange("p (g w u) -> p g u w", g=3, u=2))
-            elif k == "xhat":
-                if i == 0:
-                    nc.vector.tensor_scalar(out=rstd_mean_col[:], in0=rstd_col[:], scalar1=1.0 / RANK, scalar2=None, op0=MULT)
-                nc.vector.tensor_scalar(out=xhat[:, i, :], in0=xhat[:, i, :], scalar1=mu_col[:, i : i + 1], scalar2=rstd_col[:, i : i + 1], op0=SUB, op1=MULT)
-            elif k == "norm1":
-                t = work.tile([128, 2, RANK], F32, name="norm", tag="f32", bufs=3)
-                norm[i] = (t[:, 0, :], t[:, 1, :])
-                nc.vector.scalar_tensor_tensor(out=norm[i][0], in0=dh[i][:], scalar=rstd_mean_col[:, i : i + 1], in1=gain[:], op0=MULT, op1=MULT, accum_out=means[:, i, 0:1])
-                if len(norm) == 4:
-                    dh_done.append(True)
-            elif k == "norm2":
-                nc.vector.scalar_tensor_tensor(out=norm[i][1], in0=norm[i][0], scalar=1.0, in1=xhat[:, i, :], op0=MULT, op1=MULT, accum_out=means[:, i, 1:2])
-            elif k == "norm3":
-                nc.vector.tensor_scalar(out=norm[i][1], in0=xhat[:, i, :], scalar1=means[:, i, 1:2], scalar2=means[:, i, 0:1], op0=MULT, op1=ADD)
-            elif k == "norm4":
-                nc.vector.scalar_tensor_tensor(out=dc[:, i, :], in0=norm[i][0], scalar=float(RANK), in1=norm[i][1], op0=MULT, op1=SUB)
-
-        full, dh_done, staged = [], [], {}
-        late_banks = [0]
-
-        def matmul_mx(out, left, right, start, stop):
-            (l, l_scales, l_fmt), (r, r_scales, r_fmt) = left, right
-            nc.tensor.matmul_mx(out=out, lhsT=l.bitcast(l_fmt), lhsT_scale=l_scales, rhs=r.bitcast(r_fmt), rhs_scale=r_scales, start=start, stop=stop)
-
-        def product_bank():
-            if len(full) == PRODUCT_BANKS + len(dh_done):
-                empty(*full.pop(0))
-            if dh_done:
-                late_banks[0] += 1
-            if late_banks[0] % (PRODUCT_BANKS + 1) == PRODUCT_BANKS:
-                bank = psum.tile([128, 512], F32, name="dh")
+        def load_raw(i):
+            t = placed("raw%d" % i, [128, 2048], BF16, RAW + 4 * i)
+            raw[i] = t
+            if i < 8:
+                w = wv_w if i < 4 else wk_w
+                nc.sync.dma_start(out=t[:], in_=w[128 * (i % 4) : 128 * (i % 4) + 128, :])
             else:
-                bank = psum.tile([128, 512], F32, name="product", bufs=PRODUCT_BANKS)
-            return bank
+                nc.sync.dma_start(out=t[:], in_=grad_1_rows[:, i - 8, :])
 
-        def product(name):
-            k, *a = name.split()
-            engines = [z for z in a if z in "VS"]
-            a = [int(z) for z in a if z not in "VS"]
-            if k == "gain":
-                bank = product_bank()
-                nc.tensor.matmul(bank[:], ones[:], gain_row[:], start=True, stop=True)
-                full.append((bank, None, engines[0]))
-            elif k == "dh":
-                bank = psum.tile([128, 512], F32, name="dh")
-                dh[a[0]] = bank
-                codes, scales = dz2[a[0]]
-                for g in range(8):
-                    matmul_mx(bank[:], (codes[:, g, :], scales[:, g, :], E5M2), (w2_codes[:, g, :], w2_scales[:, g, :], E4M3), g == 0, g == 7)
-            elif k in "Al":
-                rows = slice(128 * a[0], 128 * a[0] + 128)
-                for n in (0, 1) if k == "A" else (2,):
-                    bank = product_bank()
-                    cols = slice(512 * n, 512 * n + 512)
-                    matmul_mx(bank[:], (x_codes[:, rows], x_scales[:, rows], E4M3), (dz1_token_codes[:, cols], dz1_token_scales[:, cols], E5M2), True, True)
-                    full.append((bank, (k, a[0], n), engines[n % 2]))
-            elif k == "o":
-                n, j = a
-                bank = product_bank()
-                cols = slice(512 * n, 512 * n + 512)
-                for g in range(3):
-                    left = (rope_codes[:, j, g, :], rope_scales[:, j, g, :], E5M2) if g < 2 else (latent_codes[:, j, :], latent_scales[:, j, :], E5M2)
-                    matmul_mx(bank[:], left, (wkv_codes[:, g, cols], wkv_scales[:, g, cols], E4M3), g == 0, g == 2)
-                full.append((bank, (k, j, n), engines[0]))
+        wkv_in = {}
 
-        def empty(bank, place, engine):
-            if place is None:
-                copy(engine, gain[:], bank[:])
-                return
-            k, i, n = place
-            pair, side = {"A": ((k, i), n), "l": ((k, i // 2), i % 2), "o": ((k, i, n // 2), n % 2)}[k]
-            if pair not in staged:
-                t = outputs.tile([128, 2, 512], F32, name="out", align_bytes=64)
-                staged[pair] = [t]
-            t = staged[pair][0]
-            copy(engine, t[:, side, :], bank[:])
-            staged[pair].append(side)
-            if len(staged[pair]) == 3:
-                if k == "A":
-                    nc.sync.dma_start(out=out_1_rows[:, i, 0:ROPE], in_=t[:].rearrange("p a w -> p (a w)"))
-                elif k == "l":
-                    nc.sync.dma_start(out=out_1_rows[:, i // 2 * 2 : i // 2 * 2 + 2, ROPE:WIDTH], in_=t[:])
-                else:
-                    nc.sync.dma_start(out=out_0_rows[:, i, 1024 * (n // 2) : 1024 * (n // 2) + 1024], in_=t[:].rearrange("p a w -> p (a w)"))
+        def load_wkv(n):
+            t = placed("wkv_in%d" % n, [128, 4 * WIDTH], BF16, RAW + 12 * n)
+            wkv_in[n] = t
+            nc.sync.dma_start(out=t[:], in_=wkv_rows[n])
+
+        pair_stage = []
+
+        def w_run(i):
+            if i % 2 == 0:
+                pair_stage.clear()
+                pair_stage.extend([stage_tile("w%d" % i), stage_tile("w%d" % i)])
+            places = [t[:].rearrange("p (a i n u) -> p a i n u", a=2, i=2, u=2)[:, :, i % 2] for t in pair_stage]
+            turn("w%d" % i, [words(raw[i][:], 512 * g) for g in range(4)], places)
+            stages = list(pair_stage)
+
+            def finish():
+                first = 4 if i < 4 else 0
+                for g in range(4):
+                    quantize(cols(w2_mx, RANK * (first + g) + 128 * (i % 4 - 1), 256), E4M3, stages[g // 2][:, 512 * (g % 2) : 512 * (g % 2) + 512])
+
+            return finish
+
+        def z_run(j, h):
+            rows, start = (raw[8 + j][:], 0) if h else (dk[:], DK * j)
+            return plain_run("z%d%d" % (j, h), [words(rows, start + 512 * g) for g in range(4)], cols(dz2_mx, 1024 * j + 512 * h, 512), E5M2)
+
+        def f_run(q):
+            return plain_run("f%d" % q, [words(dk[:], DK * (2 * q + i) + NOPE + 512 * g) for i in range(2) for g in range(2)], cols(rope_mx, 512 * q, 512), E5M2)
+
+        def d_run():
+            return plain_run("d", [words(dc[:], RANK * j) for j in range(4)], latent_mx, E5M2)
+
+        def k_run(n, g):
+            if g == 0:
+                wkv_mx[n] = operand("wkv%d" % n, 3 * 512, None if n < 2 else 64 + 8 * (n - 2))
+            if (n, g) in split:
+                blocks = [split[(n, g)][:, j] for j in range(4)]
+            else:
+                blocks = [words(wkv_in[n][:], WIDTH * j + 512 * g) for j in range(4)]
+            return plain_run("k%d%d" % (n, g), blocks, cols(wkv_mx[n], 512 * g, 512), E4M3)
+
+        split = {}
+
+        def k_split(n, g):
+            t = stage_tile("split")
+            split[(n, g)] = t[:].rearrange("p (j u w) -> p j u w", j=4, u=2)
+            source = wkv_in[n][:].bitcast(F32).rearrange("p (j w) -> p j w", j=4)[:, :, 256 * g : 256 * g + 256]
+            nc.vector.tensor_copy(out=split[(n, g)], in_=source.rearrange("p j (w u) -> p j u w", u=2))
+
+        def tables():
+            for e in range(2):
+                nc.vector.tensor_copy(out=cos_pairs[:, :, e], in_=cos_in[:])
+            nc.vector.tensor_scalar(out=sin_pairs[:, :, 0], in0=sin_in[:], scalar1=-1.0, scalar2=None, op0=MULT)
+            nc.vector.tensor_copy(out=sin_pairs[:, :, 1], in_=sin_in[:])
+
+        def temp():
+            t = placed("temp", [128, 1024], F32, 72, bufs=4)
+            return t
+
+        def rotate(j, first=0, last=HEADS):
+            pairs = dk[:, DK * j : DK * j + DK].rearrange("p (h w) -> p h w", w=HEAD)[:, first:last, 128:HEAD]
+            halves = []
+            for table in (cos_pairs, sin_pairs):
+                half = temp()[:, 0 : 64 * (last - first)]
+                halves.append(half.rearrange("p (h w e) -> p h w e", w=32, e=2))
+                row = table[:, 32 * j : 32 * j + 32, :].rearrange("p w e -> p (w e)")
+                nc.vector.tensor_tensor(out=half.rearrange("p (h w) -> p h w", w=64), in0=pairs, in1=row.unsqueeze(1).to_broadcast([128, last - first, 64]), op=MULT)
+            return lambda: nc.vector.tensor_tensor(out=pairs.rearrange("p h (w e) -> p h w e", e=2), in0=halves[0], in1=halves[1][:, :, :, ::-1], op=ADD)
+
+        def spread_gain():
+            bank = bank_tile("gain")
+            nc.tensor.matmul(bank[:], ones[:], gain_row[:], start=True, stop=True)
+            copy("S", gain[:], bank[:])
+            nc.vector.memset(factors[:, :, 0], 1.0 / RANK)
+            nc.vector.scalar_tensor_tensor(out=factors[:, :, 1], in0=rstd_col[:], scalar=1.0 / RANK, in1=rstd_col[:], op0=MULT, op1=MULT)
+
+        def dh(j):
+            bank = bank_tile("dh%d" % j)
+            for g in range(8):
+                matmul_mx(bank[:], cols(dz2_mx, 1024 * j + 128 * g, 128), E5M2, cols(w2_mx, RANK * g, RANK), E4M3, g == 0, g == 7)
+            t = temp()
+            s, u = t[:, 0:RANK], t[:, RANK : 2 * RANK]
+            c = c_in[:, RANK * j : RANK * j + RANK]
+            one = slice(j, j + 1)
+
+            def first():
+                nc.vector.scalar_tensor_tensor(out=s, in0=bank[:], scalar=rstd_col[:, one], in1=gain[:], op0=MULT, op1=MULT, accum_out=sums[:, j, 0:1])
+
+            def second():
+                nc.vector.scalar_tensor_tensor(out=u, in0=c, scalar=mu_col[:, one], in1=s, op0=SUB, op1=MULT, accum_out=sums[:, j, 1:2])
+
+            def third():
+                nc.vector.tensor_tensor(out=means[:, j, :], in0=sums[:, j, :], in1=factors[:, j, :], op=MULT)
+
+            def fourth():
+                nc.vector.tensor_scalar(out=u, in0=c, scalar1=mu_col[:, one], scalar2=means[:, j, 1:2], op0=SUB, op1=MULT)
+
+            def fifth():
+                nc.vector.scalar_tensor_tensor(out=dc[:, RANK * j : RANK * j + RANK], in0=s, scalar=means[:, j, 0:1], in1=u, op0=SUB, op1=SUB)
+
+            return [first, second, third, fourth, fifth]
+
+        def tokens_beside(source, mx, fmt):
+            stage = stage_tile("beside")
+
+            def lay(engine, first, last):
+                part = stage[:].bitcast(BF16)[:, 4 * first : 4 * last]
+                copy(engine, part.rearrange("p (c i j) -> p c j i", i=4, j=4), source[:, :, first:last].rearrange("p j (c i) -> p c j i", i=4))
+
+            return lay, lambda: quantize(mx, fmt, stage[:])
+
+        x_mx = {}
+
+        def x_block(c):
+            codes = keep.tile([128, 512], U32, name="x_codes", bufs=3, align_bytes=64)
+            scales = keep.tile([128, 512], U8, name="x_scales", bufs=3, align_bytes=64)
+            x_mx[c] = (codes, scales)
+            return tokens_beside(x_in[c // 2][:, :, 512 * (c % 2) : 512 * (c % 2) + 512], (codes[:], scales[:]), E4M3)
+
+        def z_block(n):
+            if n < 2:
+                source = dk[:].rearrange("p (j w) -> p j w", j=4)[:, :, NOPE + 512 * n : NOPE + 512 * n + 512]
+            else:
+                source = dc[:].rearrange("p (j w) -> p j w", j=4)
+            return tokens_beside(source, cols(token_mx, 512 * n, 512), E5M2)
+
+        def out_1_block(m, first, last):
+            row = placed("row", [128, WIDTH], F32, 24, bufs=ROW_BUFS)
+            for n in range(first, last):
+                bank = bank_tile("al%d" % m)
+                matmul_mx(bank[:], cols(x_mx[m // 4], 128 * (m % 4), 128), E4M3, cols(token_mx, 512 * n, 512), E5M2, True, True)
+                if n < last - 1:
+                    copy("S", row[:, 512 * n : 512 * n + 512], bank[:])
+
+            def finish(engine):
+                copy(engine, row[:, 512 * (last - 1) : 512 * last], bank[:])
+                nc.sync.dma_start(out=out_1_rows[:, m, 512 * first : 512 * last], in_=row[:, 512 * first : 512 * last])
+
+            return finish
+
+        pair = {}
+
+        def out_0_block(n, j):
+            if n % 2 == 0:
+                pair[(n // 2, j)] = placed("pair", [128, 1024], F32, 0, bufs=PAIR_BUFS)
+            bank = bank_tile("o%d%d" % (n, j))
+            for g in range(3):
+                left = cols(rope_mx, 256 * j + 128 * g, 128) if g < 2 else cols(latent_mx, 128 * j, 128)
+                matmul_mx(bank[:], left, E5M2, cols(wkv_mx[n], 512 * g, 512), E4M3, g == 0, g == 2)
+            side = pair[(n // 2, j)][:, 512 * (n % 2) : 512 * (n % 2) + 512]
+
+            def finish(engine):
+                copy(engine, side.rearrange("p (q j) -> p q j", j=4), bank[:].rearrange("p (j q) -> p q j", j=4))
+                if n % 2:
+                    nc.sync.dma_start(out=out_0_rows[:, j, 512 * (n - 1) : 512 * (n + 1)], in_=pair[(n // 2, j)][:])
+
+            return finish
 
         ctx.enter_context(tc.manual_schedule())
+        for half in (slice(0, 64), slice(64, 128)):
+            nc.sync.dma_start(out=cos_in[half], in_=cos_rows)
+            nc.sync.dma_start(out=sin_in[half], in_=sin_rows)
 
-        split_names = ["k " + name.split()[1] for step in STEPS for name in step[2] if name.startswith("split")]
-        last_use = {}
-        for s, (run, engines, tasks, products) in enumerate(STEPS):
-            for name in run_inputs(run) if run else []:
-                if name not in split_names:
-                    last_use[name] = s
-            for name in tasks:
-                if name.startswith("split"):
-                    last_use["k " + name.split()[1]] = s
+        def load_dk(j, first=0, last=DK):
+            nc.sync.dma_start(out=dk[:, DK * j + first : DK * j + last], in_=grad_0_rows[:, j, first:last])
 
-        waiting, issued = list(LOADS), []
-        before = None
-        for s, (run, engines, tasks, products) in enumerate(STEPS):
-            while waiting:
-                if buffered(waiting[0]):
-                    if len(issued) >= INPUT_BUFS and last_use[issued[-INPUT_BUFS]] >= s:
-                        break
-                    issued.append(waiting[0])
-                load(waiting.pop(0))
-            banks = transpose_run(run) if run else None
-            while full:
-                empty(*full.pop(0))
-            if before:
-                quantize_run(*before)
-            before = (run, copy_run(banks, engines)) if run else None
-            for name in products:
-                product(name)
-            for name in tasks:
-                task(name)
+        def load_x(h):
+            nc.sync.dma_start(out=x_in[h][:], in_=x_rows[:, :, 1024 * h : 1024 * h + 1024])
+
+        load_dk(0, 0, DK // 2)
+        load_raw(0)
+        load_dk(0, DK // 2, DK)
+        load_raw(1)
+        for j in range(1, 3):
+            load_dk(j)
+            load_raw(2 * j)
+            load_raw(2 * j + 1)
+        nc.sync.dma_start(out=mu_col[:], in_=mu_rows)
+        nc.sync.dma_start(out=rstd_col[:], in_=rstd_rows)
+        nc.sync.dma_start(out=gain_row[0:1, :], in_=kvn_g.rearrange("(o w) -> o w", o=1))
+        for i in range(6, 9):
+            load_raw(i)
+        load_dk(3)
+        load_raw(9)
+        load_x(0)
+        load_raw(10)
+        nc.sync.dma_start(out=c_in[:], in_=c_lat_rows)
+        load_raw(11)
+
+        tables()
+        add_low = rotate(0, 0, HEADS // 2)
+        add_high = rotate(0, HEADS // 2, HEADS)
+        add_low()
+        add_high()
+        w_run(0)
+        finish_w = w_run(1)
+        finish_z = z_run(0, 0)
+        finish_w()
+        for j in (1, 2):
+            w_run(2 * j)
+            finish_w = w_run(2 * j + 1)
+            add_up = rotate(j)
+            finish_z()
+            add_up()
+            if j == 1:
+                finish_z = z_run(1, 0)
+            finish_w()
+        finish_f0 = f_run(0)
+        load_wkv(0)
+        load_wkv(1)
+        load_x(1)
+        w_run(6)
+        finish_w = w_run(7)
+        finish_a0 = z_run(0, 1)
+        finish_w()
+        finish_n2 = z_run(2, 0)
+        finish_a0()
+        finish_a1 = z_run(1, 1)
+        spread_gain()
+        add_up = rotate(3)
+        finish_a1()
+        add_up()
+        norm = {0: dh(0)}
+        finish_f0()
+        lay, finish_x = x_block(0)
+        lay("S", 0, 512)
+        finish_a2 = z_run(2, 1)
+        norm[1] = dh(1)
+        finish_n3 = z_run(3, 0)
+        finish_a3 = z_run(3, 1)
+        load_wkv(2)
+        load_wkv(3)
+        lay, finish_z0 = z_block(0)
+        lay("S", 0, 512)
+        norm[0][0]()
+        finish_n2()
+        norm[0][1]()
+        finish_a2()
+        norm[0][2]()
+        finish_x()
+        norm[1][0]()
+        norm[0][3]()
+        norm[1][1]()
+        norm[0][4]()
+        finish_n3()
+        norm[1][2]()
+        finish_a3()
+        norm[1][3]()
+        norm[2] = dh(2)
+        finish_f1 = f_run(1)
+        norm[3] = dh(3)
+        lay, finish_z1 = z_block(1)
+        lay("S", 0, 512)
+        norm[2][0]()
+        norm[1][4]()
+        norm[2][1]()
+        finish_z0()
+        norm[2][2]()
+        norm[3][0]()
+        norm[2][3]()
+        norm[3][1]()
+        norm[2][4]()
+        norm[3][2]()
+        norm[3][3]()
+        finish_z1()
+        norm[3][4]()
+        lay, finish_z2 = z_block(2)
+        lay("V", 0, 512)
+        finish_f1()
+        finish_z2()
+        runs = [(n, g) for n in range(4) for g in range(3)]
+        finish_k0 = k_run(0, 0)
+        finish_k1 = k_run(0, 1)
+        lay, finish_x = x_block(1)
+        out_1_block(0, 0, 2)("S")
+        out_1_block(1, 0, 2)("S")
+        finish_d = d_run()
+        finish_k0()
+        lay("V", 0, 512)
+        finish_k1()
+        out_1_block(2, 0, 3)("V")
+        finish_x()
+        finish_k = k_run(0, 2)
+        finish_d()
+        finish_row = out_1_block(3, 0, 3)
+        for s in range(3, 15):
+            m = s + 1
+            finish_last = finish_k
+            if s < 12:
+                finish_k = k_run(runs[s][0], runs[s][1])
+            finish_row("V")
+            if s < 13:
+                finish_last()
+            if SPLIT_FROM <= s + 2 < 12:
+                k_split(*runs[s + 2])
+            if s < 5:
+                out_1_block(s - 3, 2, 3)("V" if s % 2 else "S")
+            if s >= 7:
+                out_0_block((s - 7) % 2, (s - 7) // 2)("V" if s % 2 else "S")
+            if m < 12 and m % 4 == 0:
+                lay, finish_x = x_block(m // 4 + 1)
+            if m < 12 and m % 4 < 2:
+                lay("V", 256 * (m % 4), 256 * (m % 4) + 256)
+            if m < 12 and m % 4 == 2:
+                finish_x()
+            if s >= 13:
+                out_0_block(2, s - 13)("S")
+                out_0_block(3, s - 13)("V")
+            finish_row = out_1_block(m, 0, 3)
+        finish_row("V")
+        for j in (2, 3):
+            out_0_block(2, j)("S")
+            out_0_block(3, j)("V")

@@ -29,7 +29,8 @@ KIB = 1024
 STAGE_BUFS = 9
 ROW_BUFS = 6
 PAIR_BUFS = 6
-SPLIT_FROM = 6
+SPLIT_FROM = 2
+BOTH_FROM = 3
 VECTOR_EVERY = 3
 
 
@@ -118,7 +119,7 @@ def tile_mla_pa_v_kernel(
         def words(rows, start):
             return rows.bitcast(F32)[:, start // 2 : start // 2 + 256].rearrange("p (w u) -> p u w", u=2)
 
-        def turn(name, blocks, places):
+        def turn(name, blocks, places, engines="SS"):
             banks = []
             for b in range(2):
                 bank = bank_tile(name)
@@ -127,12 +128,12 @@ def tile_mla_pa_v_kernel(
                     for u in range(2):
                         nc.tensor.transpose(banks[b][:, a, u, :], blocks[2 * b + a][:, u, :], identity[:])
             for b in range(2):
-                copy("S", places[b], banks[b].rearrange("p a u n -> p a n u"))
+                copy(engines[b], places[b], banks[b].rearrange("p a u n -> p a n u"))
 
-        def plain_run(name, blocks, mx, fmt):
+        def plain_run(name, blocks, mx, fmt, engines="SS"):
             stage = stage_tile(name)
             halves = stage[:].rearrange("p (b a n u) -> p b a n u", b=2, a=2, u=2)
-            turn(name, blocks, [halves[:, b] for b in range(2)])
+            turn(name, blocks, [halves[:, b] for b in range(2)], engines)
             return lambda: quantize(mx, fmt, stage[:])
 
         raw = {}
@@ -177,17 +178,17 @@ def tile_mla_pa_v_kernel(
         def f_run(q):
             return plain_run("f%d" % q, [words(dk[:], DK * (2 * q + i) + NOPE + 512 * g) for i in range(2) for g in range(2)], cols(rope_mx, 512 * q, 512), E5M2)
 
-        def d_run():
-            return plain_run("d", [words(dc[:], RANK * j) for j in range(4)], latent_mx, E5M2)
+        def d_run(engines):
+            return plain_run("d", [words(dc[:], RANK * j) for j in range(4)], latent_mx, E5M2, engines)
 
-        def k_run(n, g):
+        def k_run(n, g, engines="SS"):
             if g == 0:
-                wkv_mx[n] = operand("wkv%d" % n, 3 * 512, None if n < 2 else 64 + 8 * (n - 2))
+                wkv_mx[n] = operand("wkv%d" % n, 3 * 512, (136, 144, 64, 72)[n])
             if (n, g) in split:
                 blocks = [split[(n, g)][:, j] for j in range(4)]
             else:
                 blocks = [words(wkv_in[n][:], WIDTH * j + 512 * g) for j in range(4)]
-            return plain_run("k%d%d" % (n, g), blocks, cols(wkv_mx[n], 512 * g, 512), E4M3)
+            return plain_run("k%d%d" % (n, g), blocks, cols(wkv_mx[n], 512 * g, 512), E4M3, engines)
 
         split = {}
 
@@ -221,6 +222,8 @@ def tile_mla_pa_v_kernel(
             bank = bank_tile("gain")
             nc.tensor.matmul(bank[:], ones[:], gain_row[:], start=True, stop=True)
             copy("S", gain[:], bank[:])
+
+        def norm_factors():
             nc.vector.memset(factors[:, :, 0], 1.0 / RANK)
             nc.vector.scalar_tensor_tensor(out=factors[:, :, 1], in0=rstd_col[:], scalar=1.0 / RANK, in1=rstd_col[:], op0=MULT, op1=MULT)
 
@@ -228,30 +231,31 @@ def tile_mla_pa_v_kernel(
             bank = bank_tile("dh%d" % j)
             for g in range(8):
                 matmul_mx(bank[:], cols(dz2_mx, 1024 * j + 128 * g, 128), E5M2, cols(w2_mx, RANK * g, RANK), E4M3, g == 0, g == 7)
-            t = temp()
-            s, u = t[:, 0:RANK], t[:, RANK : 2 * RANK]
+            part = []
             c = c_in[:, RANK * j : RANK * j + RANK]
             one = slice(j, j + 1)
 
             def first():
-                nc.vector.scalar_tensor_tensor(out=s, in0=bank[:], scalar=rstd_col[:, one], in1=gain[:], op0=MULT, op1=MULT, accum_out=sums[:, j, 0:1])
+                t = temp()
+                part.extend([t[:, 0:RANK], t[:, RANK : 2 * RANK]])
+                nc.vector.scalar_tensor_tensor(out=part[0], in0=bank[:], scalar=rstd_col[:, one], in1=gain[:], op0=MULT, op1=MULT, accum_out=sums[:, j, 0:1])
 
             def second():
-                nc.vector.scalar_tensor_tensor(out=u, in0=c, scalar=mu_col[:, one], in1=s, op0=SUB, op1=MULT, accum_out=sums[:, j, 1:2])
+                nc.vector.scalar_tensor_tensor(out=part[1], in0=c, scalar=mu_col[:, one], in1=part[0], op0=SUB, op1=MULT, accum_out=sums[:, j, 1:2])
 
             def third():
                 nc.vector.tensor_tensor(out=means[:, j, :], in0=sums[:, j, :], in1=factors[:, j, :], op=MULT)
 
             def fourth():
-                nc.vector.tensor_scalar(out=u, in0=c, scalar1=mu_col[:, one], scalar2=means[:, j, 1:2], op0=SUB, op1=MULT)
+                nc.vector.tensor_scalar(out=part[1], in0=c, scalar1=mu_col[:, one], scalar2=means[:, j, 1:2], op0=SUB, op1=MULT)
 
             def fifth():
-                nc.vector.scalar_tensor_tensor(out=dc[:, RANK * j : RANK * j + RANK], in0=s, scalar=means[:, j, 0:1], in1=u, op0=SUB, op1=SUB)
+                nc.vector.scalar_tensor_tensor(out=dc[:, RANK * j : RANK * j + RANK], in0=part[0], scalar=means[:, j, 0:1], in1=part[1], op0=SUB, op1=SUB)
 
             return [first, second, third, fourth, fifth]
 
-        def tokens_beside(source, mx, fmt):
-            stage = stage_tile("beside")
+        def tokens_beside(source, mx, fmt, early):
+            stage = placed("beside", [128, 1024], F32, 136, bufs=4) if early else stage_tile("beside")
 
             def lay(engine, first, last):
                 part = stage[:].bitcast(BF16)[:, 4 * first : 4 * last]
@@ -265,26 +269,45 @@ def tile_mla_pa_v_kernel(
             codes = keep.tile([128, 512], U32, name="x_codes", bufs=3, align_bytes=64)
             scales = keep.tile([128, 512], U8, name="x_scales", bufs=3, align_bytes=64)
             x_mx[c] = (codes, scales)
-            return tokens_beside(x_in[c // 2][:, :, 512 * (c % 2) : 512 * (c % 2) + 512], (codes[:], scales[:]), E4M3)
+            return tokens_beside(x_in[c // 2][:, :, 512 * (c % 2) : 512 * (c % 2) + 512], (codes[:], scales[:]), E4M3, c < 2)
 
         def z_block(n):
             if n < 2:
                 source = dk[:].rearrange("p (j w) -> p j w", j=4)[:, :, NOPE + 512 * n : NOPE + 512 * n + 512]
             else:
                 source = dc[:].rearrange("p (j w) -> p j w", j=4)
-            return tokens_beside(source, cols(token_mx, 512 * n, 512), E5M2)
+            return tokens_beside(source, cols(token_mx, 512 * n, 512), E5M2, n < 2)
 
-        def out_1_block(m, first, last):
+        def out_1_bank(m, n):
+            bank = bank_tile("al%d" % m)
+            matmul_mx(bank[:], cols(x_mx[m // 4], 128 * (m % 4), 128), E4M3, cols(token_mx, 512 * n, 512), E5M2, True, True)
+            return bank
+
+        def two_banks_tile():
+            return placed("pair", [128, 1024], F32, 0, bufs=PAIR_BUFS)
+
+        def rope_part(m, engines):
+            t = two_banks_tile()
+            for n in range(2):
+                copy(engines[n], t[:, 512 * n : 512 * n + 512], out_1_bank(m, n)[:])
+            return lambda: nc.sync.dma_start(out=out_1_rows[:, m, 0:ROPE], in_=t[:])
+
+        def latent_part(m, engines):
+            t = two_banks_tile()
+            for i in range(2):
+                copy(engines[i], t[:, 512 * i : 512 * i + 512], out_1_bank(m + i, 2)[:])
+            nc.sync.dma_start(out=out_1_rows[:, m : m + 2, ROPE:WIDTH], in_=t[:].rearrange("p (i w) -> p i w", i=2))
+
+        def whole_rows(m, second):
             row = placed("row", [128, WIDTH], F32, 24, bufs=ROW_BUFS)
-            for n in range(first, last):
-                bank = bank_tile("al%d" % m)
-                matmul_mx(bank[:], cols(x_mx[m // 4], 128 * (m % 4), 128), E4M3, cols(token_mx, 512 * n, 512), E5M2, True, True)
-                if n < last - 1:
-                    copy("S", row[:, 512 * n : 512 * n + 512], bank[:])
+            for n in range(3):
+                bank = out_1_bank(m, n)
+                if n < 2:
+                    copy(("S", second)[n], row[:, 512 * n : 512 * n + 512], bank[:])
 
             def finish(engine):
-                copy(engine, row[:, 512 * (last - 1) : 512 * last], bank[:])
-                nc.sync.dma_start(out=out_1_rows[:, m, 512 * first : 512 * last], in_=row[:, 512 * first : 512 * last])
+                copy(engine, row[:, ROPE:WIDTH], bank[:])
+                nc.sync.dma_start(out=out_1_rows[:, m, :], in_=row[:])
 
             return finish
 
@@ -292,7 +315,7 @@ def tile_mla_pa_v_kernel(
 
         def out_0_block(n, j):
             if n % 2 == 0:
-                pair[(n // 2, j)] = placed("pair", [128, 1024], F32, 0, bufs=PAIR_BUFS)
+                pair[(n // 2, j)] = two_banks_tile()
             bank = bank_tile("o%d%d" % (n, j))
             for g in range(3):
                 left = cols(rope_mx, 256 * j + 128 * g, 128) if g < 2 else cols(latent_mx, 128 * j, 128)
@@ -311,153 +334,159 @@ def tile_mla_pa_v_kernel(
             nc.sync.dma_start(out=cos_in[half], in_=cos_rows)
             nc.sync.dma_start(out=sin_in[half], in_=sin_rows)
 
-        def load_dk(j, first=0, last=DK):
-            nc.sync.dma_start(out=dk[:, DK * j + first : DK * j + last], in_=grad_0_rows[:, j, first:last])
+        def load_dk(j):
+            nc.sync.dma_start(out=dk[:, DK * j : DK * j + DK], in_=grad_0_rows[:, j, :])
 
         def load_x(h):
             nc.sync.dma_start(out=x_in[h][:], in_=x_rows[:, :, 1024 * h : 1024 * h + 1024])
 
-        load_dk(0, 0, DK // 2)
-        load_raw(0)
-        load_dk(0, DK // 2, DK)
-        load_raw(1)
-        for j in range(1, 3):
-            load_dk(j)
-            load_raw(2 * j)
-            load_raw(2 * j + 1)
-        nc.sync.dma_start(out=mu_col[:], in_=mu_rows)
-        nc.sync.dma_start(out=rstd_col[:], in_=rstd_rows)
+        load_dk(0)
+        load_dk(1)
         nc.sync.dma_start(out=gain_row[0:1, :], in_=kvn_g.rearrange("(o w) -> o w", o=1))
-        for i in range(6, 9):
+        for i in range(0, 3):
+            load_raw(i)
+        load_dk(2)
+        for i in range(3, 8):
             load_raw(i)
         load_dk(3)
-        load_raw(9)
+        nc.sync.dma_start(out=mu_col[:], in_=mu_rows)
+        nc.sync.dma_start(out=rstd_col[:], in_=rstd_rows)
+        for i in range(8, 12):
+            load_raw(i)
         load_x(0)
-        load_raw(10)
         nc.sync.dma_start(out=c_in[:], in_=c_lat_rows)
-        load_raw(11)
 
         tables()
-        add_low = rotate(0, 0, HEADS // 2)
-        add_high = rotate(0, HEADS // 2, HEADS)
-        add_low()
-        add_high()
+        spread_gain()
+        add_0 = rotate(0)
+        add_1 = rotate(1)
+        add_0()
+        add_1()
         w_run(0)
-        finish_w = w_run(1)
-        finish_z = z_run(0, 0)
-        finish_w()
-        for j in (1, 2):
-            w_run(2 * j)
-            finish_w = w_run(2 * j + 1)
-            add_up = rotate(j)
-            finish_z()
-            add_up()
-            if j == 1:
-                finish_z = z_run(1, 0)
-            finish_w()
-        finish_f0 = f_run(0)
+        q_w0 = w_run(1)
+        w_run(2)
+        q_z0 = z_run(0, 0)
+        q_z1 = z_run(1, 0)
+        q_w1 = w_run(3)
         load_wkv(0)
+        q_w0()
+        add_2 = rotate(2)
+        q_z0()
+        add_2()
+        q_w1()
+        w_run(4)
+        q_w2 = w_run(5)
         load_wkv(1)
         load_x(1)
+        q_z1()
         w_run(6)
-        finish_w = w_run(7)
-        finish_a0 = z_run(0, 1)
-        finish_w()
-        finish_n2 = z_run(2, 0)
-        finish_a0()
-        finish_a1 = z_run(1, 1)
-        spread_gain()
-        add_up = rotate(3)
-        finish_a1()
-        add_up()
-        norm = {0: dh(0)}
-        finish_f0()
-        lay, finish_x = x_block(0)
-        lay("S", 0, 512)
-        finish_a2 = z_run(2, 1)
-        norm[1] = dh(1)
-        finish_n3 = z_run(3, 0)
-        finish_a3 = z_run(3, 1)
+        q_w3 = w_run(7)
+        q_w2()
+        q_f0 = f_run(0)
+        q_z2 = z_run(2, 0)
+        add_3 = rotate(3)
+        q_w3()
+        add_3()
+        q_a = [z_run(j, 1) for j in range(4)]
         load_wkv(2)
-        load_wkv(3)
-        lay, finish_z0 = z_block(0)
-        lay("S", 0, 512)
-        norm[0][0]()
-        finish_n2()
-        norm[0][1]()
-        finish_a2()
-        norm[0][2]()
-        finish_x()
-        norm[1][0]()
-        norm[0][3]()
-        norm[1][1]()
-        norm[0][4]()
-        finish_n3()
-        norm[1][2]()
-        finish_a3()
-        norm[1][3]()
+        q_a[0]()
+        q_z3 = z_run(3, 0)
+        q_f1 = f_run(1)
+        norm_factors()
+        q_a[1]()
+        norm = {0: dh(0), 1: dh(1)}
+        lay_z0, q_t0 = z_block(0)
+        lay_z1, q_t1 = z_block(1)
+        lay_x, q_x = x_block(0)
+        lay_z0("V", 0, 256)
+        lay_z1("V", 0, 256)
+        lay_z0("S", 256, 512)
+        lay_z1("S", 256, 512)
+        q_z2()
+        q_a[2]()
         norm[2] = dh(2)
-        finish_f1 = f_run(1)
-        norm[3] = dh(3)
-        lay, finish_z1 = z_block(1)
-        lay("S", 0, 512)
+        lay_x1, q_x1 = x_block(1)
+        lay_x1("S", 0, 512)
+        q_k = [k_run(0, 0)]
+        lay_x("V", 0, 512)
+        q_f0()
+        norm[0][0]()
+        q_x()
+        q_t0()
+        norm[1][0]()
+        q_t1()
+        stores = [rope_part(0, "SS"), rope_part(1, "SS")]
+        norm[0][1]()
+        q_z3()
+        norm[1][1]()
+        q_a[3]()
         norm[2][0]()
-        norm[1][4]()
+        norm[0][2]()
+        norm[1][2]()
+        norm[3] = dh(3)
+        stores += [rope_part(2, "SS"), rope_part(3, "SS")]
+        q_k.append(k_run(0, 1))
         norm[2][1]()
-        finish_z0()
+        norm[0][3]()
+        q_x1()
         norm[2][2]()
+        norm[1][3]()
         norm[3][0]()
-        norm[2][3]()
+        norm[0][4]()
         norm[3][1]()
-        norm[2][4]()
+        norm[1][4]()
         norm[3][2]()
+        norm[2][3]()
         norm[3][3]()
-        finish_z1()
+        norm[2][4]()
         norm[3][4]()
-        lay, finish_z2 = z_block(2)
-        lay("V", 0, 512)
-        finish_f1()
-        finish_z2()
-        runs = [(n, g) for n in range(4) for g in range(3)]
-        finish_k0 = k_run(0, 0)
-        finish_k1 = k_run(0, 1)
-        lay, finish_x = x_block(1)
-        out_1_block(0, 0, 2)("S")
-        out_1_block(1, 0, 2)("S")
-        finish_d = d_run()
-        finish_k0()
-        lay("V", 0, 512)
-        finish_k1()
-        out_1_block(2, 0, 3)("V")
-        finish_x()
-        finish_k = k_run(0, 2)
-        finish_d()
-        finish_row = out_1_block(3, 0, 3)
-        for s in range(3, 15):
-            m = s + 1
-            finish_last = finish_k
-            if s < 12:
-                finish_k = k_run(runs[s][0], runs[s][1])
+        q_f1()
+        for store in stores:
+            store()
+        load_wkv(3)
+        for m in (4, 6):
+            rope_part(m, "SS")()
+            rope_part(m + 1, "SS")()
+            q_k.append(k_run(m // 6, 2 * (1 - m // 6)))
+        lay_z2, q_t2 = z_block(2)
+        lay_z2("V", 0, 512)
+        q_k[0]()
+        q_t2()
+        q_d = d_run("SV")
+        latent_part(0, "SV")
+        q_k[1]()
+        latent_part(2, "SV")
+        lay_x, q_x = x_block(2)
+        lay_x("V", 0, 512)
+        q_k.append(k_run(1, 1))
+        q_k[2]()
+        q_x()
+        latent_part(4, "SV")
+        q_d()
+        latent_part(6, "SV")
+        q_k[3]()
+        q_last = k_run(1, 2)
+        q_k[4]()
+        runs = [(n, g) for n in (2, 3) for g in range(3)]
+        finish_row = whole_rows(8, "S")
+        for s in range(7):
+            if s < 6:
+                q_next = k_run(*runs[s])
             finish_row("V")
-            if s < 13:
-                finish_last()
-            if SPLIT_FROM <= s + 2 < 12:
+            q_last()
+            q_last = q_next
+            if SPLIT_FROM <= s + 2 < 6:
                 k_split(*runs[s + 2])
-            if s < 5:
-                out_1_block(s - 3, 2, 3)("V" if s % 2 else "S")
-            if s >= 7:
-                out_0_block((s - 7) % 2, (s - 7) // 2)("V" if s % 2 else "S")
-            if m < 12 and m % 4 == 0:
-                lay, finish_x = x_block(m // 4 + 1)
-            if m < 12 and m % 4 < 2:
-                lay("V", 256 * (m % 4), 256 * (m % 4) + 256)
-            if m < 12 and m % 4 == 2:
-                finish_x()
-            if s >= 13:
-                out_0_block(2, s - 13)("S")
-                out_0_block(3, s - 13)("V")
-            finish_row = out_1_block(m, 0, 3)
+            out_0_block(s % 2, s // 2)("V" if s % 2 else "S")
+            if s == 0:
+                lay_x, q_x = x_block(3)
+            if s < 2:
+                lay_x("V", 256 * s, 256 * s + 256)
+            if s == 2:
+                q_x()
+            finish_row = whole_rows(9 + s, "V" if s >= BOTH_FROM else "S")
         finish_row("V")
-        for j in (2, 3):
-            out_0_block(2, j)("S")
-            out_0_block(3, j)("V")
+        out_0_block(1, 3)("S")
+        for j in range(4):
+            out_0_block(2, j)("V")
+            out_0_block(3, j)("S")

@@ -30,7 +30,7 @@ STAGE_BUFS = 9
 ROW_BUFS = 6
 PAIR_BUFS = 6
 SPLIT_FROM = 2
-BOTH_FROM = 3
+BOTH_FROM = 4
 VECTOR_EVERY = 3
 
 
@@ -42,8 +42,8 @@ def tile_mla_pa_v_kernel(
     grad_0_rows = grad_0.rearrange("b s h d -> (b s) (h d)").rearrange("(p j) w -> p j w", j=4)
     grad_1_rows = grad_1.rearrange("b s h d -> (b s) (h d)").rearrange("(p j) w -> p j w", j=4)
     c_lat_rows = c_lat.flatten_outer_dims().rearrange("(p j) w -> p (j w)", j=4)
-    mu_rows = mu.flatten_outer_dims().rearrange("(p j) o -> p (j o)", j=4)
-    rstd_rows = rstd.flatten_outer_dims().rearrange("(p j) o -> p (j o)", j=4)
+    mu_row = mu.flatten_outer_dims().rearrange("t o -> o t")
+    rstd_row = rstd.flatten_outer_dims().rearrange("t o -> o t")
     wkv_rows = wkv_a_w.rearrange("(n p j) w -> n p (j w)", p=128, j=4)
     out_0_rows = out_0.flatten_outer_dims().rearrange("(p j) w -> p j w", j=4)
     out_1_rows = out_1.rearrange("(m p) w -> p m w", p=128)
@@ -66,14 +66,16 @@ def tile_mla_pa_v_kernel(
         ones = kept("ones", [128, 128], BF16)
         nc.gpsimd.memset(ones[:], 1.0)
         gain_row = kept("gain_row", [128, RANK], BF16)
-        nc.gpsimd.memset(gain_row[:], 0.0)
+        nc.vector.memset(gain_row[:], 0.0)
         gain = kept("gain", [128, RANK], F32)
         cos_in = kept("cos_in", [128, 128], BF16)
         sin_in = kept("sin_in", [128, 128], BF16)
         cos_pairs = kept("cos_pairs", [128, 128, 2], BF16)
         sin_pairs = kept("sin_pairs", [128, 128, 2], BF16)
-        mu_col = kept("mu_col", [128, 4], F32)
-        rstd_col = kept("rstd_col", [128, 4], F32)
+        stat_rows = placed("stat_rows", [128, 512], F32, 44)
+        nc.vector.memset(stat_rows[:], 0.0)
+        stats = kept("stats", [128, 4, 2], F32)
+        mu_col, rstd_col = stats[:, :, 0], stats[:, :, 1]
         factors = kept("factors", [128, 4, 2], F32)
         sums = kept("sums", [128, 4, 2], F32)
         means = kept("means", [128, 4, 2], F32)
@@ -101,6 +103,8 @@ def tile_mla_pa_v_kernel(
         def copy(engine, out, in_):
             if engine == "V":
                 nc.vector.tensor_copy(out=out, in_=in_)
+            elif engine == "G":
+                nc.gpsimd.tensor_scalar(out=out, in0=in_, scalar1=1.0, scalar2=0.0, op0=MULT, op1=ADD)
             else:
                 nc.scalar.copy(out=out, in_=in_)
 
@@ -223,9 +227,15 @@ def tile_mla_pa_v_kernel(
             nc.tensor.matmul(bank[:], ones[:], gain_row[:], start=True, stop=True)
             copy("S", gain[:], bank[:])
 
+        def stat_columns():
+            bank = bank_tile("stats")
+            for j in range(4):
+                nc.tensor.transpose(bank[:, 128 * j : 128 * j + 128], stat_rows[:].rearrange("o (p j) -> o j p", j=4)[:, j, :], identity[:])
+            copy("S", stats[:], bank[:].rearrange("p (j o) -> p j o", j=4)[:, :, 0:2])
+
         def norm_factors():
             nc.vector.memset(factors[:, :, 0], 1.0 / RANK)
-            nc.vector.scalar_tensor_tensor(out=factors[:, :, 1], in0=rstd_col[:], scalar=1.0 / RANK, in1=rstd_col[:], op0=MULT, op1=MULT)
+            nc.vector.scalar_tensor_tensor(out=factors[:, :, 1], in0=rstd_col, scalar=1.0 / RANK, in1=rstd_col, op0=MULT, op1=MULT)
 
         def dh(j):
             bank = bank_tile("dh%d" % j)
@@ -324,7 +334,9 @@ def tile_mla_pa_v_kernel(
 
             def finish(engine):
                 copy(engine, side.rearrange("p (q j) -> p q j", j=4), bank[:].rearrange("p (j q) -> p q j", j=4))
-                if n % 2:
+                if (n // 2, j) == (1, 3):
+                    nc.sync.dma_start(out=out_0_rows[:, j, 512 * n : 512 * n + 512], in_=side)
+                elif n % 2:
                     nc.sync.dma_start(out=out_0_rows[:, j, 512 * (n - 1) : 512 * (n + 1)], in_=pair[(n // 2, j)][:])
 
             return finish
@@ -341,40 +353,44 @@ def tile_mla_pa_v_kernel(
             nc.sync.dma_start(out=x_in[h][:], in_=x_rows[:, :, 1024 * h : 1024 * h + 1024])
 
         load_dk(0)
-        load_dk(1)
         nc.sync.dma_start(out=gain_row[0:1, :], in_=kvn_g.rearrange("(o w) -> o w", o=1))
-        for i in range(0, 3):
+        nc.sync.dma_start(out=stat_rows[0:1, :], in_=mu_row)
+        nc.sync.dma_start(out=stat_rows[1:2, :], in_=rstd_row)
+        load_raw(0)
+        load_raw(1)
+        load_dk(1)
+        for i in range(2, 5):
             load_raw(i)
         load_dk(2)
-        for i in range(3, 8):
+        for i in range(5, 8):
             load_raw(i)
         load_dk(3)
-        nc.sync.dma_start(out=mu_col[:], in_=mu_rows)
-        nc.sync.dma_start(out=rstd_col[:], in_=rstd_rows)
         for i in range(8, 12):
             load_raw(i)
         load_x(0)
-        nc.sync.dma_start(out=c_in[:], in_=c_lat_rows)
 
         tables()
         spread_gain()
+        stat_columns()
         add_0 = rotate(0)
-        add_1 = rotate(1)
+        norm_factors()
         add_0()
-        add_1()
         w_run(0)
         q_w0 = w_run(1)
-        w_run(2)
         q_z0 = z_run(0, 0)
-        q_z1 = z_run(1, 0)
-        q_w1 = w_run(3)
-        load_wkv(0)
+        add_1 = rotate(1)
         q_w0()
-        add_2 = rotate(2)
-        q_z0()
-        add_2()
-        q_w1()
+        add_1()
+        w_run(2)
+        q_w1 = w_run(3)
         w_run(4)
+        q_z1 = z_run(1, 0)
+        load_wkv(0)
+        nc.sync.dma_start(out=c_in[:], in_=c_lat_rows)
+        q_z0()
+        add_2 = rotate(2)
+        q_w1()
+        add_2()
         q_w2 = w_run(5)
         load_wkv(1)
         load_x(1)
@@ -385,107 +401,111 @@ def tile_mla_pa_v_kernel(
         q_f0 = f_run(0)
         q_z2 = z_run(2, 0)
         add_3 = rotate(3)
-        q_w3()
+        q_f0()
         add_3()
+        q_w3()
         q_a = [z_run(j, 1) for j in range(4)]
         load_wkv(2)
         q_a[0]()
         q_z3 = z_run(3, 0)
         q_f1 = f_run(1)
-        norm_factors()
         q_a[1]()
-        norm = {0: dh(0), 1: dh(1)}
+        def lay_on_gpsimd(lay):
+            for part in range(4):
+                lay("G", 128 * part, 128 * part + 128)
+
+        norm = [dh(0)]
         lay_z0, q_t0 = z_block(0)
         lay_z1, q_t1 = z_block(1)
-        lay_x, q_x = x_block(0)
-        lay_z0("V", 0, 256)
-        lay_z1("V", 0, 256)
-        lay_z0("S", 256, 512)
-        lay_z1("S", 256, 512)
+        lay_x, q_x0 = x_block(0)
+        lay_on_gpsimd(lay_x)
+        lay_x, q_x1 = x_block(1)
+        lay_on_gpsimd(lay_x)
+        lay_z0("S", 0, 512)
         q_z2()
         q_a[2]()
-        norm[2] = dh(2)
-        lay_x1, q_x1 = x_block(1)
-        lay_x1("S", 0, 512)
-        q_k = [k_run(0, 0)]
-        lay_x("V", 0, 512)
-        q_f0()
-        norm[0][0]()
-        q_x()
-        q_t0()
-        norm[1][0]()
-        q_t1()
-        stores = [rope_part(0, "SS"), rope_part(1, "SS")]
-        norm[0][1]()
+        lay_z1("V", 0, 256)
         q_z3()
-        norm[1][1]()
         q_a[3]()
-        norm[2][0]()
-        norm[0][2]()
-        norm[1][2]()
-        norm[3] = dh(3)
-        stores += [rope_part(2, "SS"), rope_part(3, "SS")]
-        q_k.append(k_run(0, 1))
-        norm[2][1]()
-        norm[0][3]()
-        q_x1()
-        norm[2][2]()
-        norm[1][3]()
-        norm[3][0]()
-        norm[0][4]()
-        norm[3][1]()
-        norm[1][4]()
-        norm[3][2]()
-        norm[2][3]()
-        norm[3][3]()
-        norm[2][4]()
-        norm[3][4]()
+        q_k = [k_run(0, 0)]
+        norm.append(dh(1))
+        lay_z1("S", 256, 512)
+        norm[0][0]()
+        q_t0()
         q_f1()
+        q_k.append(k_run(0, 1))
+        norm.append(dh(2))
+        norm[0][1]()
+        q_x0()
+        norm[0][2]()
+        norm[1][0]()
+        norm[0][3]()
+        q_t1()
+        norm[1][1]()
+        norm[0][4]()
+        norm[1][2]()
+        stores = [rope_part(0, "SS"), rope_part(1, "SS")]
+        norm.append(dh(3))
+        norm[2][0]()
+        norm[1][3]()
+        norm[2][1]()
+        norm[1][4]()
+        norm[2][2]()
+        q_x1()
+        norm[2][3]()
+        stores += [rope_part(2, "SS"), rope_part(3, "SS")]
+        q_k.append(k_run(0, 2))
+        norm[3][0]()
+        norm[2][4]()
+        norm[3][1]()
+        norm[3][2]()
+        norm[3][3]()
         for store in stores:
             store()
         load_wkv(3)
-        for m in (4, 6):
-            rope_part(m, "SS")()
-            rope_part(m + 1, "SS")()
-            q_k.append(k_run(m // 6, 2 * (1 - m // 6)))
-        lay_z2, q_t2 = z_block(2)
-        lay_z2("V", 0, 512)
-        q_k[0]()
-        q_t2()
-        q_d = d_run("SV")
-        latent_part(0, "SV")
-        q_k[1]()
-        latent_part(2, "SV")
+        rope_part(4, "SS")()
+        norm[3][4]()
         lay_x, q_x = x_block(2)
-        lay_x("V", 0, 512)
-        q_k.append(k_run(1, 1))
+        lay_on_gpsimd(lay_x)
+        lay_z2, q_t2 = z_block(2)
+        q_k[0]()
+        lay_z2("V", 0, 512)
+        q_k[1]()
+        rope_part(5, "SS")()
+        q_k.append(k_run(1, 0))
+        q_t2()
+        rope_part(6, "SV")()
+        rope_part(7, "SV")()
+        q_d = d_run("SS")
         q_k[2]()
         q_x()
-        latent_part(4, "SV")
-        q_d()
-        latent_part(6, "SV")
+        latent_part(0, "SV")
         q_k[3]()
-        q_last = k_run(1, 2)
-        q_k[4]()
-        runs = [(n, g) for n in (2, 3) for g in range(3)]
-        finish_row = whole_rows(8, "S")
-        for s in range(7):
-            if s < 6:
+        latent_part(2, "SV")
+        q_last = k_run(1, 1)
+        q_d()
+        latent_part(4, "SV")
+        latent_part(6, "SV")
+        lay_x, q_x = x_block(3)
+        lay_on_gpsimd(lay_x)
+        runs = [(1, 2)] + [(n, g) for n in (2, 3) for g in range(3)]
+        finish_row = None
+        for s in range(8):
+            if s < 7:
                 q_next = k_run(*runs[s])
-            finish_row("V")
+            if SPLIT_FROM <= s + 1 < 7:
+                k_split(*runs[s + 1])
+            if finish_row:
+                finish_row("V")
             q_last()
             q_last = q_next
-            if SPLIT_FROM <= s + 2 < 6:
-                k_split(*runs[s + 2])
-            out_0_block(s % 2, s // 2)("V" if s % 2 else "S")
-            if s == 0:
-                lay_x, q_x = x_block(3)
-            if s < 2:
-                lay_x("V", 256 * s, 256 * s + 256)
+            if s >= 2:
+                out_0_block(s % 2, (s - 2) // 2)("V" if s % 2 else "S")
             if s == 2:
                 q_x()
-            finish_row = whole_rows(9 + s, "V" if s >= BOTH_FROM else "S")
+            finish_row = whole_rows(8 + s, "V" if s >= BOTH_FROM else "S")
         finish_row("V")
+        out_0_block(0, 3)("V")
         out_0_block(1, 3)("S")
         for j in range(4):
             out_0_block(2, j)("V")

@@ -30,7 +30,7 @@ STAGE_BUFS = 9
 ROW_BUFS = 6
 PAIR_BUFS = 6
 SPLIT_FROM = 2
-BOTH_FROM = 4
+BOTH_FROM = 5
 VECTOR_EVERY = 3
 
 
@@ -42,8 +42,8 @@ def tile_mla_pa_v_kernel(
     grad_0_rows = grad_0.rearrange("b s h d -> (b s) (h d)").rearrange("(p j) w -> p j w", j=4)
     grad_1_rows = grad_1.rearrange("b s h d -> (b s) (h d)").rearrange("(p j) w -> p j w", j=4)
     c_lat_rows = c_lat.flatten_outer_dims().rearrange("(p j) w -> p (j w)", j=4)
-    mu_row = mu.flatten_outer_dims().rearrange("t o -> o t")
-    rstd_row = rstd.flatten_outer_dims().rearrange("t o -> o t")
+    mu_rows = mu.flatten_outer_dims().rearrange("(p j) o -> p (j o)", j=4)
+    rstd_rows = rstd.flatten_outer_dims().rearrange("(p j) o -> p (j o)", j=4)
     wkv_rows = wkv_a_w.rearrange("(n p j) w -> n p (j w)", p=128, j=4)
     out_0_rows = out_0.flatten_outer_dims().rearrange("(p j) w -> p j w", j=4)
     out_1_rows = out_1.rearrange("(m p) w -> p m w", p=128)
@@ -66,16 +66,14 @@ def tile_mla_pa_v_kernel(
         ones = kept("ones", [128, 128], BF16)
         nc.gpsimd.memset(ones[:], 1.0)
         gain_row = kept("gain_row", [128, RANK], BF16)
-        nc.vector.memset(gain_row[:], 0.0)
+        nc.gpsimd.memset(gain_row[:], 0.0)
         gain = kept("gain", [128, RANK], F32)
         cos_in = kept("cos_in", [128, 128], BF16)
         sin_in = kept("sin_in", [128, 128], BF16)
         cos_pairs = kept("cos_pairs", [128, 128, 2], BF16)
         sin_pairs = kept("sin_pairs", [128, 128, 2], BF16)
-        stat_rows = placed("stat_rows", [128, 512], F32, 44)
-        nc.vector.memset(stat_rows[:], 0.0)
-        stats = kept("stats", [128, 4, 2], F32)
-        mu_col, rstd_col = stats[:, :, 0], stats[:, :, 1]
+        mu_col = kept("mu_col", [128, 4], F32)
+        rstd_col = kept("rstd_col", [128, 4], F32)
         factors = kept("factors", [128, 4, 2], F32)
         sums = kept("sums", [128, 4, 2], F32)
         means = kept("means", [128, 4, 2], F32)
@@ -103,8 +101,6 @@ def tile_mla_pa_v_kernel(
         def copy(engine, out, in_):
             if engine == "V":
                 nc.vector.tensor_copy(out=out, in_=in_)
-            elif engine == "G":
-                nc.gpsimd.tensor_scalar(out=out, in0=in_, scalar1=1.0, scalar2=0.0, op0=MULT, op1=ADD)
             else:
                 nc.scalar.copy(out=out, in_=in_)
 
@@ -227,15 +223,9 @@ def tile_mla_pa_v_kernel(
             nc.tensor.matmul(bank[:], ones[:], gain_row[:], start=True, stop=True)
             copy("S", gain[:], bank[:])
 
-        def stat_columns():
-            bank = bank_tile("stats")
-            for j in range(4):
-                nc.tensor.transpose(bank[:, 128 * j : 128 * j + 128], stat_rows[:].rearrange("o (p j) -> o j p", j=4)[:, j, :], identity[:])
-            copy("S", stats[:], bank[:].rearrange("p (j o) -> p j o", j=4)[:, :, 0:2])
-
         def norm_factors():
             nc.vector.memset(factors[:, :, 0], 1.0 / RANK)
-            nc.vector.scalar_tensor_tensor(out=factors[:, :, 1], in0=rstd_col, scalar=1.0 / RANK, in1=rstd_col, op0=MULT, op1=MULT)
+            nc.vector.scalar_tensor_tensor(out=factors[:, :, 1], in0=rstd_col[:], scalar=1.0 / RANK, in1=rstd_col[:], op0=MULT, op1=MULT)
 
         def dh(j):
             bank = bank_tile("dh%d" % j)
@@ -354,8 +344,6 @@ def tile_mla_pa_v_kernel(
 
         load_dk(0)
         nc.sync.dma_start(out=gain_row[0:1, :], in_=kvn_g.rearrange("(o w) -> o w", o=1))
-        nc.sync.dma_start(out=stat_rows[0:1, :], in_=mu_row)
-        nc.sync.dma_start(out=stat_rows[1:2, :], in_=rstd_row)
         load_raw(0)
         load_raw(1)
         load_dk(1)
@@ -365,16 +353,15 @@ def tile_mla_pa_v_kernel(
         for i in range(5, 8):
             load_raw(i)
         load_dk(3)
+        nc.sync.dma_start(out=mu_col[:], in_=mu_rows)
+        nc.sync.dma_start(out=rstd_col[:], in_=rstd_rows)
         for i in range(8, 12):
             load_raw(i)
         load_x(0)
 
         tables()
         spread_gain()
-        stat_columns()
-        add_0 = rotate(0)
-        norm_factors()
-        add_0()
+        rotate(0)()
         w_run(0)
         q_w0 = w_run(1)
         q_z0 = z_run(0, 0)
@@ -409,33 +396,28 @@ def tile_mla_pa_v_kernel(
         q_a[0]()
         q_z3 = z_run(3, 0)
         q_f1 = f_run(1)
+        norm_factors()
         q_a[1]()
-        def lay_on_gpsimd(lay):
-            for part in range(4):
-                lay("G", 128 * part, 128 * part + 128)
-
         norm = [dh(0)]
         lay_z0, q_t0 = z_block(0)
         lay_z1, q_t1 = z_block(1)
-        lay_x, q_x0 = x_block(0)
-        lay_on_gpsimd(lay_x)
-        lay_x, q_x1 = x_block(1)
-        lay_on_gpsimd(lay_x)
+        lay_x0, q_x0 = x_block(0)
+        lay_x1, q_x1 = x_block(1)
         lay_z0("S", 0, 512)
         q_z2()
         q_a[2]()
-        lay_z1("V", 0, 256)
-        q_z3()
-        q_a[3]()
+        lay_x0("V", 0, 512)
         q_k = [k_run(0, 0)]
         norm.append(dh(1))
-        lay_z1("S", 256, 512)
+        lay_z1("S", 0, 512)
         norm[0][0]()
         q_t0()
-        q_f1()
+        q_z3()
         q_k.append(k_run(0, 1))
         norm.append(dh(2))
+        lay_x1("S", 0, 512)
         norm[0][1]()
+        q_a[3]()
         q_x0()
         norm[0][2]()
         norm[1][0]()
@@ -453,6 +435,7 @@ def tile_mla_pa_v_kernel(
         norm[2][2]()
         q_x1()
         norm[2][3]()
+        q_f1()
         stores += [rope_part(2, "SS"), rope_part(3, "SS")]
         q_k.append(k_run(0, 2))
         norm[3][0]()
@@ -465,8 +448,6 @@ def tile_mla_pa_v_kernel(
         load_wkv(3)
         rope_part(4, "SS")()
         norm[3][4]()
-        lay_x, q_x = x_block(2)
-        lay_on_gpsimd(lay_x)
         lay_z2, q_t2 = z_block(2)
         q_k[0]()
         lay_z2("V", 0, 512)
@@ -478,16 +459,17 @@ def tile_mla_pa_v_kernel(
         rope_part(7, "SV")()
         q_d = d_run("SS")
         q_k[2]()
-        q_x()
+        lay_x, q_x = x_block(2)
+        lay_x("V", 0, 512)
         latent_part(0, "SV")
         q_k[3]()
         latent_part(2, "SV")
         q_last = k_run(1, 1)
+        q_x()
         q_d()
         latent_part(4, "SV")
         latent_part(6, "SV")
         lay_x, q_x = x_block(3)
-        lay_on_gpsimd(lay_x)
         runs = [(1, 2)] + [(n, g) for n in (2, 3) for g in range(3)]
         finish_row = None
         for s in range(8):
@@ -501,6 +483,8 @@ def tile_mla_pa_v_kernel(
             q_last = q_next
             if s >= 2:
                 out_0_block(s % 2, (s - 2) // 2)("V" if s % 2 else "S")
+            if s < 2:
+                lay_x("V", 256 * s, 256 * s + 256)
             if s == 2:
                 q_x()
             finish_row = whole_rows(8 + s, "V" if s >= BOTH_FROM else "S")

@@ -26,12 +26,7 @@ BYTES = (
 )
 
 KIB = 1024
-STAGE_BUFS = 9
-ROW_BUFS = 6
-PAIR_BUFS = 6
-SPLIT_FROM = 2
-BOTH_FROM = 5
-VECTOR_EVERY = 3
+STAGE_BUFS = 10
 
 
 def tile_mla_pa_v_kernel(
@@ -39,11 +34,12 @@ def tile_mla_pa_v_kernel(
 ):
     nc = tc.nc
     x_rows = x.flatten_outer_dims().rearrange("(p j) w -> p j w", j=4)
-    grad_0_rows = grad_0.rearrange("b s h d -> (b s) (h d)").rearrange("(p j) w -> p j w", j=4)
-    grad_1_rows = grad_1.rearrange("b s h d -> (b s) (h d)").rearrange("(p j) w -> p j w", j=4)
+    grad_0_rows = grad_0.rearrange("b s h d -> (b s) (h d)").rearrange("(p j) w -> p (j w)", j=4)
+    grad_1_rows = grad_1.rearrange("b s h d -> (b s) (h d)").rearrange("(p j) w -> p (j w)", j=4)
     c_lat_rows = c_lat.flatten_outer_dims().rearrange("(p j) w -> p (j w)", j=4)
     mu_rows = mu.flatten_outer_dims().rearrange("(p j) o -> p (j o)", j=4)
     rstd_rows = rstd.flatten_outer_dims().rearrange("(p j) o -> p (j o)", j=4)
+    w2_rows = [w.rearrange("(p j) w -> p j w", j=4) for w in (wk_w, wv_w)]
     wkv_rows = wkv_a_w.rearrange("(n p j) w -> n p (j w)", p=128, j=4)
     out_0_rows = out_0.flatten_outer_dims().rearrange("(p j) w -> p j w", j=4)
     out_1_rows = out_1.rearrange("(m p) w -> p m w", p=128)
@@ -53,13 +49,13 @@ def tile_mla_pa_v_kernel(
     with ExitStack() as ctx:
         keep = ctx.enter_context(tc.tile_pool(name="keep", bufs=1))
         shared = ctx.enter_context(tc.tile_pool(name="shared", bufs=1))
-        psum = ctx.enter_context(tc.psum_pool(name="psum", bufs=8))
+        psum = ctx.enter_context(tc.psum_pool(name="psum", bufs=1))
 
         def kept(name, shape, dtype):
             return keep.tile(shape, dtype, name=name, align_bytes=64)
 
         def placed(name, shape, dtype, kib, bufs=1):
-            return shared.tile(shape, dtype, name=name, bufs=bufs, align_bytes=64, offset=kib * KIB)
+            return shared.tile(shape, dtype, name=name, bufs=bufs, align_bytes=64, offset=int(kib * KIB))
 
         identity = kept("identity", [128, 128], F32)
         make_identity(nc, identity[:])
@@ -77,23 +73,22 @@ def tile_mla_pa_v_kernel(
         factors = kept("factors", [128, 4, 2], F32)
         sums = kept("sums", [128, 4, 2], F32)
         means = kept("means", [128, 4, 2], F32)
-        x_in = [kept("x_in%d" % h, [128, 4, 1024], BF16) for h in range(2)]
-        dc = kept("dc", [128, 4 * RANK], BF16)
 
-        def operand(name, width, kib=None):
-            if kib is None:
-                return kept(name + "_codes", [128, width], U32), kept(name + "_scales", [128, width], U8)
-            return placed(name + "_codes", [128, width], U32, kib), placed(name + "_scales", [128, width], U8, kib + width // 256)
+        def operand(name, width, kib):
+            return placed(name + "_codes", [128, width], U32, kib), placed(name + "_scales", [128, width], U8, kib + width / 256)
 
-        wkv_mx = {}
-        token_mx = operand("dz1_token", WIDTH)
-        rope_mx = operand("rope", 4 * 2 * 128)
-        latent_mx = operand("latent", 4 * 128)
+        RAW, TEMP, C_AT, X_AT, STAGE = 64, 112, 128, 136, 180
         dk = placed("dk", [128, 4 * DK], BF16, 0)
         w2_mx = operand("w2", 8 * RANK, 24)
         dz2_mx = operand("dz2", 4 * 8 * 128, 44)
-        c_in = placed("c_in", [128, 4 * RANK], F32, 64)
-        RAW = 88
+        c_in = placed("c_in", [128, 4 * RANK], F32, C_AT)
+        x_in = [placed("x_in%d" % h, [128, 4, 1024], BF16, X_AT + 8 * h) for h in range(2)]
+        x_mx = [operand("x%d" % c, 512, 152 + 2.5 * c) for c in range(4)]
+        token_mx = operand("dz1_token", WIDTH, 162)
+        rope_mx = operand("rope", 4 * 2 * 128, 169.5)
+        dc = placed("dc", [128, 4 * RANK], BF16, 174.5)
+        wkv_mx = {}
+        late_mx = {}
 
         def cols(mx, start, width):
             return mx[0][:, start : start + width], mx[1][:, start : start + width]
@@ -104,11 +99,22 @@ def tile_mla_pa_v_kernel(
             else:
                 nc.scalar.copy(out=out, in_=in_)
 
-        def stage_tile(name):
-            return keep.tile([128, 1024], F32, name=name, tag="stage", bufs=STAGE_BUFS, align_bytes=64)
+        free_stages = [STAGE + 4 * i for i in range(STAGE_BUFS)]
+        count = []
 
-        def bank_tile(name):
-            return psum.tile([128, 512], F32, name=name, tag="bank")
+        def stage_tile():
+            kib = free_stages.pop(0)
+            count.append(kib)
+            return placed("stage%d" % len(count), [128, 1024], F32, kib), lambda: free_stages.append(kib)
+
+        ring = list(range(8))
+        held = []
+
+        def bank_tile(name, number=None):
+            if number is None:
+                number = ring.pop(0)
+                ring.append(number)
+            return psum.tile([128, 512], F32, name=name, tag="bank%d" % number)
 
         def quantize(mx, fmt, in_):
             nc.vector.quantize_mx(out=mx[0].bitcast(fmt), scales=mx[1], in_=in_.bitcast(BF16))
@@ -119,7 +125,11 @@ def tile_mla_pa_v_kernel(
         def words(rows, start):
             return rows.bitcast(F32)[:, start // 2 : start // 2 + 256].rearrange("p (w u) -> p u w", u=2)
 
-        def turn(name, blocks, places, engines="SS"):
+        later = []
+
+        def turn(name, blocks, fmt, engines="SS"):
+            stage, release = stage_tile()
+            halves = stage[:].rearrange("p (b a n u) -> p b a n u", b=2, a=2, u=2)
             banks = []
             for b in range(2):
                 bank = bank_tile(name)
@@ -127,25 +137,32 @@ def tile_mla_pa_v_kernel(
                 for a in range(2):
                     for u in range(2):
                         nc.tensor.transpose(banks[b][:, a, u, :], blocks[2 * b + a][:, u, :], identity[:])
-            for b in range(2):
-                copy(engines[b], places[b], banks[b].rearrange("p a u n -> p a n u"))
+            empty = [lambda engine, b=b: copy(engine, halves[:, b], banks[b].rearrange("p a u n -> p a n u")) for b in range(2)]
+            for b in range(len(engines)):
+                empty[b](engines[b])
+            later.extend(empty[len(engines) :])
 
-        def plain_run(name, blocks, mx, fmt, engines="SS"):
-            stage = stage_tile(name)
-            halves = stage[:].rearrange("p (b a n u) -> p b a n u", b=2, a=2, u=2)
-            turn(name, blocks, [halves[:, b] for b in range(2)], engines)
-            return lambda: quantize(mx, fmt, stage[:])
+            def finish(mx):
+                quantize(mx, fmt, stage[:])
+                release()
+
+            return finish
 
         raw = {}
 
-        def load_raw(i):
-            t = placed("raw%d" % i, [128, 2048], BF16, RAW + 4 * i)
-            raw[i] = t
-            if i < 8:
-                w = wv_w if i < 4 else wk_w
-                nc.sync.dma_start(out=t[:], in_=w[128 * (i % 4) : 128 * (i % 4) + 128, :])
-            else:
-                nc.sync.dma_start(out=t[:], in_=grad_1_rows[:, i - 8, :])
+        def load_w(s, h, first=0, width=2048):
+            t = placed("w%d%d%d" % (s, h, first), [128, 2 * width], BF16, RAW + 16 * (1 - s) + 8 * h + first / 256)
+            for a in range(first // 1024, (first + width) // 1024):
+                raw[(s, h, a)] = (t, width, 1024 * a - first)
+            nc.sync.dma_start(out=t[:].rearrange("p (i w) -> p i w", i=2), in_=w2_rows[s][:, 2 * h : 2 * h + 2, first : first + width])
+
+        grad_1_in = {}
+
+        def load_grad_1(j, count=1):
+            t = placed("grad_1_in%d" % j, [128, 2048 * count], BF16, RAW + 32 + 4 * j)
+            for i in range(count):
+                grad_1_in[j + i] = t[:, 2048 * i : 2048 * i + 2048]
+            nc.sync.dma_start(out=t[:], in_=grad_1_rows[:, 2048 * j : 2048 * (j + count)])
 
         wkv_in = {}
 
@@ -154,49 +171,55 @@ def tile_mla_pa_v_kernel(
             wkv_in[n] = t
             nc.sync.dma_start(out=t[:], in_=wkv_rows[n])
 
-        pair_stage = []
+        def load_dk(j, first=0, last=HEADS):
+            part = slice(DK * j + HEAD * first, DK * j + HEAD * last)
+            nc.sync.dma_start(out=dk[:, part], in_=grad_0_rows[:, part])
 
-        def w_run(i):
-            if i % 2 == 0:
-                pair_stage.clear()
-                pair_stage.extend([stage_tile("w%d" % i), stage_tile("w%d" % i)])
-            places = [t[:].rearrange("p (a i n u) -> p a i n u", a=2, i=2, u=2)[:, :, i % 2] for t in pair_stage]
-            turn("w%d" % i, [words(raw[i][:], 512 * g) for g in range(4)], places)
-            stages = list(pair_stage)
+        def load_x(h):
+            nc.sync.dma_start(out=x_in[h][:], in_=x_rows[:, :, 1024 * h : 1024 * h + 1024])
 
-            def finish():
-                first = 4 if i < 4 else 0
-                for g in range(4):
-                    quantize(cols(w2_mx, RANK * (first + g) + 128 * (i % 4 - 1), 256), E4M3, stages[g // 2][:, 512 * (g % 2) : 512 * (g % 2) + 512])
+        def w_run(s, h, a):
+            t, width, start = raw[(s, h, a)]
+            finish = turn("w", [words(t[:], width * i + start + 512 * b) for b in range(2) for i in range(2)], E4M3)
+            return lambda: finish(cols(w2_mx, 2048 * h + 256 * (4 * s + 2 * a), 512))
 
-            return finish
-
-        def z_run(j, h):
-            rows, start = (raw[8 + j][:], 0) if h else (dk[:], DK * j)
-            return plain_run("z%d%d" % (j, h), [words(rows, start + 512 * g) for g in range(4)], cols(dz2_mx, 1024 * j + 512 * h, 512), E5M2)
+        def z_run(j, s):
+            rows, start = (grad_1_in[j], 0) if s else (dk[:], DK * j)
+            finish = turn("z%d%d" % (j, s), [words(rows, start + 512 * g) for g in range(4)], E5M2)
+            return lambda: finish(cols(dz2_mx, 1024 * j + 512 * s, 512))
 
         def f_run(q):
-            return plain_run("f%d" % q, [words(dk[:], DK * (2 * q + i) + NOPE + 512 * g) for i in range(2) for g in range(2)], cols(rope_mx, 512 * q, 512), E5M2)
+            finish = turn("f", [words(dk[:], DK * (2 * q + i) + NOPE + 512 * g) for i in range(2) for g in range(2)], E5M2)
+            return lambda: finish(cols(rope_mx, 512 * q, 512))
 
         def d_run(engines):
-            return plain_run("d", [words(dc[:], RANK * j) for j in range(4)], latent_mx, E5M2, engines)
-
-        def k_run(n, g, engines="SS"):
-            if g == 0:
-                wkv_mx[n] = operand("wkv%d" % n, 3 * 512, (136, 144, 64, 72)[n])
-            if (n, g) in split:
-                blocks = [split[(n, g)][:, j] for j in range(4)]
-            else:
-                blocks = [words(wkv_in[n][:], WIDTH * j + 512 * g) for j in range(4)]
-            return plain_run("k%d%d" % (n, g), blocks, cols(wkv_mx[n], 512 * g, 512), E4M3, engines)
+            finish = turn("d", [words(dc[:], RANK * j) for j in range(4)], E5M2, engines)
+            late_mx["latent"] = operand("latent", 4 * 128, 54)
+            return lambda: finish(cols(late_mx["latent"], 0, 512))
 
         split = {}
 
+        def k_run(n, g, engines="SS"):
+            if (n, g) in split:
+                blocks = [split[(n, g)][0][:, j] for j in range(4)]
+            else:
+                blocks = [words(wkv_in[n][:], WIDTH * j + 512 * g) for j in range(4)]
+            finish = turn("k%d%d" % (n, g), blocks, E4M3, engines)
+            if (n, g) in split:
+                split[(n, g)][1]()
+
+            def done():
+                if n not in wkv_mx:
+                    wkv_mx[n] = operand("wkv%d" % n, 3 * 512, 24 + 7.5 * n)
+                finish(cols(wkv_mx[n], 512 * g, 512))
+
+            return done
+
         def k_split(n, g):
-            t = stage_tile("split")
-            split[(n, g)] = t[:].rearrange("p (j u w) -> p j u w", j=4, u=2)
+            t, release = stage_tile()
+            split[(n, g)] = t[:].rearrange("p (j u w) -> p j u w", j=4, u=2), release
             source = wkv_in[n][:].bitcast(F32).rearrange("p (j w) -> p j w", j=4)[:, :, 256 * g : 256 * g + 256]
-            nc.vector.tensor_copy(out=split[(n, g)], in_=source.rearrange("p j (w u) -> p j u w", u=2))
+            nc.vector.tensor_copy(out=split[(n, g)][0], in_=source.rearrange("p j (w u) -> p j u w", u=2))
 
         def tables():
             for e in range(2):
@@ -205,8 +228,7 @@ def tile_mla_pa_v_kernel(
             nc.vector.tensor_copy(out=sin_pairs[:, :, 1], in_=sin_in[:])
 
         def temp():
-            t = placed("temp", [128, 1024], F32, 72, bufs=4)
-            return t
+            return placed("temp", [128, 1024], F32, TEMP, bufs=4)
 
         def rotate(j, first=0, last=HEADS):
             pairs = dk[:, DK * j : DK * j + DK].rearrange("p (h w) -> p h w", w=HEAD)[:, first:last, 128:HEAD]
@@ -228,9 +250,10 @@ def tile_mla_pa_v_kernel(
             nc.vector.scalar_tensor_tensor(out=factors[:, :, 1], in0=rstd_col[:], scalar=1.0 / RANK, in1=rstd_col[:], op0=MULT, op1=MULT)
 
         def dh(j):
-            bank = bank_tile("dh%d" % j)
-            for g in range(8):
-                matmul_mx(bank[:], cols(dz2_mx, 1024 * j + 128 * g, 128), E5M2, cols(w2_mx, RANK * g, RANK), E4M3, g == 0, g == 7)
+            bank = bank_tile("dh%d" % j, held[j % 2])
+            for h in range(2):
+                for g in range(8):
+                    matmul_mx(bank[:, 256 * h : 256 * h + 256], cols(dz2_mx, 1024 * j + 128 * g, 128), E5M2, cols(w2_mx, 2048 * h + 256 * g, 256), E4M3, g == 0, g == 7)
             part = []
             c = c_in[:, RANK * j : RANK * j + RANK]
             one = slice(j, j + 1)
@@ -238,7 +261,15 @@ def tile_mla_pa_v_kernel(
             def first():
                 t = temp()
                 part.extend([t[:, 0:RANK], t[:, RANK : 2 * RANK]])
-                nc.vector.scalar_tensor_tensor(out=part[0], in0=bank[:], scalar=rstd_col[:, one], in1=gain[:], op0=MULT, op1=MULT, accum_out=sums[:, j, 0:1])
+                nc.vector.scalar_tensor_tensor(
+                    out=part[0].rearrange("p (q j) -> p q j", j=4),
+                    in0=bank[:].rearrange("p (j q) -> p q j", j=4),
+                    scalar=rstd_col[:, one],
+                    in1=gain[:].rearrange("p (q j) -> p q j", j=4),
+                    op0=MULT,
+                    op1=MULT,
+                    accum_out=sums[:, j, 0:1],
+                )
 
             def second():
                 nc.vector.scalar_tensor_tensor(out=part[1], in0=c, scalar=mu_col[:, one], in1=part[0], op0=SUB, op1=MULT, accum_out=sums[:, j, 1:2])
@@ -254,243 +285,289 @@ def tile_mla_pa_v_kernel(
 
             return [first, second, third, fourth, fifth]
 
-        def tokens_beside(source, mx, fmt, early):
-            stage = placed("beside", [128, 1024], F32, 136, bufs=4) if early else stage_tile("beside")
+        def tokens_beside(source, mx, fmt, engine):
+            stage, release = stage_tile()
+            copy(engine, stage[:].bitcast(BF16).rearrange("p (c i j) -> p c j i", i=4, j=4), source.rearrange("p j (c i) -> p c j i", i=4))
 
-            def lay(engine, first, last):
-                part = stage[:].bitcast(BF16)[:, 4 * first : 4 * last]
-                copy(engine, part.rearrange("p (c i j) -> p c j i", i=4, j=4), source[:, :, first:last].rearrange("p j (c i) -> p c j i", i=4))
+            def finish():
+                quantize(mx, fmt, stage[:])
+                release()
 
-            return lay, lambda: quantize(mx, fmt, stage[:])
+            return finish
 
-        x_mx = {}
+        def x_block(c, engine="V"):
+            return tokens_beside(x_in[c // 2][:, :, 512 * (c % 2) : 512 * (c % 2) + 512], cols(x_mx[c], 0, 512), E4M3, engine)
 
-        def x_block(c):
-            codes = keep.tile([128, 512], U32, name="x_codes", bufs=3, align_bytes=64)
-            scales = keep.tile([128, 512], U8, name="x_scales", bufs=3, align_bytes=64)
-            x_mx[c] = (codes, scales)
-            return tokens_beside(x_in[c // 2][:, :, 512 * (c % 2) : 512 * (c % 2) + 512], (codes[:], scales[:]), E4M3, c < 2)
-
-        def z_block(n):
+        def z_block(n, engine="V"):
             if n < 2:
                 source = dk[:].rearrange("p (j w) -> p j w", j=4)[:, :, NOPE + 512 * n : NOPE + 512 * n + 512]
             else:
                 source = dc[:].rearrange("p (j w) -> p j w", j=4)
-            return tokens_beside(source, cols(token_mx, 512 * n, 512), E5M2, n < 2)
+            return tokens_beside(source, cols(token_mx, 512 * n, 512), E5M2, engine)
+
+        free_places = []
+        made = []
+
+        def out_tile():
+            kib = free_places.pop(0)
+            free_places.append(kib)
+            made.append(kib)
+            return placed("out%d" % len(made), [128, 2048], F32, kib)
 
         def out_1_bank(m, n):
-            bank = bank_tile("al%d" % m)
+            bank = bank_tile("al%d%d" % (m, n))
             matmul_mx(bank[:], cols(x_mx[m // 4], 128 * (m % 4), 128), E4M3, cols(token_mx, 512 * n, 512), E5M2, True, True)
             return bank
 
-        def two_banks_tile():
-            return placed("pair", [128, 1024], F32, 0, bufs=PAIR_BUFS)
-
-        def rope_part(m, engines):
-            t = two_banks_tile()
-            for n in range(2):
-                copy(engines[n], t[:, 512 * n : 512 * n + 512], out_1_bank(m, n)[:])
-            return lambda: nc.sync.dma_start(out=out_1_rows[:, m, 0:ROPE], in_=t[:])
-
-        def latent_part(m, engines):
-            t = two_banks_tile()
-            for i in range(2):
-                copy(engines[i], t[:, 512 * i : 512 * i + 512], out_1_bank(m + i, 2)[:])
-            nc.sync.dma_start(out=out_1_rows[:, m : m + 2, ROPE:WIDTH], in_=t[:].rearrange("p (i w) -> p i w", i=2))
-
-        def whole_rows(m, second):
-            row = placed("row", [128, WIDTH], F32, 24, bufs=ROW_BUFS)
-            for n in range(3):
-                bank = out_1_bank(m, n)
-                if n < 2:
-                    copy(("S", second)[n], row[:, 512 * n : 512 * n + 512], bank[:])
-
-            def finish(engine):
-                copy(engine, row[:, ROPE:WIDTH], bank[:])
-                nc.sync.dma_start(out=out_1_rows[:, m, :], in_=row[:])
-
-            return finish
-
-        pair = {}
-
-        def out_0_block(n, j):
-            if n % 2 == 0:
-                pair[(n // 2, j)] = two_banks_tile()
+        def out_0_bank(n, j):
             bank = bank_tile("o%d%d" % (n, j))
             for g in range(3):
-                left = cols(rope_mx, 256 * j + 128 * g, 128) if g < 2 else cols(latent_mx, 128 * j, 128)
+                left = cols(rope_mx, 256 * j + 128 * g, 128) if g < 2 else cols(late_mx["latent"], 128 * j, 128)
                 matmul_mx(bank[:], left, E5M2, cols(wkv_mx[n], 512 * g, 512), E4M3, g == 0, g == 2)
-            side = pair[(n // 2, j)][:, 512 * (n % 2) : 512 * (n % 2) + 512]
+            return bank
 
-            def finish(engine):
-                copy(engine, side.rearrange("p (q j) -> p q j", j=4), bank[:].rearrange("p (j q) -> p q j", j=4))
-                if (n // 2, j) == (1, 3):
-                    nc.sync.dma_start(out=out_0_rows[:, j, 512 * n : 512 * n + 512], in_=side)
-                elif n % 2:
-                    nc.sync.dma_start(out=out_0_rows[:, j, 512 * (n - 1) : 512 * (n + 1)], in_=pair[(n // 2, j)][:])
+        def group(kind, a):
+            t = out_tile()
+            steps = []
+            if kind == "rope":
+                pieces = [(a + i, n) for i in range(2) for n in range(2)]
+                target = out_1_rows[:, a : a + 2, 0:ROPE]
+                source = t[:].rearrange("p (i w) -> p i w", i=2)
+            elif kind == "latent":
+                pieces = [(a + i, 2) for i in range(4)]
+                target = out_1_rows[:, a : a + 4, ROPE:WIDTH]
+                source = t[:].rearrange("p (i w) -> p i w", i=4)
+            else:
+                pieces = [(a, n) for n in range(3)]
+                target = out_1_rows[:, a, :]
+                source = t[:, 0:WIDTH]
 
-            return finish
+            def step(i):
+                def run(engine=None):
+                    bank = out_1_bank(*pieces[i])
+                    later.append(lambda e: copy(e, t[:, 512 * i : 512 * i + 512], bank[:]))
+                    if engine:
+                        later.pop()(engine)
+
+                return run
+
+            return [step(i) for i in range(len(pieces))], lambda: nc.sync.dma_start(out=target, in_=source)
+
+        def group_0(half, first, count, only=None):
+            t = out_tile()
+
+            def step(j, n):
+                def run(engine=None):
+                    side = t[:, 1024 * (j - first) + 512 * n : 1024 * (j - first) + 512 * n + 512]
+                    bank = out_0_bank(2 * half + n, j)
+                    later.append(lambda e: copy(e, side.rearrange("p (q j) -> p q j", j=4), bank[:].rearrange("p (j q) -> p q j", j=4)))
+                    if engine:
+                        later.pop()(engine)
+
+                return run
+
+            def store():
+                nc.sync.dma_start(out=out_0_rows[:, first : first + count, 1024 * half : 1024 * half + 1024], in_=t[:, 0 : 1024 * count].rearrange("p (j w) -> p j w", j=count))
+
+            if only is not None:
+                part = slice(512 * only, 512 * only + 512)
+                return [step(first, only)], lambda: nc.sync.dma_start(out=out_0_rows[:, first, 1024 * half : 1024 * half + 1024][:, part], in_=t[:, part])
+            return [step(j, n) for j in range(first, first + count) for n in range(2)], store
 
         ctx.enter_context(tc.manual_schedule())
+
+        halves = [(s, h, a) for s in (1, 0) for h in range(2) for a in range(2)]
+
+        def load_half(i):
+            load_w(halves[i][0], halves[i][1], 1024 * halves[i][2], 1024)
+
         for half in (slice(0, 64), slice(64, 128)):
             nc.sync.dma_start(out=cos_in[half], in_=cos_rows)
             nc.sync.dma_start(out=sin_in[half], in_=sin_rows)
-
-        def load_dk(j):
-            nc.sync.dma_start(out=dk[:, DK * j : DK * j + DK], in_=grad_0_rows[:, j, :])
-
-        def load_x(h):
-            nc.sync.dma_start(out=x_in[h][:], in_=x_rows[:, :, 1024 * h : 1024 * h + 1024])
-
-        load_dk(0)
+        load_dk(0, 0, 8)
+        load_dk(0, 8, 16)
+        load_half(0)
         nc.sync.dma_start(out=gain_row[0:1, :], in_=kvn_g.rearrange("(o w) -> o w", o=1))
-        load_raw(0)
-        load_raw(1)
-        load_dk(1)
-        for i in range(2, 5):
-            load_raw(i)
-        load_dk(2)
-        for i in range(5, 8):
-            load_raw(i)
-        load_dk(3)
-        nc.sync.dma_start(out=mu_col[:], in_=mu_rows)
-        nc.sync.dma_start(out=rstd_col[:], in_=rstd_rows)
-        for i in range(8, 12):
-            load_raw(i)
-        load_x(0)
+        for j in range(1, 4):
+            load_dk(j)
+            load_half(2 * j - 1)
+            load_half(2 * j)
+        load_grad_1(0)
+        load_half(7)
+        for j in range(1, 4):
+            load_grad_1(j)
 
         tables()
+        add_a = rotate(0, 0, 8)
+        add_b = rotate(0, 8, 16)
+        add_a()
+        add_b()
+        q_w = [w_run(*halves[0])]
+        q_nope = [z_run(0, 0)]
+        add = rotate(1)
+        q_w[0]()
+        add()
+        q_w.extend([w_run(*halves[i]) for i in (1, 2)])
         spread_gain()
-        rotate(0)()
-        w_run(0)
-        q_w0 = w_run(1)
-        q_z0 = z_run(0, 0)
-        add_1 = rotate(1)
-        q_w0()
-        add_1()
-        w_run(2)
-        q_w1 = w_run(3)
-        w_run(4)
-        q_z1 = z_run(1, 0)
+        q_nope.append(z_run(1, 0))
+        q_f = [f_run(0)]
+        add = rotate(2)
+        q_w[1]()
+        add()
+        q_w.extend([w_run(*halves[i]) for i in (3, 4)])
+        q_nope.append(z_run(2, 0))
         load_wkv(0)
-        nc.sync.dma_start(out=c_in[:], in_=c_lat_rows)
-        q_z0()
-        add_2 = rotate(2)
-        q_w1()
-        add_2()
-        q_w2 = w_run(5)
-        load_wkv(1)
+        nc.sync.dma_start(out=mu_col[:], in_=mu_rows)
+        nc.sync.dma_start(out=rstd_col[:], in_=rstd_rows)
+        load_x(0)
         load_x(1)
-        q_z1()
-        w_run(6)
-        q_w3 = w_run(7)
-        q_w2()
-        q_f0 = f_run(0)
-        q_z2 = z_run(2, 0)
-        add_3 = rotate(3)
-        q_f0()
-        add_3()
-        q_w3()
-        q_a = [z_run(j, 1) for j in range(4)]
+        nc.sync.dma_start(out=c_in[:], in_=c_lat_rows)
+        add = rotate(3)
+        q_w[2]()
+        add()
+        q_w.extend([w_run(*halves[i]) for i in (5, 6)])
+        q_w[3]()
+        q_w[4]()
+        q_v = [z_run(0, 1)]
+        q_nope[0]()
+        q_nope.append(z_run(3, 0))
+        q_w[5]()
+        q_w.append(w_run(*halves[7]))
+        load_wkv(1)
+        q_t = [z_block(0)]
+        q_w[6]()
+        q_f.append(f_run(1))
+        q_t[0]()
+        q_v.append(z_run(1, 1))
+        q_v[0]()
+        q_t.append(z_block(1))
+        q_w[7]()
+        q_v.append(z_run(2, 1))
+        q_t[1]()
+        q_nope[1]()
+        q_v.append(z_run(3, 1))
         load_wkv(2)
-        q_a[0]()
-        q_z3 = z_run(3, 0)
-        q_f1 = f_run(1)
+        load_wkv(3)
+        q_v[1]()
         norm_factors()
-        q_a[1]()
+
+        def banks(steps, engines):
+            for step, engine in zip(steps, engines):
+                step(engine)
+
+        def rope(i, engines="SSSS"):
+            steps, store = group("rope", 2 * i)
+            banks(steps, engines)
+            store()
+
+        def latent(i, engines):
+            steps, store = group("latent", 4 * i)
+            banks(steps, engines)
+            store()
+
+        def zero(half, j, engines):
+            steps, store = group_0(half, j, 1)
+            banks(steps, engines)
+            store()
+
+
+        q_k = {(0, 0): k_run(0, 0)}
+        q_nope[2]()
+        q_v[2]()
+        q_x = [x_block(0)]
+        held.extend([ring.pop(0), ring.pop(0)])
         norm = [dh(0)]
-        lay_z0, q_t0 = z_block(0)
-        lay_z1, q_t1 = z_block(1)
-        lay_x0, q_x0 = x_block(0)
-        lay_x1, q_x1 = x_block(1)
-        lay_z0("S", 0, 512)
-        q_z2()
-        q_a[2]()
-        lay_x0("V", 0, 512)
-        q_k = [k_run(0, 0)]
-        norm.append(dh(1))
-        lay_z1("S", 0, 512)
+        q_nope[3]()
+        q_x[0]()
+        q_x.append(x_block(1, "S"))
+        q_k[(0, 1)] = k_run(0, 1)
         norm[0][0]()
-        q_t0()
-        q_z3()
-        q_k.append(k_run(0, 1))
-        norm.append(dh(2))
-        lay_x1("S", 0, 512)
+        q_v[3]()
+        free_places.extend([0, 8, 16, 220])
+        rope(0)
+        norm.append(dh(1))
+        q_x.append(x_block(2, "V"))
         norm[0][1]()
-        q_a[3]()
-        q_x0()
+        q_x[1]()
         norm[0][2]()
-        norm[1][0]()
+        q_x.append(x_block(3, "S"))
+        q_x[2]()
         norm[0][3]()
-        q_t1()
-        norm[1][1]()
+        norm[1][0]()
         norm[0][4]()
+        norm[1][1]()
+        rope(1)
+        norm.append(dh(2))
+        q_x[3]()
         norm[1][2]()
-        stores = [rope_part(0, "SS"), rope_part(1, "SS")]
-        norm.append(dh(3))
-        norm[2][0]()
+        q_f[0]()
         norm[1][3]()
-        norm[2][1]()
+        norm[2][0]()
         norm[1][4]()
+        norm[2][1]()
+        rope(2)
+        norm.append(dh(3))
+        q_f[1]()
         norm[2][2]()
-        q_x1()
         norm[2][3]()
-        q_f1()
-        stores += [rope_part(2, "SS"), rope_part(3, "SS")]
-        q_k.append(k_run(0, 2))
         norm[3][0]()
         norm[2][4]()
         norm[3][1]()
+        ring.extend(held)
+        rope(3)
+        q_k[(0, 0)]()
         norm[3][2]()
+        q_k[(0, 1)]()
         norm[3][3]()
-        for store in stores:
-            store()
-        load_wkv(3)
-        rope_part(4, "SS")()
+        q_k[(0, 2)] = k_run(0, 2, "SV")
         norm[3][4]()
-        lay_z2, q_t2 = z_block(2)
-        q_k[0]()
-        lay_z2("V", 0, 512)
-        q_k[1]()
-        rope_part(5, "SS")()
-        q_k.append(k_run(1, 0))
+        free_places.insert(0, 64)
+        rope(4)
+        q_k[(1, 0)] = k_run(1, 0, "SV")
+        q_t2 = z_block(2)
+        q_k[(0, 2)]()
+        free_places.extend([112, 120, 128])
+        rope(5, "SSSV")
+        q_k[(1, 1)] = k_run(1, 1, "SV")
+        k_split(1, 2)
+        rope(6, "SSSS")
         q_t2()
-        rope_part(6, "SV")()
-        rope_part(7, "SV")()
-        q_d = d_run("SS")
-        q_k[2]()
-        lay_x, q_x = x_block(2)
-        lay_x("V", 0, 512)
-        latent_part(0, "SV")
-        q_k[3]()
-        latent_part(2, "SV")
-        q_last = k_run(1, 1)
-        q_x()
+        q_d = d_run("SV")
+        q_k[(1, 0)]()
+        k_split(2, 0)
+        rope(7, "SSSS")
+        q_k[(1, 2)] = k_run(1, 2, "VV")
+        q_k[(1, 1)]()
         q_d()
-        latent_part(4, "SV")
-        latent_part(6, "SV")
-        lay_x, q_x = x_block(3)
-        runs = [(1, 2)] + [(n, g) for n in (2, 3) for g in range(3)]
-        finish_row = None
-        for s in range(8):
-            if s < 7:
-                q_next = k_run(*runs[s])
-            if SPLIT_FROM <= s + 1 < 7:
-                k_split(*runs[s + 1])
-            if finish_row:
-                finish_row("V")
-            q_last()
-            q_last = q_next
-            if s >= 2:
-                out_0_block(s % 2, (s - 2) // 2)("V" if s % 2 else "S")
-            if s < 2:
-                lay_x("V", 256 * s, 256 * s + 256)
-            if s == 2:
-                q_x()
-            finish_row = whole_rows(8 + s, "V" if s >= BOTH_FROM else "S")
-        finish_row("V")
-        out_0_block(0, 3)("V")
-        out_0_block(1, 3)("S")
-        for j in range(4):
-            out_0_block(2, j)("V")
-            out_0_block(3, j)("S")
+        free_places.append(76)
+        latent(0, "SSSS")
+        q_k[(1, 2)]()
+        q_k[(2, 0)] = k_run(2, 0, "SV")
+        k_split(2, 1)
+        k_split(2, 2)
+        zero(0, 0, "SV")
+        latent(1, "SSSV")
+        q_k[(2, 1)] = k_run(2, 1, "SV")
+        q_k[(2, 2)] = k_run(2, 2, "SS")
+        k_split(3, 0)
+        k_split(3, 1)
+        zero(0, 1, "SV")
+        latent(2, "SSVV")
+        k_split(3, 2)
+        q_k[(3, 0)] = k_run(3, 0, "SS")
+        q_k[(3, 1)] = k_run(3, 1, "SS")
+        for g in range(3):
+            q_k[(2, g)]()
+        zero(0, 2, "SV")
+        q_k[(3, 2)] = k_run(3, 2, "SS")
+        q_k[(3, 0)]()
+        q_k[(3, 1)]()
+        latent(3, "SVSV")
+        q_k[(3, 2)]()
+        zero(0, 3, "SS")
+        for j in range(3):
+            zero(1, j, "VS")
+        for n in range(2):
+            steps, store = group_0(1, 3, 1, n)
+            steps[0]("VS"[n])
+            store()

@@ -33,16 +33,16 @@ def tile_mla_pa_v_kernel(
     tc, x, wkv_a_w, wkv_a_b, kvn_g, kvn_b, wk_w, wk_b, wv_w, wv_b, cos, sin, c_lat, mu, rstd, grad_0, grad_1, out_0, out_1
 ):
     nc = tc.nc
-    x_rows = x.flatten_outer_dims().rearrange("(p j) w -> p j w", j=4)
+    x_rows = x.flatten_outer_dims().rearrange("(p j) w -> p (j w)", j=4)
     grad_0_rows = grad_0.rearrange("b s h d -> (b s) (h d)").rearrange("(p j) w -> p (j w)", j=4)
     grad_1_rows = grad_1.rearrange("b s h d -> (b s) (h d)").rearrange("(p j) w -> p (j w)", j=4)
     c_lat_rows = c_lat.flatten_outer_dims().rearrange("(p j) w -> p (j w)", j=4)
     mu_rows = mu.flatten_outer_dims().rearrange("(p j) o -> p (j o)", j=4)
     rstd_rows = rstd.flatten_outer_dims().rearrange("(p j) o -> p (j o)", j=4)
-    w2_rows = [w.rearrange("(p j) w -> p j w", j=4) for w in (wk_w, wv_w)]
+    w2_rows = [w.rearrange("(p j) w -> p (j w)", j=4) for w in (wk_w, wv_w)]
     wkv_rows = wkv_a_w.rearrange("(n p j) w -> n p (j w)", p=128, j=4)
     out_0_rows = out_0.flatten_outer_dims().rearrange("(p j) w -> p j w", j=4)
-    out_1_rows = out_1.rearrange("(m p) w -> p m w", p=128)
+    out_1_rows = out_1.rearrange("(c p e) w -> p c e w", p=128, e=4)
     cos_rows = cos.rearrange("(q j) w -> q (j w)", j=4)
     sin_rows = sin.rearrange("(q j) w -> q (j w)", j=4)
 
@@ -82,7 +82,7 @@ def tile_mla_pa_v_kernel(
         w2_mx = operand("w2", 8 * RANK, 24)
         dz2_mx = operand("dz2", 4 * 8 * 128, 44)
         c_in = placed("c_in", [128, 4 * RANK], F32, C_AT)
-        x_in = [placed("x_in%d" % h, [128, 4, 1024], BF16, X_AT + 8 * h) for h in range(2)]
+        x_in = placed("x_in", [128, 4 * DIM], BF16, X_AT)
         x_mx = [operand("x%d" % c, 512, 152 + 2.5 * c) for c in range(4)]
         token_mx = operand("dz1_token", WIDTH, 162)
         rope_mx = operand("rope", 4 * 2 * 128, 169.5)
@@ -125,11 +125,7 @@ def tile_mla_pa_v_kernel(
         def words(rows, start):
             return rows.bitcast(F32)[:, start // 2 : start // 2 + 256].rearrange("p (w u) -> p u w", u=2)
 
-        later = []
-
-        def turn(name, blocks, fmt, engines="SS"):
-            stage, release = stage_tile()
-            halves = stage[:].rearrange("p (b a n u) -> p b a n u", b=2, a=2, u=2)
+        def transposes(name, blocks, places, engines):
             banks = []
             for b in range(2):
                 bank = bank_tile(name)
@@ -137,10 +133,13 @@ def tile_mla_pa_v_kernel(
                 for a in range(2):
                     for u in range(2):
                         nc.tensor.transpose(banks[b][:, a, u, :], blocks[2 * b + a][:, u, :], identity[:])
-            empty = [lambda engine, b=b: copy(engine, halves[:, b], banks[b].rearrange("p a u n -> p a n u")) for b in range(2)]
-            for b in range(len(engines)):
-                empty[b](engines[b])
-            later.extend(empty[len(engines) :])
+            for b in range(2):
+                copy(engines[b], places[b], banks[b].rearrange("p a u n -> p a n u"))
+
+        def turn(name, blocks, fmt, engines="SS"):
+            stage, release = stage_tile()
+            halves = stage[:].rearrange("p (b a n u) -> p b a n u", b=2, a=2, u=2)
+            transposes(name, blocks, [halves[:, b] for b in range(2)], engines)
 
             def finish(mx):
                 quantize(mx, fmt, stage[:])
@@ -150,11 +149,11 @@ def tile_mla_pa_v_kernel(
 
         raw = {}
 
-        def load_w(s, h, first=0, width=2048):
-            t = placed("w%d%d%d" % (s, h, first), [128, 2 * width], BF16, RAW + 16 * (1 - s) + 8 * h + first / 256)
-            for a in range(first // 1024, (first + width) // 1024):
-                raw[(s, h, a)] = (t, width, 1024 * a - first)
-            nc.sync.dma_start(out=t[:].rearrange("p (i w) -> p i w", i=2), in_=w2_rows[s][:, 2 * h : 2 * h + 2, first : first + width])
+        def load_w(s, j, count):
+            t = placed("w%d%d" % (s, j), [128, 2048 * count], BF16, RAW + 16 * (1 - s) + 4 * j)
+            for i in range(count):
+                raw[(s, j + i)] = t[:, 2048 * i : 2048 * i + 2048]
+            nc.sync.dma_start(out=t[:], in_=w2_rows[s][:, 2048 * j : 2048 * (j + count)])
 
         grad_1_in = {}
 
@@ -175,13 +174,24 @@ def tile_mla_pa_v_kernel(
             part = slice(DK * j + HEAD * first, DK * j + HEAD * last)
             nc.sync.dma_start(out=dk[:, part], in_=grad_0_rows[:, part])
 
-        def load_x(h):
-            nc.sync.dma_start(out=x_in[h][:], in_=x_rows[:, :, 1024 * h : 1024 * h + 1024])
+        def load_x():
+            nc.sync.dma_start(out=x_in[:], in_=x_rows)
 
-        def w_run(s, h, a):
-            t, width, start = raw[(s, h, a)]
-            finish = turn("w", [words(t[:], width * i + start + 512 * b) for b in range(2) for i in range(2)], E4M3)
-            return lambda: finish(cols(w2_mx, 2048 * h + 256 * (4 * s + 2 * a), 512))
+        pair = []
+
+        def w_run(s, j):
+            if j % 2 == 0:
+                pair.clear()
+                pair.extend([stage_tile(), stage_tile()])
+            stages = list(pair)
+            places = [t[:].rearrange("p (a i n u) -> p a i n u", a=2, i=2, u=2)[:, :, j % 2] for t, release in stages]
+            transposes("w", [words(raw[(s, j)], 512 * g) for g in range(4)], places, "SS")
+
+            def finish(b):
+                quantize(cols(w2_mx, 2048 * (j // 2) + 256 * (4 * s + 2 * b), 512), E4M3, stages[b][0][:])
+                stages[b][1]()
+
+            return [lambda b=b: finish(b) for b in range(2)]
 
         def z_run(j, s):
             rows, start = (grad_1_in[j], 0) if s else (dk[:], DK * j)
@@ -285,9 +295,9 @@ def tile_mla_pa_v_kernel(
 
             return [first, second, third, fourth, fifth]
 
-        def tokens_beside(source, mx, fmt, engine):
+        def tokens_beside(source, mx, fmt, engine, order):
             stage, release = stage_tile()
-            copy(engine, stage[:].bitcast(BF16).rearrange("p (c i j) -> p c j i", i=4, j=4), source.rearrange("p j (c i) -> p c j i", i=4))
+            copy(engine, stage[:].bitcast(BF16).rearrange(order[0], i=4, j=4), source.rearrange(order[1], i=4))
 
             def finish():
                 quantize(mx, fmt, stage[:])
@@ -296,14 +306,14 @@ def tile_mla_pa_v_kernel(
             return finish
 
         def x_block(c, engine="V"):
-            return tokens_beside(x_in[c // 2][:, :, 512 * (c % 2) : 512 * (c % 2) + 512], cols(x_mx[c], 0, 512), E4M3, engine)
+            return tokens_beside(x_in[:].rearrange("p (j w) -> p j w", j=4)[:, :, 512 * c : 512 * c + 512], cols(x_mx[c], 0, 512), E4M3, engine, ("p (i c j) -> p c i j", "p j (c i) -> p c i j"))
 
         def z_block(n, engine="V"):
             if n < 2:
                 source = dk[:].rearrange("p (j w) -> p j w", j=4)[:, :, NOPE + 512 * n : NOPE + 512 * n + 512]
             else:
                 source = dc[:].rearrange("p (j w) -> p j w", j=4)
-            return tokens_beside(source, cols(token_mx, 512 * n, 512), E5M2, engine)
+            return tokens_beside(source, cols(token_mx, 512 * n, 512), E5M2, engine, ("p (c i j) -> p c j i", "p j (c i) -> p c j i"))
 
         free_places = []
         made = []
@@ -326,43 +336,33 @@ def tile_mla_pa_v_kernel(
                 matmul_mx(bank[:], left, E5M2, cols(wkv_mx[n], 512 * g, 512), E4M3, g == 0, g == 2)
             return bank
 
-        def group(kind, a):
+        def group(kind, c, e):
             t = out_tile()
-            steps = []
             if kind == "rope":
-                pieces = [(a + i, n) for i in range(2) for n in range(2)]
-                target = out_1_rows[:, a : a + 2, 0:ROPE]
+                pieces = [(r, n) for r in e for n in range(2)]
+                target = out_1_rows[:, c, e[0] : e[1] + 1 : e[1] - e[0], 0:ROPE]
                 source = t[:].rearrange("p (i w) -> p i w", i=2)
             elif kind == "latent":
-                pieces = [(a + i, 2) for i in range(4)]
-                target = out_1_rows[:, a : a + 4, ROPE:WIDTH]
+                pieces = [(r, 2) for r in range(4)]
+                target = out_1_rows[:, c, :, ROPE:WIDTH]
                 source = t[:].rearrange("p (i w) -> p i w", i=4)
             else:
-                pieces = [(a, n) for n in range(3)]
-                target = out_1_rows[:, a, :]
-                source = t[:, 0:WIDTH]
+                pieces = [(e, 2), (e + 1, 0), (e + 1, 1), (e + 1, 2)]
+                target = out_1_rows[:, c].rearrange("p e w -> p (e w)")[:, WIDTH * e + ROPE : WIDTH * (e + 2)]
+                source = t[:]
 
             def step(i):
-                def run(engine=None):
-                    bank = out_1_bank(*pieces[i])
-                    later.append(lambda e: copy(e, t[:, 512 * i : 512 * i + 512], bank[:]))
-                    if engine:
-                        later.pop()(engine)
+                return lambda engine: copy(engine, t[:, 512 * i : 512 * i + 512], out_1_bank(4 * c + pieces[i][0], pieces[i][1])[:])
 
-                return run
-
-            return [step(i) for i in range(len(pieces))], lambda: nc.sync.dma_start(out=target, in_=source)
+            return [step(i) for i in range(4)], lambda: nc.sync.dma_start(out=target, in_=source)
 
         def group_0(half, first, count, only=None):
             t = out_tile()
 
             def step(j, n):
-                def run(engine=None):
+                def run(engine):
                     side = t[:, 1024 * (j - first) + 512 * n : 1024 * (j - first) + 512 * n + 512]
-                    bank = out_0_bank(2 * half + n, j)
-                    later.append(lambda e: copy(e, side.rearrange("p (q j) -> p q j", j=4), bank[:].rearrange("p (j q) -> p q j", j=4)))
-                    if engine:
-                        later.pop()(engine)
+                    copy(engine, side.rearrange("p (q j) -> p q j", j=4), out_0_bank(2 * half + n, j)[:].rearrange("p (j q) -> p q j", j=4))
 
                 return run
 
@@ -376,92 +376,82 @@ def tile_mla_pa_v_kernel(
 
         ctx.enter_context(tc.manual_schedule())
 
-        halves = [(s, h, a) for s in (1, 0) for h in range(2) for a in range(2)]
-
-        def load_half(i):
-            load_w(halves[i][0], halves[i][1], 1024 * halves[i][2], 1024)
-
         for half in (slice(0, 64), slice(64, 128)):
             nc.sync.dma_start(out=cos_in[half], in_=cos_rows)
             nc.sync.dma_start(out=sin_in[half], in_=sin_rows)
         load_dk(0, 0, 8)
         load_dk(0, 8, 16)
-        load_half(0)
+        load_w(1, 0, 1)
         nc.sync.dma_start(out=gain_row[0:1, :], in_=kvn_g.rearrange("(o w) -> o w", o=1))
-        for j in range(1, 4):
-            load_dk(j)
-            load_half(2 * j - 1)
-            load_half(2 * j)
-        load_grad_1(0)
-        load_half(7)
-        for j in range(1, 4):
-            load_grad_1(j)
+        load_dk(1)
+        load_w(1, 1, 1)
+        load_w(1, 2, 1)
+        load_dk(2)
+        load_w(1, 3, 1)
+        load_w(0, 0, 1)
+        load_dk(3)
+        load_w(0, 1, 1)
+        load_w(0, 2, 2)
+        load_grad_1(0, 2)
+        load_x()
 
         tables()
         add_a = rotate(0, 0, 8)
         add_b = rotate(0, 8, 16)
         add_a()
         add_b()
-        q_w = [w_run(*halves[0])]
+        w_run(1, 0)
         q_nope = [z_run(0, 0)]
         add = rotate(1)
-        q_w[0]()
+        q_nope[0]()
         add()
-        q_w.extend([w_run(*halves[i]) for i in (1, 2)])
+        q_w = w_run(1, 1)
+        w_run(1, 2)
         spread_gain()
         q_nope.append(z_run(1, 0))
         q_f = [f_run(0)]
         add = rotate(2)
-        q_w[1]()
+        q_w[0]()
         add()
-        q_w.extend([w_run(*halves[i]) for i in (3, 4)])
+        q_w.extend(w_run(1, 3))
+        w_run(0, 0)
+        q_w[1]()
         q_nope.append(z_run(2, 0))
-        load_wkv(0)
+        load_grad_1(2, 2)
         nc.sync.dma_start(out=mu_col[:], in_=mu_rows)
         nc.sync.dma_start(out=rstd_col[:], in_=rstd_rows)
-        load_x(0)
-        load_x(1)
+        load_wkv(0)
         nc.sync.dma_start(out=c_in[:], in_=c_lat_rows)
         add = rotate(3)
         q_w[2]()
         add()
-        q_w.extend([w_run(*halves[i]) for i in (5, 6)])
+        q_w.extend(w_run(0, 1))
         q_w[3]()
         q_w[4]()
-        q_v = [z_run(0, 1)]
-        q_nope[0]()
-        q_nope.append(z_run(3, 0))
+        w_run(0, 2)
         q_w[5]()
-        q_w.append(w_run(*halves[7]))
-        load_wkv(1)
+        q_w.extend(w_run(0, 3))
         q_t = [z_block(0)]
-        q_w[6]()
-        q_f.append(f_run(1))
-        q_t[0]()
-        q_v.append(z_run(1, 1))
-        q_v[0]()
-        q_t.append(z_block(1))
-        q_w[7]()
-        q_v.append(z_run(2, 1))
-        q_t[1]()
+        q_v = [z_run(0, 1)]
         q_nope[1]()
-        q_v.append(z_run(3, 1))
-        load_wkv(2)
-        load_wkv(3)
+        q_nope.append(z_run(3, 0))
+        q_t[0]()
+        load_wkv(1)
+        q_w[6]()
+        q_v.append(z_run(1, 1))
+        q_w[7]()
+        q_v[0]()
+        q_f.append(f_run(1))
+        q_t.append(z_block(1))
         q_v[1]()
-        norm_factors()
+        q_t[1]()
 
         def banks(steps, engines):
             for step, engine in zip(steps, engines):
                 step(engine)
 
-        def rope(i, engines="SSSS"):
-            steps, store = group("rope", 2 * i)
-            banks(steps, engines)
-            store()
-
-        def latent(i, engines):
-            steps, store = group("latent", 4 * i)
+        def part(kind, c, e, engines="SSSS"):
+            steps, store = group(kind, c, e)
             banks(steps, engines)
             store()
 
@@ -470,99 +460,109 @@ def tile_mla_pa_v_kernel(
             banks(steps, engines)
             store()
 
-
-        q_k = {(0, 0): k_run(0, 0)}
-        q_nope[2]()
-        q_v[2]()
-        q_x = [x_block(0)]
         held.extend([ring.pop(0), ring.pop(0)])
         norm = [dh(0)]
-        q_nope[3]()
-        q_x[0]()
-        q_x.append(x_block(1, "S"))
-        q_k[(0, 1)] = k_run(0, 1)
-        norm[0][0]()
-        q_v[3]()
-        free_places.extend([0, 8, 16, 220])
-        rope(0)
+        q_x = [x_block(0), x_block(1, "S"), x_block(3, "S")]
+        q_v.append(z_run(2, 1))
         norm.append(dh(1))
-        q_x.append(x_block(2, "V"))
-        norm[0][1]()
+        norm_factors()
+        q_nope[2]()
+        q_x[0]()
+        norm[0][0]()
+        q_v.append(z_run(3, 1))
+        load_wkv(2)
+        load_wkv(3)
         q_x[1]()
-        norm[0][2]()
-        q_x.append(x_block(3, "S"))
-        q_x[2]()
-        norm[0][3]()
+        q_x.insert(2, x_block(2, "V"))
         norm[1][0]()
-        norm[0][4]()
-        norm[1][1]()
-        rope(1)
-        norm.append(dh(2))
+        q_nope[3]()
+        q_x[2]()
+        free_places.extend([0, 8, 16, 220])
+        part("rope", 0, (0, 1))
+        q_k = {(0, 0): k_run(0, 0)}
+        q_v[2]()
+        norm[0][1]()
         q_x[3]()
+        norm[1][1]()
+        norm[0][2]()
+        norm.append(dh(2))
+        q_v[3]()
         norm[1][2]()
-        q_f[0]()
+        norm[0][3]()
         norm[1][3]()
+        norm[0][4]()
+        part("rope", 0, (2, 3))
         norm[2][0]()
+        norm.append(dh(3))
         norm[1][4]()
         norm[2][1]()
-        rope(2)
-        norm.append(dh(3))
-        q_f[1]()
+        q_f[0]()
         norm[2][2]()
-        norm[2][3]()
+        part("rope", 1, (0, 2))
         norm[3][0]()
-        norm[2][4]()
+        norm[2][3]()
         norm[3][1]()
-        ring.extend(held)
-        rope(3)
-        q_k[(0, 0)]()
+        norm[2][4]()
         norm[3][2]()
-        q_k[(0, 1)]()
+        ring.extend(held)
+        q_k[(0, 1)] = k_run(0, 1, "SS")
+        q_f[1]()
         norm[3][3]()
-        q_k[(0, 2)] = k_run(0, 2, "SV")
+        q_k[(0, 0)]()
         norm[3][4]()
-        free_places.insert(0, 64)
-        rope(4)
-        q_k[(1, 0)] = k_run(1, 0, "SV")
+        part("rope", 2, (0, 2))
+        for kib in (128, 120, 112):
+            free_places.insert(0, kib)
+        q_k[(0, 1)]()
         q_t2 = z_block(2)
-        q_k[(0, 2)]()
-        free_places.extend([112, 120, 128])
-        rope(5, "SSSV")
-        q_k[(1, 1)] = k_run(1, 1, "SV")
-        k_split(1, 2)
-        rope(6, "SSSS")
+        q_k[(0, 2)] = k_run(0, 2, "SV")
+        free_places.insert(0, 64)
         q_t2()
+        part("rope", 3, (0, 2), "SSSV")
+        q_k[(1, 0)] = k_run(1, 0, "SV")
+        latent_steps, latent_store = group("latent", 0, None)
+        rest = [group("rest", 1, e) for e in (0, 2)]
+        for steps, store in rest:
+            banks(steps[1:3], "SS")
+        k_split(1, 1)
         q_d = d_run("SV")
-        q_k[(1, 0)]()
-        k_split(2, 0)
-        rope(7, "SSSS")
-        q_k[(1, 2)] = k_run(1, 2, "VV")
-        q_k[(1, 1)]()
+        k_split(1, 2)
+        banks(latent_steps, "VSVS")
+        latent_store()
+        for steps, store in rest:
+            banks(steps[0:4:3], "VS")
+            store()
+        q_k[(0, 2)]()
         q_d()
-        free_places.append(76)
-        latent(0, "SSSS")
+        k_split(2, 0)
+        q_k[(1, 1)] = k_run(1, 1, "SV")
+        q_k[(1, 2)] = k_run(1, 2, "SV")
+        q_k[(1, 0)]()
+        free_places.insert(0, 76)
+        part("rest", 2, 0, "SSSS")
+        q_k[(1, 1)]()
         q_k[(1, 2)]()
         q_k[(2, 0)] = k_run(2, 0, "SV")
         k_split(2, 1)
         k_split(2, 2)
         zero(0, 0, "SV")
-        latent(1, "SSSV")
+        part("rest", 2, 2, "SSSV")
         q_k[(2, 1)] = k_run(2, 1, "SV")
         q_k[(2, 2)] = k_run(2, 2, "SS")
         k_split(3, 0)
         k_split(3, 1)
         zero(0, 1, "SV")
-        latent(2, "SSVV")
+        part("rest", 3, 0, "SSVV")
         k_split(3, 2)
-        q_k[(3, 0)] = k_run(3, 0, "SS")
-        q_k[(3, 1)] = k_run(3, 1, "SS")
+        q_k[(3, 0)] = k_run(3, 0, "SV")
+        q_k[(3, 1)] = k_run(3, 1, "SV")
         for g in range(3):
             q_k[(2, g)]()
-        zero(0, 2, "SV")
+        zero(0, 2, "SS")
         q_k[(3, 2)] = k_run(3, 2, "SS")
         q_k[(3, 0)]()
         q_k[(3, 1)]()
-        latent(3, "SVSV")
+        part("rest", 3, 2, "SVSV")
         q_k[(3, 2)]()
         zero(0, 3, "SS")
         for j in range(3):

@@ -391,9 +391,10 @@ def tile_mla_pa_v_kernel(
         load_w(0, 0, 1)
         load_dk(3)
         load_w(0, 1, 1)
-        load_w(0, 2, 2)
+        load_w(0, 2, 1)
+        load_w(0, 3, 1)
         load_grad_1(0, 2)
-        load_x()
+        load_grad_1(2, 2)
 
         tables()
         add_a = rotate(0, 0, 8)
@@ -402,12 +403,12 @@ def tile_mla_pa_v_kernel(
         add_b()
         w_run(1, 0)
         q_nope = [z_run(0, 0)]
+        spread_gain()
         add = rotate(1)
         q_nope[0]()
         add()
         q_w = w_run(1, 1)
         w_run(1, 2)
-        spread_gain()
         q_nope.append(z_run(1, 0))
         q_f = [f_run(0)]
         add = rotate(2)
@@ -417,11 +418,11 @@ def tile_mla_pa_v_kernel(
         w_run(0, 0)
         q_w[1]()
         q_nope.append(z_run(2, 0))
-        load_grad_1(2, 2)
+        load_x()
         nc.sync.dma_start(out=mu_col[:], in_=mu_rows)
         nc.sync.dma_start(out=rstd_col[:], in_=rstd_rows)
-        load_wkv(0)
         nc.sync.dma_start(out=c_in[:], in_=c_lat_rows)
+        load_wkv(0)
         add = rotate(3)
         q_w[2]()
         add()
@@ -432,19 +433,25 @@ def tile_mla_pa_v_kernel(
         q_w[5]()
         q_w.extend(w_run(0, 3))
         q_t = [z_block(0)]
-        q_v = [z_run(0, 1)]
-        q_nope[1]()
         q_nope.append(z_run(3, 0))
+        q_nope[1]()
+        q_v = [z_run(0, 1)]
         q_t[0]()
         load_wkv(1)
         q_w[6]()
         q_v.append(z_run(1, 1))
         q_w[7]()
+        q_v.append(z_run(2, 1))
         q_v[0]()
+        q_v.append(z_run(3, 1))
+        load_wkv(2)
+        load_wkv(3)
+        q_v[1]()
         q_f.append(f_run(1))
         q_t.append(z_block(1))
-        q_v[1]()
+        q_x = [x_block(0), x_block(1, "S"), x_block(2, "S")]
         q_t[1]()
+        q_x[0]()
 
         def banks(steps, engines):
             for step, engine in zip(steps, engines):
@@ -461,113 +468,87 @@ def tile_mla_pa_v_kernel(
             store()
 
         held.extend([ring.pop(0), ring.pop(0)])
-        norm = [dh(0)]
-        q_x = [x_block(0), x_block(1, "S"), x_block(3, "S")]
-        q_v.append(z_run(2, 1))
-        norm.append(dh(1))
+        norm = [dh(0), dh(1)]
         norm_factors()
-        q_nope[2]()
-        q_x[0]()
         norm[0][0]()
-        q_v.append(z_run(3, 1))
-        load_wkv(2)
-        load_wkv(3)
-        q_x[1]()
-        q_x.insert(2, x_block(2, "V"))
-        norm[1][0]()
-        q_nope[3]()
-        q_x[2]()
-        free_places.extend([0, 8, 16, 220])
-        part("rope", 0, (0, 1))
-        q_k = {(0, 0): k_run(0, 0)}
-        q_v[2]()
+        q_nope[2]()
         norm[0][1]()
-        q_x[3]()
-        norm[1][1]()
-        norm[0][2]()
+        q_v[2]()
+        free_places.extend([0, 8, 16, 220])
+        part("rope", 0, (0, 2))
+        q_x.append(x_block(3, "S"))
         norm.append(dh(2))
+        norm[1][0]()
+        q_x[1]()
+        norm[1][1]()
+        q_nope[3]()
+        norm[0][2]()
         q_v[3]()
+        part("rope", 1, (0, 2))
+        norm.append(dh(3))
         norm[1][2]()
         norm[0][3]()
-        norm[1][3]()
-        norm[0][4]()
-        part("rope", 0, (2, 3))
         norm[2][0]()
-        norm.append(dh(3))
-        norm[1][4]()
+        norm[0][4]()
         norm[2][1]()
-        q_f[0]()
+        norm[1][3]()
+        q_x[2]()
         norm[2][2]()
-        part("rope", 1, (0, 2))
+        q_k = {(0, 0): k_run(0, 0)}
+        norm[1][4]()
         norm[3][0]()
+        part("rope", 2, (0, 2))
         norm[2][3]()
         norm[3][1]()
-        norm[2][4]()
+        q_x[3]()
         norm[3][2]()
         ring.extend(held)
-        q_k[(0, 1)] = k_run(0, 1, "SS")
-        q_f[1]()
+        q_k[(0, 1)] = k_run(0, 1)
+        norm[2][4]()
         norm[3][3]()
-        q_k[(0, 0)]()
+        q_f[0]()
         norm[3][4]()
-        part("rope", 2, (0, 2))
-        for kib in (128, 120, 112):
-            free_places.insert(0, kib)
-        q_k[(0, 1)]()
+        q_f[1]()
         q_t2 = z_block(2)
-        q_k[(0, 2)] = k_run(0, 2, "SV")
-        free_places.insert(0, 64)
+        part("rope", 3, (0, 2), "SSSS")
+        q_k[(0, 2)] = k_run(0, 2, "SS")
+        for kib in (128, 120, 112, 64):
+            free_places.insert(0, kib)
+        rest = [group("rest", 0, e) for e in (0, 2)]
+        q_k[(0, 0)]()
         q_t2()
-        part("rope", 3, (0, 2), "SSSV")
-        q_k[(1, 0)] = k_run(1, 0, "SV")
-        latent_steps, latent_store = group("latent", 0, None)
-        rest = [group("rest", 1, e) for e in (0, 2)]
         for steps, store in rest:
-            banks(steps[1:3], "SS")
-        k_split(1, 1)
-        q_d = d_run("SV")
-        k_split(1, 2)
-        banks(latent_steps, "VSVS")
-        latent_store()
+            banks(steps[1:3], "VS")
+        q_k[(1, 0)] = k_run(1, 0, "VS")
         for steps, store in rest:
             banks(steps[0:4:3], "VS")
             store()
-        q_k[(0, 2)]()
-        q_d()
-        k_split(2, 0)
-        q_k[(1, 1)] = k_run(1, 1, "SV")
-        q_k[(1, 2)] = k_run(1, 2, "SV")
-        q_k[(1, 0)]()
-        free_places.insert(0, 76)
-        part("rest", 2, 0, "SSSS")
-        q_k[(1, 1)]()
-        q_k[(1, 2)]()
-        q_k[(2, 0)] = k_run(2, 0, "SV")
-        k_split(2, 1)
-        k_split(2, 2)
+        waiting = [q_k[(0, 1)], q_k[(0, 2)], q_k[(1, 0)]]
+        later = [(1, 1), None, (1, 2), (2, 0), (2, 1)]
+        ahead = [[], [], [(2, 0)], [(2, 1)], [(2, 2), (3, 0)], [(3, 1), (3, 2)]]
+        for beat in range(6):
+            c, e = divmod(beat + 2, 2)
+            for run in ahead[beat]:
+                k_split(*run)
+            waiting.pop(0)()
+            part("rest", c, 2 * e, "SVSV")
+            if beat == 3:
+                free_places.insert(0, 76)
+            if beat < 5:
+                waiting.append(k_run(*later[beat]) if later[beat] else d_run("SS"))
+        waiting.extend([k_run(2, 2), k_run(3, 0, "SV")])
         zero(0, 0, "SV")
-        part("rest", 2, 2, "SSSV")
-        q_k[(2, 1)] = k_run(2, 1, "SV")
-        q_k[(2, 2)] = k_run(2, 2, "SS")
-        k_split(3, 0)
-        k_split(3, 1)
-        zero(0, 1, "SV")
-        part("rest", 3, 0, "SSVV")
-        k_split(3, 2)
-        q_k[(3, 0)] = k_run(3, 0, "SV")
-        q_k[(3, 1)] = k_run(3, 1, "SV")
-        for g in range(3):
-            q_k[(2, g)]()
-        zero(0, 2, "SS")
-        q_k[(3, 2)] = k_run(3, 2, "SS")
-        q_k[(3, 0)]()
-        q_k[(3, 1)]()
-        part("rest", 3, 2, "SVSV")
-        q_k[(3, 2)]()
-        zero(0, 3, "SS")
+        waiting.pop(0)()
+        waiting.pop(0)()
+        waiting.extend([k_run(3, 1, "SV"), k_run(3, 2, "SV")])
+        for j in (1, 2):
+            waiting.pop(0)()
+            waiting.pop(0)()
+            zero(0, j, "SS")
+        zero(0, 3, "SV")
         for j in range(3):
-            zero(1, j, "VS")
+            zero(1, j, "SV")
         for n in range(2):
             steps, store = group_0(1, 3, 1, n)
-            steps[0]("VS"[n])
+            steps[0]("SV"[n])
             store()

@@ -127,6 +127,7 @@ def tile_mla_pa_v_kernel(
 
         def transposes(name, blocks, places, engines):
             banks = []
+            ring[0], ring[1] = ring[1], ring[0]
             for b in range(2):
                 bank = bank_tile(name)
                 banks.append(bank[:].rearrange("p (a u n) -> p a u n", a=2, u=2))

@@ -42,7 +42,7 @@ def tile_mla_pa_v_kernel(
     w2_rows = [w.rearrange("(p j) w -> p (j w)", j=4) for w in (wk_w, wv_w)]
     wkv_rows = wkv_a_w.rearrange("(n p j) w -> n p (j w)", p=128, j=4)
     out_0_rows = out_0.flatten_outer_dims().rearrange("(p j) w -> p j w", j=4)
-    out_1_rows = out_1.rearrange("(c p e) w -> p c e w", p=128, e=4)
+    out_1_rows = out_1.rearrange("(c i p e) w -> p c i e w", i=2, p=128, e=2)
     cos_rows = cos.rearrange("(q j) w -> q (j w)", j=4)
     sin_rows = sin.rearrange("(q j) w -> q (j w)", j=4)
 
@@ -298,7 +298,7 @@ def tile_mla_pa_v_kernel(
 
         def tokens_beside(source, mx, fmt, engine, order):
             stage, release = stage_tile()
-            copy(engine, stage[:].bitcast(BF16).rearrange(order[0], i=4, j=4), source.rearrange(order[1], i=4))
+            copy(engine, stage[:].bitcast(BF16).rearrange(order, r=2, e=2, j=4), source.rearrange("p j (c r e) -> p c j r e", r=2, e=2))
 
             def finish():
                 quantize(mx, fmt, stage[:])
@@ -307,14 +307,14 @@ def tile_mla_pa_v_kernel(
             return finish
 
         def x_block(c, engine="V"):
-            return tokens_beside(x_in[:].rearrange("p (j w) -> p j w", j=4)[:, :, 512 * c : 512 * c + 512], cols(x_mx[c], 0, 512), E4M3, engine, ("p (i c j) -> p c i j", "p j (c i) -> p c i j"))
+            return tokens_beside(x_in[:].rearrange("p (j w) -> p j w", j=4)[:, :, 512 * c : 512 * c + 512], cols(x_mx[c], 0, 512), E4M3, engine, "p (e c r j) -> p c j r e")
 
         def z_block(n, engine="V"):
             if n < 2:
                 source = dk[:].rearrange("p (j w) -> p j w", j=4)[:, :, NOPE + 512 * n : NOPE + 512 * n + 512]
             else:
                 source = dc[:].rearrange("p (j w) -> p j w", j=4)
-            return tokens_beside(source, cols(token_mx, 512 * n, 512), E5M2, engine, ("p (c i j) -> p c j i", "p j (c i) -> p c j i"))
+            return tokens_beside(source, cols(token_mx, 512 * n, 512), E5M2, engine, "p (c r e j) -> p c j r e")
 
         free_places = []
         made = []
@@ -337,19 +337,15 @@ def tile_mla_pa_v_kernel(
                 matmul_mx(bank[:], left, E5M2, cols(wkv_mx[n], 512 * g, 512), E4M3, g == 0, g == 2)
             return bank
 
-        def group(kind, c, e):
+        def group(kind, c, i):
             t = out_tile()
             if kind == "rope":
-                pieces = [(r, n) for r in e for n in range(2)]
-                target = out_1_rows[:, c, e[0] : e[1] + 1 : e[1] - e[0], 0:ROPE]
+                pieces = [(r, n) for r in range(2) for n in range(2)]
+                target = out_1_rows[:, c, :, 0, 0:ROPE]
                 source = t[:].rearrange("p (i w) -> p i w", i=2)
-            elif kind == "latent":
-                pieces = [(r, 2) for r in range(4)]
-                target = out_1_rows[:, c, :, ROPE:WIDTH]
-                source = t[:].rearrange("p (i w) -> p i w", i=4)
             else:
-                pieces = [(e, 2), (e + 1, 0), (e + 1, 1), (e + 1, 2)]
-                target = out_1_rows[:, c].rearrange("p e w -> p (e w)")[:, WIDTH * e + ROPE : WIDTH * (e + 2)]
+                pieces = [(i, 2), (2 + i, 0), (2 + i, 1), (2 + i, 2)]
+                target = out_1_rows[:, c, i].rearrange("p e w -> p (e w)")[:, ROPE : 2 * WIDTH]
                 source = t[:]
 
             def step(i):
@@ -476,7 +472,7 @@ def tile_mla_pa_v_kernel(
         norm[0][1]()
         q_v[2]()
         free_places.extend([0, 8, 16, 220])
-        part("rope", 0, (0, 2))
+        part("rope", 0, None)
         q_x.append(x_block(3, "S"))
         norm.append(dh(2))
         norm[1][0]()
@@ -485,7 +481,7 @@ def tile_mla_pa_v_kernel(
         q_nope[3]()
         norm[0][2]()
         q_v[3]()
-        part("rope", 1, (0, 2))
+        part("rope", 1, None)
         norm.append(dh(3))
         norm[1][2]()
         norm[0][3]()
@@ -498,7 +494,7 @@ def tile_mla_pa_v_kernel(
         q_k = {(0, 0): k_run(0, 0)}
         norm[1][4]()
         norm[3][0]()
-        part("rope", 2, (0, 2))
+        part("rope", 2, None)
         norm[2][3]()
         norm[3][1]()
         q_x[3]()
@@ -511,11 +507,11 @@ def tile_mla_pa_v_kernel(
         norm[3][4]()
         q_f[1]()
         q_t2 = z_block(2)
-        part("rope", 3, (0, 2), "SSSS")
+        part("rope", 3, None, "SSSS")
         q_k[(0, 2)] = k_run(0, 2, "SS")
         for kib in (128, 120, 112, 64):
             free_places.insert(0, kib)
-        rest = [group("rest", 0, e) for e in (0, 2)]
+        rest = [group("rest", 0, e) for e in range(2)]
         q_k[(0, 0)]()
         q_t2()
         for steps, store in rest:
@@ -532,7 +528,7 @@ def tile_mla_pa_v_kernel(
             for run in ahead[beat]:
                 k_split(*run)
             waiting.pop(0)()
-            part("rest", c, 2 * e, "SVSV")
+            part("rest", c, e, "SVSV")
             if beat == 3:
                 free_places.insert(0, 76)
             if beat < 5:

@@ -189,7 +189,8 @@ def tile_mla_pa_v_kernel(
             transposes("w", [words(raw[(s, j)], 512 * g) for g in range(4)], places, "SS")
 
             def finish(b):
-                quantize(cols(w2_mx, 2048 * (j // 2) + 256 * (4 * s + 2 * b), 512), E4M3, stages[b][0][:])
+                for a in range(2):
+                    quantize(cols(w2_mx, 512 * (4 * s + 2 * b + a) + 256 * (j // 2), 256), E4M3, stages[b][0][:, 512 * a : 512 * a + 512])
                 stages[b][1]()
 
             return [lambda b=b: finish(b) for b in range(2)]
@@ -262,9 +263,8 @@ def tile_mla_pa_v_kernel(
 
         def dh(j):
             bank = bank_tile("dh%d" % j, held[j % 2])
-            for h in range(2):
-                for g in range(8):
-                    matmul_mx(bank[:, 256 * h : 256 * h + 256], cols(dz2_mx, 1024 * j + 128 * g, 128), E5M2, cols(w2_mx, 2048 * h + 256 * g, 256), E4M3, g == 0, g == 7)
+            for g in range(8):
+                matmul_mx(bank[:], cols(dz2_mx, 1024 * j + 128 * g, 128), E5M2, cols(w2_mx, 512 * g, 512), E4M3, g == 0, g == 7)
             part = []
             c = c_in[:, RANK * j : RANK * j + RANK]
             one = slice(j, j + 1)

@@ -522,7 +522,7 @@ def tile_mla_pa_v_kernel(
             store()
         waiting = [q_k[(0, 1)], q_k[(0, 2)], q_k[(1, 0)]]
         later = [(1, 1), None, (1, 2), (2, 0), (2, 1)]
-        ahead = [[], [], [(2, 0)], [(2, 1)], [(2, 2), (3, 0)], [(3, 1), (3, 2)]]
+        ahead = [[], [], [], [], [(2, 2), (3, 0)], [(3, 1), (3, 2)]]
         for beat in range(6):
             c, e = divmod(beat + 2, 2)
             for run in ahead[beat]:

@@ -27,6 +27,7 @@ BYTES = (
 
 KIB = 1024
 STAGE_BUFS = 10
+HELPED = 8
 
 
 def tile_mla_pa_v_kernel(
@@ -62,12 +63,10 @@ def tile_mla_pa_v_kernel(
         ones = kept("ones", [128, 128], BF16)
         nc.gpsimd.memset(ones[:], 1.0)
         gain_row = kept("gain_row", [128, RANK], BF16)
-        nc.gpsimd.memset(gain_row[:], 0.0)
         gain = kept("gain", [128, RANK], F32)
-        cos_in = kept("cos_in", [128, 128], BF16)
-        sin_in = kept("sin_in", [128, 128], BF16)
-        cos_pairs = kept("cos_pairs", [128, 128, 2], BF16)
-        sin_pairs = kept("sin_pairs", [128, 128, 2], BF16)
+        angles = kept("angles", [128, 128], BF16)
+        pick = kept("pick", [128, 3, 128], BF16)
+        sin_pairs = kept("sin_pairs", [128, 256], BF16)
         mu_col = kept("mu_col", [128, 4], F32)
         rstd_col = kept("rstd_col", [128, 4], F32)
         factors = kept("factors", [128, 4, 2], F32)
@@ -102,12 +101,12 @@ def tile_mla_pa_v_kernel(
         free_stages = [STAGE + 4 * i for i in range(STAGE_BUFS)]
         count = []
 
-        def stage_tile():
-            kib = free_stages.pop(0)
+        def stage_tile(which=0):
+            kib = free_stages.pop(which)
             count.append(kib)
             return placed("stage%d" % len(count), [128, 1024], F32, kib), lambda: free_stages.append(kib)
 
-        ring = list(range(8))
+        ring = list(range(7))
         held = []
 
         def bank_tile(name, number=None):
@@ -127,7 +126,6 @@ def tile_mla_pa_v_kernel(
 
         def transposes(name, blocks, places, engines):
             banks = []
-            ring[0], ring[1] = ring[1], ring[0]
             for b in range(2):
                 bank = bank_tile(name)
                 banks.append(bank[:].rearrange("p (a u n) -> p a u n", a=2, u=2))
@@ -188,12 +186,12 @@ def tile_mla_pa_v_kernel(
             places = [t[:].rearrange("p (a i n u) -> p a i n u", a=2, i=2, u=2)[:, :, j % 2] for t, release in stages]
             transposes("w", [words(raw[(s, j)], 512 * g) for g in range(4)], places, "SS")
 
-            def finish(b):
-                for a in range(2):
-                    quantize(cols(w2_mx, 512 * (4 * s + 2 * b + a) + 256 * (j // 2), 256), E4M3, stages[b][0][:, 512 * a : 512 * a + 512])
-                stages[b][1]()
+            def finish(b, a):
+                quantize(cols(w2_mx, 512 * (4 * s + 2 * b + a) + 256 * (j // 2), 256), E4M3, stages[b][0][:, 512 * a : 512 * a + 512])
+                if a == 1:
+                    stages[b][1]()
 
-            return [lambda b=b: finish(b) for b in range(2)]
+            return [lambda b=b, a=a: finish(b, a) for b in range(2) for a in range(2)]
 
         def z_run(j, s):
             rows, start = (grad_1_in[j], 0) if s else (dk[:], DK * j)
@@ -233,24 +231,56 @@ def tile_mla_pa_v_kernel(
             source = wkv_in[n][:].bitcast(F32).rearrange("p (j w) -> p j w", j=4)[:, :, 256 * g : 256 * g + 256]
             nc.vector.tensor_copy(out=split[(n, g)][0], in_=source.rearrange("p j (w u) -> p j u w", u=2))
 
-        def tables():
+        def pickers():
+            nc.vector.memset(gain_row[:], 0.0)
+            nc.vector.memset(pick[:], 0.0)
+            low = identity[0:64, 0:64].unsqueeze(1).to_broadcast([64, 2, 64])
+            high = identity[64:128, 64:128].unsqueeze(1).to_broadcast([64, 2, 64])
+            nc.vector.tensor_copy(out=pick[0:64, 0, :].rearrange("p (a q) -> p a q", a=2), in_=low)
+            nc.vector.tensor_copy(out=pick[64:128, 1, :].rearrange("p (a q) -> p a q", a=2), in_=high)
+            nc.vector.tensor_scalar(out=pick[64:128, 2, :].rearrange("p (a q) -> p a q", a=2), in0=high, scalar1=-1.0, scalar2=None, op0=MULT)
+
+        table = []
+
+        def spread(bank, which):
             for e in range(2):
-                nc.vector.tensor_copy(out=cos_pairs[:, :, e], in_=cos_in[:])
-            nc.vector.tensor_scalar(out=sin_pairs[:, :, 0], in0=sin_in[:], scalar1=-1.0, scalar2=None, op0=MULT)
-            nc.vector.tensor_copy(out=sin_pairs[:, :, 1], in_=sin_in[:])
+                nc.tensor.matmul(bank.rearrange("p (w e) -> p w e", e=2)[:, :, e], pick[:, which[e], :], angles[:], start=True, stop=True)
+
+        def tables():
+            spare = bank_tile("sin_spare")
+            bank = bank_tile("table", 7)
+            spread(spare[:, 0:256], (2, 1))
+            spread(bank[:, 0:256], (0, 0))
+            spread(bank[:, 256:512], (2, 1))
+            copy("S", sin_pairs[:], spare[:, 0:256])
+            table.append(bank)
 
         def temp():
             return placed("temp", [128, 1024], F32, TEMP, bufs=4)
 
-        def rotate(j, first=0, last=HEADS):
-            pairs = dk[:, DK * j : DK * j + DK].rearrange("p (h w) -> p h w", w=HEAD)[:, first:last, 128:HEAD]
-            halves = []
-            for table in (cos_pairs, sin_pairs):
-                half = temp()[:, 0 : 64 * (last - first)]
-                halves.append(half.rearrange("p (h w e) -> p h w e", w=32, e=2))
-                row = table[:, 32 * j : 32 * j + 32, :].rearrange("p w e -> p (w e)")
-                nc.vector.tensor_tensor(out=half.rearrange("p (h w) -> p h w", w=64), in0=pairs, in1=row.unsqueeze(1).to_broadcast([128, last - first, 64]), op=MULT)
-            return lambda: nc.vector.tensor_tensor(out=pairs.rearrange("p h (w e) -> p h w e", e=2), in0=halves[0], in1=halves[1][:, :, :, ::-1], op=ADD)
+        def rotate(j):
+            pairs = dk[:, DK * j : DK * j + DK].rearrange("p (h w) -> p h w", w=HEAD)[:, :, 128:HEAD]
+            by_cos = temp()[:].rearrange("p (h w) -> p h w", w=64)
+            stage, release = stage_tile(-1)
+            by_sin = stage[:].rearrange("p (h w) -> p h w", w=64)
+
+            def product(engine, out, heads, row):
+                engine.tensor_tensor(out=out[:, heads], in0=pairs[:, heads], in1=row.unsqueeze(1).to_broadcast([128, heads.stop - heads.start, 64]), op=MULT)
+
+            product(nc.gpsimd, by_sin, slice(0, HELPED), sin_pairs[:, 64 * j : 64 * j + 64])
+            product(nc.vector, by_cos, slice(0, HEADS), table[0][:, 64 * j : 64 * j + 64])
+            product(nc.vector, by_sin, slice(HELPED, HEADS), table[0][:, 256 + 64 * j : 256 + 64 * j + 64])
+
+            def add():
+                nc.vector.tensor_tensor(
+                    out=pairs.rearrange("p h (w e) -> p h w e", e=2),
+                    in0=by_cos.rearrange("p h (w e) -> p h w e", e=2),
+                    in1=by_sin.rearrange("p h (w e) -> p h w e", e=2)[:, :, :, ::-1],
+                    op=ADD,
+                )
+                release()
+
+            return add
 
         def spread_gain():
             bank = bank_tile("gain")
@@ -353,102 +383,18 @@ def tile_mla_pa_v_kernel(
 
             return [step(i) for i in range(4)], lambda: nc.sync.dma_start(out=target, in_=source)
 
-        def group_0(half, first, count, only=None):
+        def group_0(half, first, count):
             t = out_tile()
+            rows = t[:, 0 : 1024 * count].rearrange("p (j w) -> p j w", j=count)
 
-            def step(j, n):
-                def run(engine):
-                    side = t[:, 1024 * (j - first) + 512 * n : 1024 * (j - first) + 512 * n + 512]
-                    copy(engine, side.rearrange("p (q j) -> p q j", j=4), out_0_bank(2 * half + n, j)[:].rearrange("p (j q) -> p q j", j=4))
+            def step(j, n, engine):
+                side = rows[:, j - first, 512 * n : 512 * n + 512]
+                copy(engine, side.rearrange("p (q j) -> p q j", j=4), out_0_bank(2 * half + n, j)[:].rearrange("p (j q) -> p q j", j=4))
 
-                return run
+            def store(start=0, stop=1024):
+                nc.sync.dma_start(out=out_0_rows[:, first : first + count, 1024 * half + start : 1024 * half + stop], in_=rows[:, :, start:stop])
 
-            def store():
-                nc.sync.dma_start(out=out_0_rows[:, first : first + count, 1024 * half : 1024 * half + 1024], in_=t[:, 0 : 1024 * count].rearrange("p (j w) -> p j w", j=count))
-
-            if only is not None:
-                part = slice(512 * only, 512 * only + 512)
-                return [step(first, only)], lambda: nc.sync.dma_start(out=out_0_rows[:, first, 1024 * half : 1024 * half + 1024][:, part], in_=t[:, part])
-            return [step(j, n) for j in range(first, first + count) for n in range(2)], store
-
-        ctx.enter_context(tc.manual_schedule())
-
-        for half in (slice(0, 64), slice(64, 128)):
-            nc.sync.dma_start(out=cos_in[half], in_=cos_rows)
-            nc.sync.dma_start(out=sin_in[half], in_=sin_rows)
-        load_dk(0, 0, 8)
-        load_dk(0, 8, 16)
-        load_w(1, 0, 1)
-        nc.sync.dma_start(out=gain_row[0:1, :], in_=kvn_g.rearrange("(o w) -> o w", o=1))
-        load_dk(1)
-        load_w(1, 1, 1)
-        load_w(1, 2, 1)
-        load_dk(2)
-        load_w(1, 3, 1)
-        load_w(0, 0, 1)
-        load_dk(3)
-        load_w(0, 1, 1)
-        load_w(0, 2, 1)
-        load_w(0, 3, 1)
-        load_grad_1(0, 2)
-        load_grad_1(2, 2)
-
-        tables()
-        add_a = rotate(0, 0, 8)
-        add_b = rotate(0, 8, 16)
-        add_a()
-        add_b()
-        w_run(1, 0)
-        q_nope = [z_run(0, 0)]
-        spread_gain()
-        add = rotate(1)
-        q_nope[0]()
-        add()
-        q_w = w_run(1, 1)
-        w_run(1, 2)
-        q_nope.append(z_run(1, 0))
-        q_f = [f_run(0)]
-        add = rotate(2)
-        q_w[0]()
-        add()
-        q_w.extend(w_run(1, 3))
-        w_run(0, 0)
-        q_w[1]()
-        q_nope.append(z_run(2, 0))
-        load_x()
-        nc.sync.dma_start(out=mu_col[:], in_=mu_rows)
-        nc.sync.dma_start(out=rstd_col[:], in_=rstd_rows)
-        nc.sync.dma_start(out=c_in[:], in_=c_lat_rows)
-        load_wkv(0)
-        add = rotate(3)
-        q_w[2]()
-        add()
-        q_w.extend(w_run(0, 1))
-        q_w[3]()
-        q_w[4]()
-        w_run(0, 2)
-        q_w[5]()
-        q_w.extend(w_run(0, 3))
-        q_t = [z_block(0)]
-        q_nope.append(z_run(3, 0))
-        q_nope[1]()
-        q_v = [z_run(0, 1)]
-        q_t[0]()
-        load_wkv(1)
-        q_w[6]()
-        q_v.append(z_run(1, 1))
-        q_w[7]()
-        q_v.append(z_run(2, 1))
-        q_v[0]()
-        q_v.append(z_run(3, 1))
-        load_wkv(2)
-        load_wkv(3)
-        q_v[1]()
-        q_f.append(f_run(1))
-        q_t.append(z_block(1))
-        q_x = [x_block(0), x_block(1, "S"), x_block(2, "S")]
-        q_t[1]()
-        q_x[0]()
+            return step, store
 
         def banks(steps, engines):
             for step, engine in zip(steps, engines):
@@ -459,9 +405,90 @@ def tile_mla_pa_v_kernel(
             banks(steps, engines)
             store()
 
+        def run(queue, count=1):
+            for i in range(count):
+                queue.pop(0)()
+
+        ctx.enter_context(tc.manual_schedule())
+
+        pickers()
+        nc.sync.dma_start(out=angles[0:64], in_=cos_rows)
+        nc.sync.dma_start(out=angles[64:128], in_=sin_rows)
+        load_dk(0)
+        nc.sync.dma_start(out=gain_row[0:1, :], in_=kvn_g.rearrange("(o w) -> o w", o=1))
+        load_w(1, 0, 1)
+        load_w(1, 1, 1)
+        load_dk(1)
+        load_w(1, 2, 1)
+        load_w(1, 3, 1)
+        load_dk(2)
+        load_w(0, 0, 1)
+        load_w(0, 1, 1)
+        load_dk(3)
+        load_w(0, 2, 1)
+        load_w(0, 3, 1)
+        load_grad_1(0, 1)
+        load_grad_1(1, 1)
+        load_grad_1(2, 2)
+
+        tables()
+        spread_gain()
+        rotate(0)()
+        w_run(1, 0)
+        q_w = w_run(1, 1)
+        q_nope = [z_run(0, 0)]
+        add = rotate(1)
+        run(q_w)
+        add()
+        w_run(1, 2)
+        run(q_w, 3)
+        q_w.extend(w_run(1, 3))
+        q_nope.append(z_run(1, 0))
+        q_f = [f_run(0)]
+        add = rotate(2)
+        run(q_w)
+        add()
+        w_run(0, 0)
+        run(q_w, 3)
+        q_w.extend(w_run(0, 1))
+        q_nope.append(z_run(2, 0))
+        load_x()
+        nc.sync.dma_start(out=mu_col[:], in_=mu_rows)
+        nc.sync.dma_start(out=rstd_col[:], in_=rstd_rows)
+        nc.sync.dma_start(out=c_in[:], in_=c_lat_rows)
+        add = rotate(3)
+        ring.append(7)
+        run(q_w)
+        add()
+        w_run(0, 2)
+        run(q_w, 3)
+        q_w.extend(w_run(0, 3))
+        load_wkv(0)
+        q_nope[0]()
+        q_v = [z_run(0, 1)]
+        q_nope[1]()
+        q_nope.append(z_run(3, 0))
+        run(q_w, 4)
+        load_wkv(1)
+        q_v.append(z_run(1, 1))
+        q_v[0]()
+        q_t = [z_block(0)]
+        q_f.append(f_run(1))
+        q_v[1]()
+        q_t[0]()
+        q_v.append(z_run(2, 1))
+        q_t.append(z_block(1))
+        q_v.append(z_run(3, 1))
+        load_wkv(2)
+        load_wkv(3)
+        q_x = [x_block(0), x_block(1, "S"), x_block(2, "S")]
+        q_t[1]()
+        q_x[0]()
+
         def zero(half, j, engines):
-            steps, store = group_0(half, j, 1)
-            banks(steps, engines)
+            step, store = group_0(half, j, 1)
+            for n in range(2):
+                step(j, n, engines[n])
             store()
 
         held.extend([ring.pop(0), ring.pop(0)])
@@ -545,7 +572,7 @@ def tile_mla_pa_v_kernel(
         zero(0, 3, "SV")
         for j in range(3):
             zero(1, j, "SV")
+        step, store = group_0(1, 3, 1)
         for n in range(2):
-            steps, store = group_0(1, 3, 1, n)
-            steps[0]("SV"[n])
-            store()
+            step(3, n, "SV"[n])
+            store(512 * n, 512 * n + 512)

@@ -27,7 +27,8 @@ BYTES = (
 
 KIB = 1024
 STAGE_BUFS = 10
-HELPED = 8
+HELPED = 9
+WK_STAGE = 152
 
 
 def tile_mla_pa_v_kernel(
@@ -126,13 +127,13 @@ def tile_mla_pa_v_kernel(
 
         def transposes(name, blocks, places, engines):
             banks = []
-            for b in range(2):
+            for b in range(len(places)):
                 bank = bank_tile(name)
                 banks.append(bank[:].rearrange("p (a u n) -> p a u n", a=2, u=2))
                 for a in range(2):
                     for u in range(2):
                         nc.tensor.transpose(banks[b][:, a, u, :], blocks[2 * b + a][:, u, :], identity[:])
-            for b in range(2):
+            for b in range(len(places)):
                 copy(engines[b], places[b], banks[b].rearrange("p a u n -> p a n u"))
 
         def turn(name, blocks, fmt, engines="SS"):
@@ -193,14 +194,37 @@ def tile_mla_pa_v_kernel(
 
             return [lambda b=b, a=a: finish(b, a) for b in range(2) for a in range(2)]
 
+        wide = []
+
+        def wk_run(j):
+            if j == 0:
+                wide.extend([placed("wk_stage%d" % b, [128, 2048], F32, WK_STAGE + 8 * b) for b in range(2)])
+            places = [t[:].rearrange("p (a j n u) -> p a j n u", a=2, j=4, u=2)[:, :, j] for t in wide]
+            transposes("w", [words(raw[(0, j)], 512 * g) for g in range(4)], places, "SS")
+
+        def wk_quantize(g):
+            quantize(cols(w2_mx, 512 * g, 512), E4M3, wide[g // 2][:, 1024 * (g % 2) : 1024 * (g % 2) + 1024])
+
         def z_run(j, s):
             rows, start = (grad_1_in[j], 0) if s else (dk[:], DK * j)
             finish = turn("z%d%d" % (j, s), [words(rows, start + 512 * g) for g in range(4)], E5M2)
             return lambda: finish(cols(dz2_mx, 1024 * j + 512 * s, 512))
 
-        def f_run(q):
-            finish = turn("f", [words(dk[:], DK * (2 * q + i) + NOPE + 512 * g) for i in range(2) for g in range(2)], E5M2)
-            return lambda: finish(cols(rope_mx, 512 * q, 512))
+        rope_pair = []
+
+        def f_run(j):
+            if j % 2 == 0:
+                rope_pair.clear()
+                rope_pair.extend(stage_tile())
+            stage, release = rope_pair
+            place = stage[:].rearrange("p (b a n u) -> p b a n u", b=2, a=2, u=2)[:, j % 2]
+            transposes("f", [words(dk[:], DK * j + NOPE + 512 * g) for g in range(2)], [place], "S")
+
+            def finish():
+                quantize(cols(rope_mx, 512 * (j // 2), 512), E5M2, stage[:])
+                release()
+
+            return finish
 
         def d_run(engines):
             finish = turn("d", [words(dc[:], RANK * j) for j in range(4)], E5M2, engines)
@@ -225,14 +249,15 @@ def tile_mla_pa_v_kernel(
 
             return done
 
-        def k_split(n, g):
+        def k_split(n, g, engine="V"):
             t, release = stage_tile()
             split[(n, g)] = t[:].rearrange("p (j u w) -> p j u w", j=4, u=2), release
             source = wkv_in[n][:].bitcast(F32).rearrange("p (j w) -> p j w", j=4)[:, :, 256 * g : 256 * g + 256]
-            nc.vector.tensor_copy(out=split[(n, g)][0], in_=source.rearrange("p j (w u) -> p j u w", u=2))
+            copy(engine, split[(n, g)][0], source.rearrange("p j (w u) -> p j u w", u=2))
 
         def pickers():
             nc.vector.memset(gain_row[:], 0.0)
+            nc.vector.memset(factors[:, :, 0], 1.0 / RANK)
             nc.vector.memset(pick[:], 0.0)
             low = identity[0:64, 0:64].unsqueeze(1).to_broadcast([64, 2, 64])
             high = identity[64:128, 64:128].unsqueeze(1).to_broadcast([64, 2, 64])
@@ -288,7 +313,6 @@ def tile_mla_pa_v_kernel(
             copy("S", gain[:], bank[:])
 
         def norm_factors():
-            nc.vector.memset(factors[:, :, 0], 1.0 / RANK)
             nc.vector.scalar_tensor_tensor(out=factors[:, :, 1], in0=rstd_col[:], scalar=1.0 / RANK, in1=rstd_col[:], op0=MULT, op1=MULT)
 
         def dh(j):
@@ -346,14 +370,11 @@ def tile_mla_pa_v_kernel(
                 source = dc[:].rearrange("p (j w) -> p j w", j=4)
             return tokens_beside(source, cols(token_mx, 512 * n, 512), E5M2, engine, "p (c r e j) -> p c j r e")
 
-        free_places = []
         made = []
 
-        def out_tile():
-            kib = free_places.pop(0)
-            free_places.append(kib)
+        def out_tile(kib, width):
             made.append(kib)
-            return placed("out%d" % len(made), [128, 2048], F32, kib)
+            return placed("out%d" % len(made), [128, width], F32, kib)
 
         def out_1_bank(m, n):
             bank = bank_tile("al%d%d" % (m, n))
@@ -367,25 +388,35 @@ def tile_mla_pa_v_kernel(
                 matmul_mx(bank[:], left, E5M2, cols(wkv_mx[n], 512 * g, 512), E4M3, g == 0, g == 2)
             return bank
 
-        def group(kind, c, i):
-            t = out_tile()
-            if kind == "rope":
-                pieces = [(r, n) for r in range(2) for n in range(2)]
-                target = out_1_rows[:, c, :, 0, 0:ROPE]
-                source = t[:].rearrange("p (i w) -> p i w", i=2)
-            else:
-                pieces = [(i, 2), (2 + i, 0), (2 + i, 1), (2 + i, 2)]
-                target = out_1_rows[:, c, i].rearrange("p e w -> p (e w)")[:, ROPE : 2 * WIDTH]
-                source = t[:]
+        def out_1_part(c, i, first, last, kib, engines):
+            count = last - first
+            t = out_tile(kib, 1024 * count)
+            for e in range(2):
+                for n in range(first, last):
+                    place = count * e + n - first
+                    copy(engines[place], t[:, 512 * place : 512 * place + 512], out_1_bank(4 * c + 2 * e + i, n)[:])
+            nc.sync.dma_start(out=out_1_rows[:, c, i, :, 512 * first : 512 * last], in_=t[:].rearrange("p (e w) -> p e w", e=2))
+
+        def out_1_rest(c, i, kib, engines):
+            t = out_tile(kib, 2048)
+            for place, (e, n) in enumerate([(0, 2), (1, 0), (1, 1), (1, 2)]):
+                copy(engines[place], t[:, 512 * place : 512 * place + 512], out_1_bank(4 * c + 2 * e + i, n)[:])
+            nc.sync.dma_start(out=out_1_rows[:, c, i].rearrange("p e w -> p (e w)")[:, ROPE : 2 * WIDTH], in_=t[:])
+
+        def out_1_early(c, kib):
+            t = out_tile(kib, 2048)
 
             def step(i):
-                return lambda engine: copy(engine, t[:, 512 * i : 512 * i + 512], out_1_bank(4 * c + pieces[i][0], pieces[i][1])[:])
+                for n in range(2):
+                    copy("S", t[:, 1024 * i + 512 * n : 1024 * i + 512 * n + 512], out_1_bank(4 * c + i, n)[:])
+                if i == 1:
+                    nc.sync.dma_start(out=out_1_rows[:, c, :, 0, 0:ROPE], in_=t[:].rearrange("p (i w) -> p i w", i=2))
 
-            return [step(i) for i in range(4)], lambda: nc.sync.dma_start(out=target, in_=source)
+            return step
 
-        def group_0(half, first, count):
-            t = out_tile()
-            rows = t[:, 0 : 1024 * count].rearrange("p (j w) -> p j w", j=count)
+        def group_0(half, first, count, kib):
+            t = out_tile(kib, 1024 * count)
+            rows = t[:].rearrange("p (j w) -> p j w", j=count)
 
             def step(j, n, engine):
                 side = rows[:, j - first, 512 * n : 512 * n + 512]
@@ -395,15 +426,6 @@ def tile_mla_pa_v_kernel(
                 nc.sync.dma_start(out=out_0_rows[:, first : first + count, 1024 * half + start : 1024 * half + stop], in_=rows[:, :, start:stop])
 
             return step, store
-
-        def banks(steps, engines):
-            for step, engine in zip(steps, engines):
-                step(engine)
-
-        def part(kind, c, e, engines="SSSS"):
-            steps, store = group(kind, c, e)
-            banks(steps, engines)
-            store()
 
         def run(queue, count=1):
             for i in range(count):
@@ -437,6 +459,7 @@ def tile_mla_pa_v_kernel(
         w_run(1, 0)
         q_w = w_run(1, 1)
         q_nope = [z_run(0, 0)]
+        f_run(0)
         add = rotate(1)
         run(q_w)
         add()
@@ -444,135 +467,146 @@ def tile_mla_pa_v_kernel(
         run(q_w, 3)
         q_w.extend(w_run(1, 3))
         q_nope.append(z_run(1, 0))
-        q_f = [f_run(0)]
+        q_f = [f_run(1)]
         add = rotate(2)
         run(q_w)
         add()
-        w_run(0, 0)
+        wk_run(0)
         run(q_w, 3)
-        q_w.extend(w_run(0, 1))
+        wk_run(1)
         q_nope.append(z_run(2, 0))
+        f_run(2)
         load_x()
         nc.sync.dma_start(out=mu_col[:], in_=mu_rows)
         nc.sync.dma_start(out=rstd_col[:], in_=rstd_rows)
         nc.sync.dma_start(out=c_in[:], in_=c_lat_rows)
         add = rotate(3)
         ring.append(7)
-        run(q_w)
-        add()
-        w_run(0, 2)
-        run(q_w, 3)
-        q_w.extend(w_run(0, 3))
-        load_wkv(0)
         q_nope[0]()
-        q_v = [z_run(0, 1)]
+        add()
+        wk_run(2)
+        wk_run(3)
+        load_wkv(0)
         q_nope[1]()
+        q_t = [z_block(0)]
+        q_v = [z_run(0, 1)]
         q_nope.append(z_run(3, 0))
-        run(q_w, 4)
+        for g in range(4):
+            wk_quantize(g)
         load_wkv(1)
         q_v.append(z_run(1, 1))
         q_v[0]()
-        q_t = [z_block(0)]
-        q_f.append(f_run(1))
-        q_v[1]()
+        q_f.append(f_run(3))
         q_t[0]()
-        q_v.append(z_run(2, 1))
         q_t.append(z_block(1))
+        q_v.append(z_run(2, 1))
+        q_v[1]()
         q_v.append(z_run(3, 1))
         load_wkv(2)
         load_wkv(3)
-        q_x = [x_block(0), x_block(1, "S"), x_block(2, "S")]
         q_t[1]()
-        q_x[0]()
-
-        def zero(half, j, engines):
-            step, store = group_0(half, j, 1)
-            for n in range(2):
-                step(j, n, engines[n])
-            store()
+        q_x = [x_block(0, "S"), x_block(1, "S")]
+        q_nope[2]()
+        norm_factors()
+        q_v[2]()
 
         held.extend([ring.pop(0), ring.pop(0)])
         norm = [dh(0), dh(1)]
-        norm_factors()
         norm[0][0]()
-        q_nope[2]()
+        q_x[0]()
         norm[0][1]()
-        q_v[2]()
-        free_places.extend([0, 8, 16, 220])
-        part("rope", 0, None)
-        q_x.append(x_block(3, "S"))
-        norm.append(dh(2))
-        norm[1][0]()
-        q_x[1]()
-        norm[1][1]()
         q_nope[3]()
         norm[0][2]()
-        q_v[3]()
-        part("rope", 1, None)
-        norm.append(dh(3))
-        norm[1][2]()
+        out_1_part(0, 0, 0, 2, 0, "SSSS")
+        q_x.append(x_block(2, "S"))
+        norm.append(dh(2))
+        norm[1][0]()
         norm[0][3]()
-        norm[2][0]()
+        norm[1][1]()
+        q_v[3]()
+        norm[1][2]()
+        out_1_part(0, 1, 0, 2, 8, "SSSS")
+        norm.append(dh(3))
         norm[0][4]()
-        norm[2][1]()
+        q_x[1]()
         norm[1][3]()
+        norm[2][0]()
+        norm[1][4]()
+        norm[2][1]()
+        early = [out_1_early(1, 16), out_1_early(2, 220)]
+        q_k = [k_run(0, 0)]
+        early[0](0)
         q_x[2]()
         norm[2][2]()
-        q_k = {(0, 0): k_run(0, 0)}
-        norm[1][4]()
         norm[3][0]()
-        part("rope", 2, None)
         norm[2][3]()
         norm[3][1]()
-        q_x[3]()
-        norm[3][2]()
         ring.extend(held)
-        q_k[(0, 1)] = k_run(0, 1)
+        q_k.append(k_run(0, 1))
+        early[0](1)
         norm[2][4]()
+        norm[3][2]()
+        run(q_k)
         norm[3][3]()
-        q_f[0]()
+        q_k.append(k_run(0, 2))
+        early[1](0)
         norm[3][4]()
-        q_f[1]()
         q_t2 = z_block(2)
-        part("rope", 3, None, "SSSS")
-        q_k[(0, 2)] = k_run(0, 2, "SS")
-        for kib in (128, 120, 112, 64):
-            free_places.insert(0, kib)
-        rest = [group("rest", 0, e) for e in range(2)]
-        q_k[(0, 0)]()
         q_t2()
-        for steps, store in rest:
-            banks(steps[1:3], "VS")
-        q_k[(1, 0)] = k_run(1, 0, "VS")
-        for steps, store in rest:
-            banks(steps[0:4:3], "VS")
-            store()
-        waiting = [q_k[(0, 1)], q_k[(0, 2)], q_k[(1, 0)]]
-        later = [(1, 1), None, (1, 2), (2, 0), (2, 1)]
-        ahead = [[], [], [], [], [(2, 2), (3, 0)], [(3, 1), (3, 2)]]
-        for beat in range(6):
-            c, e = divmod(beat + 2, 2)
-            for run in ahead[beat]:
-                k_split(*run)
-            waiting.pop(0)()
-            part("rest", c, e, "SVSV")
-            if beat == 3:
-                free_places.insert(0, 76)
-            if beat < 5:
-                waiting.append(k_run(*later[beat]) if later[beat] else d_run("SS"))
-        waiting.extend([k_run(2, 2), k_run(3, 0, "SV")])
-        zero(0, 0, "SV")
-        waiting.pop(0)()
-        waiting.pop(0)()
-        waiting.extend([k_run(3, 1, "SV"), k_run(3, 2, "SV")])
-        for j in (1, 2):
-            waiting.pop(0)()
-            waiting.pop(0)()
-            zero(0, j, "SS")
-        zero(0, 3, "SV")
-        for j in range(3):
-            zero(1, j, "SV")
-        step, store = group_0(1, 3, 1)
+        q_d = d_run("VV")
+        early[1](1)
+        run(q_k)
+        q_d()
+        out_1_part(0, 0, 2, 3, 112, "SS")
+        out_1_part(0, 1, 2, 3, 116, "SV")
+        q_f[0]()
+        q_f[1]()
+        run(q_k)
+        out_1_rest(1, 0, 120, "SSSS")
+        left = [group_0(0, 0, 2, 128), group_0(0, 2, 2, 0)]
+        q_k.append(k_run(1, 0, "VS"))
+        out_1_rest(1, 1, 8, "VSVV")
+        for j in range(2):
+            left[0][0](j, 0, "S")
+        q_x.append(x_block(3))
+        out_1_rest(2, 0, 64, "SSVS")
+        q_k.append(k_run(1, 1))
+        q_x[3]()
+        run(q_k)
+        out_1_rest(2, 1, 16, "VSVV")
+        for j in range(2, 4):
+            left[1][0](j, 0, "S")
+        k_split(2, 0)
+        run(q_k)
+        q_k.append(k_run(1, 2))
+        k_split(2, 1)
+        out_1_part(3, 0, 0, 3, 112, "SVSVSV")
+        run(q_k)
+        q_k.extend([k_run(2, 0), k_run(2, 1)])
+        k_split(2, 2)
+        k_split(3, 0)
+        for j in range(2):
+            left[0][0](j, 1, "SV"[j])
+        left[0][1]()
+        q_k.extend([k_run(2, 2), k_run(3, 0)])
+        k_split(3, 1)
+        k_split(3, 2)
+        out_1_part(3, 1, 0, 3, 76, "VVSVSV")
+        q_k.extend([k_run(3, 1), k_run(3, 2)])
+        run(q_k, 3)
+        for j in range(2, 4):
+            left[1][0](j, 1, "S")
+        left[1][1]()
+        run(q_k, 3)
+        right = [group_0(1, j, 1, kib) for j, kib in enumerate((8, 12, 64, 68))]
+        for j in range(2):
+            right[j][0](j, 0, "S")
+        for j in range(2):
+            right[j][0](j, 1, "SV"[j])
+            right[j][1]()
         for n in range(2):
-            step(3, n, "SV"[n])
-            store(512 * n, 512 * n + 512)
+            right[2][0](2, n, "SV"[n])
+        right[2][1]()
+        for n in range(2):
+            right[3][0](3, n, "SV"[n])
+            right[3][1](512 * n, 512 * n + 512)

@@ -35,7 +35,7 @@ def tile_mla_pa_v_kernel(
     tc, x, wkv_a_w, wkv_a_b, kvn_g, kvn_b, wk_w, wk_b, wv_w, wv_b, cos, sin, c_lat, mu, rstd, grad_0, grad_1, out_0, out_1
 ):
     nc = tc.nc
-    x_rows = x.flatten_outer_dims().rearrange("(p j) w -> p (j w)", j=4)
+    x_rows = x.flatten_outer_dims().rearrange("(p j) w -> p j w", j=4)
     grad_0_rows = grad_0.rearrange("b s h d -> (b s) (h d)").rearrange("(p j) w -> p (j w)", j=4)
     grad_1_rows = grad_1.rearrange("b s h d -> (b s) (h d)").rearrange("(p j) w -> p (j w)", j=4)
     c_lat_rows = c_lat.flatten_outer_dims().rearrange("(p j) w -> p (j w)", j=4)
@@ -82,7 +82,7 @@ def tile_mla_pa_v_kernel(
         w2_mx = operand("w2", 8 * RANK, 24)
         dz2_mx = operand("dz2", 4 * 8 * 128, 44)
         c_in = placed("c_in", [128, 4 * RANK], F32, C_AT)
-        x_in = placed("x_in", [128, 4 * DIM], BF16, X_AT)
+        x_in = [placed("x_in%d" % h, [128, 4 * 1024], BF16, X_AT + 8 * h) for h in range(2)]
         x_mx = [operand("x%d" % c, 512, 152 + 2.5 * c) for c in range(4)]
         token_mx = operand("dz1_token", WIDTH, 162)
         rope_mx = operand("rope", 4 * 2 * 128, 169.5)
@@ -174,8 +174,8 @@ def tile_mla_pa_v_kernel(
             part = slice(DK * j + HEAD * first, DK * j + HEAD * last)
             nc.sync.dma_start(out=dk[:, part], in_=grad_0_rows[:, part])
 
-        def load_x():
-            nc.sync.dma_start(out=x_in[:], in_=x_rows)
+        def load_x(h):
+            nc.sync.dma_start(out=x_in[h][:].rearrange("p (j w) -> p j w", j=4), in_=x_rows[:, :, 1024 * h : 1024 * h + 1024])
 
         pair = []
 
@@ -361,7 +361,7 @@ def tile_mla_pa_v_kernel(
             return finish
 
         def x_block(c, engine="V"):
-            return tokens_beside(x_in[:].rearrange("p (j w) -> p j w", j=4)[:, :, 512 * c : 512 * c + 512], cols(x_mx[c], 0, 512), E4M3, engine, "p (e c r j) -> p c j r e")
+            return tokens_beside(x_in[c // 2][:].rearrange("p (j w) -> p j w", j=4)[:, :, 512 * (c % 2) : 512 * (c % 2) + 512], cols(x_mx[c], 0, 512), E4M3, engine, "p (e c r j) -> p c j r e")
 
         def z_block(n, engine="V"):
             if n < 2:
@@ -476,10 +476,11 @@ def tile_mla_pa_v_kernel(
         wk_run(1)
         q_nope.append(z_run(2, 0))
         f_run(2)
-        load_x()
+        load_x(0)
         nc.sync.dma_start(out=mu_col[:], in_=mu_rows)
         nc.sync.dma_start(out=rstd_col[:], in_=rstd_rows)
         nc.sync.dma_start(out=c_in[:], in_=c_lat_rows)
+        load_x(1)
         add = rotate(3)
         ring.append(7)
         q_nope[0]()

@@ -42,7 +42,7 @@ def tile_mla_pa_v_kernel(
     mu_rows = mu.flatten_outer_dims().rearrange("(p j) o -> p (j o)", j=4)
     rstd_rows = rstd.flatten_outer_dims().rearrange("(p j) o -> p (j o)", j=4)
     w2_rows = [w.rearrange("(p j) w -> p (j w)", j=4) for w in (wk_w, wv_w)]
-    wkv_rows = wkv_a_w.rearrange("(n p j) w -> n p (j w)", p=128, j=4)
+    wkv_rows = wkv_a_w.rearrange("(n p j) w -> p n (j w)", p=128, j=4)
     out_0_rows = out_0.flatten_outer_dims().rearrange("(p j) w -> p j w", j=4)
     out_1_rows = out_1.rearrange("(c i p e) w -> p c i e w", i=2, p=128, e=2)
     cos_rows = cos.rearrange("(q j) w -> q (j w)", j=4)
@@ -165,10 +165,11 @@ def tile_mla_pa_v_kernel(
 
         wkv_in = {}
 
-        def load_wkv(n):
-            t = placed("wkv_in%d" % n, [128, 4 * WIDTH], BF16, RAW + 12 * n)
-            wkv_in[n] = t
-            nc.sync.dma_start(out=t[:], in_=wkv_rows[n])
+        def load_wkv(first, count):
+            t = placed("wkv_in%d" % first, [128, count * 4 * WIDTH], BF16, RAW + 12 * first)
+            for n in range(count):
+                wkv_in[first + n] = t[:, 4 * WIDTH * n : 4 * WIDTH * (n + 1)]
+            nc.sync.dma_start(out=t[:].rearrange("p (n w) -> p n w", n=count), in_=wkv_rows[:, first : first + count])
 
         def load_dk(j, first=0, last=HEADS):
             part = slice(DK * j + HEAD * first, DK * j + HEAD * last)
@@ -192,7 +193,13 @@ def tile_mla_pa_v_kernel(
                 if a == 1:
                     stages[b][1]()
 
-            return [lambda b=b, a=a: finish(b, a) for b in range(2) for a in range(2)]
+            def finish_tile(b, a):
+                start = 512 * a + 256 * (j % 2)
+                quantize(cols(w2_mx, 512 * (4 * s + 2 * b + a) + 128 * j, 128), E4M3, stages[b][0][:, start : start + 256])
+                if a == 1 and j % 2 == 1:
+                    stages[b][1]()
+
+            return [lambda b=b, a=a: (finish_tile if j < 2 else finish)(b, a) for b in range(2) for a in range(2)]
 
         wide = []
 
@@ -237,7 +244,7 @@ def tile_mla_pa_v_kernel(
             if (n, g) in split:
                 blocks = [split[(n, g)][0][:, j] for j in range(4)]
             else:
-                blocks = [words(wkv_in[n][:], WIDTH * j + 512 * g) for j in range(4)]
+                blocks = [words(wkv_in[n], WIDTH * j + 512 * g) for j in range(4)]
             finish = turn("k%d%d" % (n, g), blocks, E4M3, engines)
             if (n, g) in split:
                 split[(n, g)][1]()
@@ -252,7 +259,7 @@ def tile_mla_pa_v_kernel(
         def k_split(n, g, engine="V"):
             t, release = stage_tile()
             split[(n, g)] = t[:].rearrange("p (j u w) -> p j u w", j=4, u=2), release
-            source = wkv_in[n][:].bitcast(F32).rearrange("p (j w) -> p j w", j=4)[:, :, 256 * g : 256 * g + 256]
+            source = wkv_in[n].bitcast(F32).rearrange("p (j w) -> p j w", j=4)[:, :, 256 * g : 256 * g + 256]
             copy(engine, split[(n, g)][0], source.rearrange("p j (w u) -> p j u w", u=2))
 
         def pickers():
@@ -397,6 +404,12 @@ def tile_mla_pa_v_kernel(
                     copy(engines[place], t[:, 512 * place : 512 * place + 512], out_1_bank(4 * c + 2 * e + i, n)[:])
             nc.sync.dma_start(out=out_1_rows[:, c, i, :, 512 * first : 512 * last], in_=t[:].rearrange("p (e w) -> p e w", e=2))
 
+        def out_1_row(c, i, e, kib, engines):
+            t = out_tile(kib, WIDTH)
+            for n in range(3):
+                copy(engines[n], t[:, 512 * n : 512 * n + 512], out_1_bank(4 * c + 2 * e + i, n)[:])
+            nc.sync.dma_start(out=out_1_rows[:, c, i, e, :], in_=t[:])
+
         def out_1_rest(c, i, kib, engines):
             t = out_tile(kib, 2048)
             for place, (e, n) in enumerate([(0, 2), (1, 0), (1, 1), (1, 2)]):
@@ -456,7 +469,7 @@ def tile_mla_pa_v_kernel(
         tables()
         spread_gain()
         rotate(0)()
-        w_run(1, 0)
+        run(w_run(1, 0), 4)
         q_w = w_run(1, 1)
         q_nope = [z_run(0, 0)]
         f_run(0)
@@ -487,14 +500,13 @@ def tile_mla_pa_v_kernel(
         add()
         wk_run(2)
         wk_run(3)
-        load_wkv(0)
+        load_wkv(0, 1)
         q_nope[1]()
         q_t = [z_block(0)]
         q_v = [z_run(0, 1)]
         q_nope.append(z_run(3, 0))
         for g in range(4):
             wk_quantize(g)
-        load_wkv(1)
         q_v.append(z_run(1, 1))
         q_v[0]()
         q_f.append(f_run(3))
@@ -503,8 +515,7 @@ def tile_mla_pa_v_kernel(
         q_v.append(z_run(2, 1))
         q_v[1]()
         q_v.append(z_run(3, 1))
-        load_wkv(2)
-        load_wkv(3)
+        load_wkv(1, 3)
         q_t[1]()
         q_x = [x_block(0, "S"), x_block(1, "S")]
         q_nope[2]()
@@ -592,7 +603,8 @@ def tile_mla_pa_v_kernel(
         q_k.extend([k_run(2, 2), k_run(3, 0)])
         k_split(3, 1)
         k_split(3, 2)
-        out_1_part(3, 1, 0, 3, 76, "VVSVSV")
+        out_1_row(3, 1, 0, 136, "VVS")
+        out_1_row(3, 1, 1, 144, "VSV")
         q_k.extend([k_run(3, 1), k_run(3, 2)])
         run(q_k, 3)
         for j in range(2, 4):

@@ -447,8 +447,8 @@ def tile_mla_pa_v_kernel(
         ctx.enter_context(tc.manual_schedule())
 
         pickers()
-        nc.sync.dma_start(out=angles[0:64], in_=cos_rows)
-        nc.sync.dma_start(out=angles[64:128], in_=sin_rows)
+        nc.scalar.dma_start(out=angles[0:64], in_=cos_rows)
+        nc.scalar.dma_start(out=angles[64:128], in_=sin_rows)
         load_dk(0)
         nc.sync.dma_start(out=gain_row[0:1, :], in_=kvn_g.rearrange("(o w) -> o w", o=1))
         load_w(1, 0, 1)

from contextlib import ExitStack

import concourse.mybir as mybir
from concourse.masks import make_identity

F32 = mybir.dt.float32
BF16 = mybir.dt.bfloat16
U32 = mybir.dt.uint32
U8 = mybir.dt.uint8
E4M3 = mybir.dt.float8_e4m3fn_x4
E5M2 = mybir.dt.float8_e5m2_x4
MULT = mybir.AluOpType.mult
ADD = mybir.AluOpType.add
SUB = mybir.AluOpType.subtract

TOKENS, DIM, RANK, HEADS, HEAD = 512, 2048, 512, 16, 192
NOPE, ROPE = 2048, 1024
DK = NOPE + ROPE
FEATURES = 4096
WIDTH = ROPE + RANK
FLOPS = 2 * (TOKENS * FEATURES * RANK + 2 * TOKENS * WIDTH * DIM)
BYTES = (
    2 * (TOKENS * DIM + DIM * WIDTH + RANK * FEATURES + TOKENS * (FEATURES + ROPE) + 256 * 64 + RANK)
    + 4 * (TOKENS * RANK + 2 * TOKENS)
    + 4 * (TOKENS * DIM + DIM * WIDTH)
)

KIB = 1024
STAGE_BUFS = 10
HELPED = 9
WK_STAGE = 152


def tile_mla_pa_v_kernel(
    tc, x, wkv_a_w, wkv_a_b, kvn_g, kvn_b, wk_w, wk_b, wv_w, wv_b, cos, sin, c_lat, mu, rstd, grad_0, grad_1, out_0, out_1
):
    nc = tc.nc
    x_rows = x.flatten_outer_dims().rearrange("(p j) w -> p j w", j=4)
    grad_0_rows = grad_0.rearrange("b s h d -> (b s) (h d)").rearrange("(p j) w -> p (j w)", j=4)
    grad_1_rows = grad_1.rearrange("b s h d -> (b s) (h d)").rearrange("(p j) w -> p (j w)", j=4)
    c_lat_rows = c_lat.flatten_outer_dims().rearrange("(p j) w -> p (j w)", j=4)
    mu_rows = mu.flatten_outer_dims().rearrange("(p j) o -> p (j o)", j=4)
    rstd_rows = rstd.flatten_outer_dims().rearrange("(p j) o -> p (j o)", j=4)
    w2_rows = [w.rearrange("(p j) w -> p (j w)", j=4) for w in (wk_w, wv_w)]
    wkv_rows = wkv_a_w.rearrange("(n p j) w -> p n (j w)", p=128, j=4)
    out_0_rows = out_0.flatten_outer_dims().rearrange("(p j) w -> p j w", j=4)
    out_1_rows = out_1.rearrange("(c i p e) w -> p c i e w", i=2, p=128, e=2)
    cos_rows = cos.rearrange("(q j) w -> q (j w)", j=4)
    sin_rows = sin.rearrange("(q j) w -> q (j w)", j=4)

    with ExitStack() as ctx:
        keep = ctx.enter_context(tc.tile_pool(name="keep", bufs=1))
        shared = ctx.enter_context(tc.tile_pool(name="shared", bufs=1))
        psum = ctx.enter_context(tc.psum_pool(name="psum", bufs=1))

        def kept(name, shape, dtype):
            return keep.tile(shape, dtype, name=name, align_bytes=64)

        def placed(name, shape, dtype, kib, bufs=1):
            return shared.tile(shape, dtype, name=name, bufs=bufs, align_bytes=64, offset=int(kib * KIB))

        identity = kept("identity", [128, 128], F32)
        make_identity(nc, identity[:])
        ones = kept("ones", [128, 128], BF16)
        nc.gpsimd.memset(ones[:], 1.0)
        gain_row = kept("gain_row", [128, RANK], BF16)
        gain = kept("gain", [128, RANK], F32)
        angles = kept("angles", [128, 128], BF16)
        pick = kept("pick", [128, 3, 128], BF16)
        sin_pairs = kept("sin_pairs", [128, 256], BF16)
        mu_col = kept("mu_col", [128, 4], F32)
        rstd_col = kept("rstd_col", [128, 4], F32)
        factors = kept("factors", [128, 4, 2], F32)
        sums = kept("sums", [128, 4, 2], F32)
        means = kept("means", [128, 4, 2], F32)

        def operand(name, width, kib):
            return placed(name + "_codes", [128, width], U32, kib), placed(name + "_scales", [128, width], U8, kib + width / 256)

        RAW, TEMP, C_AT, X_AT, STAGE = 64, 112, 128, 136, 180
        dk = placed("dk", [128, 4 * DK], BF16, 0)
        w2_mx = operand("w2", 8 * RANK, 24)
        dz2_mx = operand("dz2", 4 * 8 * 128, 44)
        c_in = placed("c_in", [128, 4 * RANK], F32, C_AT)
        x_in = [placed("x_in%d" % h, [128, 4 * 1024], BF16, X_AT + 8 * h) for h in range(2)]
        x_mx = [operand("x%d" % c, 512, 152 + 2.5 * c) for c in range(4)]
        token_mx = operand("dz1_token", WIDTH, 162)
        rope_mx = operand("rope", 4 * 2 * 128, 169.5)
        dc = placed("dc", [128, 4 * RANK], BF16, 174.5)
        wkv_mx = {}
        late_mx = {}

        def cols(mx, start, width):
            return mx[0][:, start : start + width], mx[1][:, start : start + width]

        def copy(engine, out, in_):
            if engine == "V":
                nc.vector.tensor_copy(out=out, in_=in_)
            else:
                nc.scalar.copy(out=out, in_=in_)

        free_stages = [STAGE + 4 * i for i in range(STAGE_BUFS)]
        count = []

        def stage_tile(which=0):
            kib = free_stages.pop(which)
            count.append(kib)
            return placed("stage%d" % len(count), [128, 1024], F32, kib), lambda: free_stages.append(kib)

        ring = list(range(7))
        held = []

        def bank_tile(name, number=None):
            if number is None:
                number = ring.pop(0)
                ring.append(number)
            return psum.tile([128, 512], F32, name=name, tag="bank%d" % number)

        def quantize(mx, fmt, in_):
            nc.vector.quantize_mx(out=mx[0].bitcast(fmt), scales=mx[1], in_=in_.bitcast(BF16))

        def matmul_mx(out, left, left_fmt, right, right_fmt, start, stop):
            nc.tensor.matmul_mx(out=out, lhsT=left[0].bitcast(left_fmt), lhsT_scale=left[1], rhs=right[0].bitcast(right_fmt), rhs_scale=right[1], start=start, stop=stop)

        def words(rows, start):
            return rows.bitcast(F32)[:, start // 2 : start // 2 + 256].rearrange("p (w u) -> p u w", u=2)

        def transposes(name, blocks, places, engines):
            banks = []
            for b in range(len(places)):
                bank = bank_tile(name)
                banks.append(bank[:].rearrange("p (a u n) -> p a u n", a=2, u=2))
                for a in range(2):
                    for u in range(2):
                        nc.tensor.transpose(banks[b][:, a, u, :], blocks[2 * b + a][:, u, :], identity[:])
            for b in range(len(places)):
                copy(engines[b], places[b], banks[b].rearrange("p a u n -> p a n u"))

        def turn(name, blocks, fmt, engines="SS"):
            stage, release = stage_tile()
            halves = stage[:].rearrange("p (b a n u) -> p b a n u", b=2, a=2, u=2)
            transposes(name, blocks, [halves[:, b] for b in range(2)], engines)

            def finish(mx):
                quantize(mx, fmt, stage[:])
                release()

            return finish

        raw = {}

        def load_w(s, j, count):
            t = placed("w%d%d" % (s, j), [128, 2048 * count], BF16, RAW + 16 * (1 - s) + 4 * j)
            for i in range(count):
                raw[(s, j + i)] = t[:, 2048 * i : 2048 * i + 2048]
            nc.sync.dma_start(out=t[:], in_=w2_rows[s][:, 2048 * j : 2048 * (j + count)])

        grad_1_in = {}

        def load_grad_1(j, count=1):
            t = placed("grad_1_in%d" % j, [128, 2048 * count], BF16, RAW + 32 + 4 * j)
            for i in range(count):
                grad_1_in[j + i] = t[:, 2048 * i : 2048 * i + 2048]
            nc.sync.dma_start(out=t[:], in_=grad_1_rows[:, 2048 * j : 2048 * (j + count)])

        wkv_in = {}

        def load_wkv(first, count):
            t = placed("wkv_in%d" % first, [128, count * 4 * WIDTH], BF16, RAW + 12 * first)
            for n in range(count):
                wkv_in[first + n] = t[:, 4 * WIDTH * n : 4 * WIDTH * (n + 1)]
            nc.sync.dma_start(out=t[:].rearrange("p (n w) -> p n w", n=count), in_=wkv_rows[:, first : first + count])

        def load_dk(j, first=0, last=HEADS):
            part = slice(DK * j + HEAD * first, DK * j + HEAD * last)
            nc.sync.dma_start(out=dk[:, part], in_=grad_0_rows[:, part])

        def load_x(h):
            nc.sync.dma_start(out=x_in[h][:].rearrange("p (j w) -> p j w", j=4), in_=x_rows[:, :, 1024 * h : 1024 * h + 1024])

        pair = []

        def w_run(s, j):
            if j % 2 == 0:
                pair.clear()
                pair.extend([stage_tile(), stage_tile()])
            stages = list(pair)
            places = [t[:].rearrange("p (a i n u) -> p a i n u", a=2, i=2, u=2)[:, :, j % 2] for t, release in stages]
            transposes("w", [words(raw[(s, j)], 512 * g) for g in range(4)], places, "SS")

            def finish(b, a):
                quantize(cols(w2_mx, 512 * (4 * s + 2 * b + a) + 256 * (j // 2), 256), E4M3, stages[b][0][:, 512 * a : 512 * a + 512])
                if a == 1:
                    stages[b][1]()

            def finish_tile(b, a):
                start = 512 * a + 256 * (j % 2)
                quantize(cols(w2_mx, 512 * (4 * s + 2 * b + a) + 128 * j, 128), E4M3, stages[b][0][:, start : start + 256])
                if a == 1 and j % 2 == 1:
                    stages[b][1]()

            return [lambda b=b, a=a: (finish_tile if j < 2 else finish)(b, a) for b in range(2) for a in range(2)]

        wide = []

        def wk_run(j):
            if j == 0:
                wide.extend([placed("wk_stage%d" % b, [128, 2048], F32, WK_STAGE + 8 * b) for b in range(2)])
            places = [t[:].rearrange("p (a j n u) -> p a j n u", a=2, j=4, u=2)[:, :, j] for t in wide]
            transposes("w", [words(raw[(0, j)], 512 * g) for g in range(4)], places, "SS")

        def wk_quantize(g):
            quantize(cols(w2_mx, 512 * g, 512), E4M3, wide[g // 2][:, 1024 * (g % 2) : 1024 * (g % 2) + 1024])

        def z_run(j, s):
            rows, start = (grad_1_in[j], 0) if s else (dk[:], DK * j)
            finish = turn("z%d%d" % (j, s), [words(rows, start + 512 * g) for g in range(4)], E5M2)
            return lambda: finish(cols(dz2_mx, 1024 * j + 512 * s, 512))

        rope_pair = []

        def f_run(j):
            if j % 2 == 0:
                rope_pair.clear()
                rope_pair.extend(stage_tile())
            stage, release = rope_pair
            place = stage[:].rearrange("p (b a n u) -> p b a n u", b=2, a=2, u=2)[:, j % 2]
            transposes("f", [words(dk[:], DK * j + NOPE + 512 * g) for g in range(2)], [place], "S")

            def finish():
                quantize(cols(rope_mx, 512 * (j // 2), 512), E5M2, stage[:])
                release()

            return finish

        def d_run(engines):
            finish = turn("d", [words(dc[:], RANK * j) for j in range(4)], E5M2, engines)
            late_mx["latent"] = operand("latent", 4 * 128, 54)
            return lambda: finish(cols(late_mx["latent"], 0, 512))

        split = {}

        def k_run(n, g, engines="SS"):
            if (n, g) in split:
                blocks = [split[(n, g)][0][:, j] for j in range(4)]
            else:
                blocks = [words(wkv_in[n], WIDTH * j + 512 * g) for j in range(4)]
            finish = turn("k%d%d" % (n, g), blocks, E4M3, engines)
            if (n, g) in split:
                split[(n, g)][1]()

            def done():
                if n not in wkv_mx:
                    wkv_mx[n] = operand("wkv%d" % n, 3 * 512, 24 + 7.5 * n)
                finish(cols(wkv_mx[n], 512 * g, 512))

            return done

        def k_split(n, g, engine="V"):
            t, release = stage_tile()
            split[(n, g)] = t[:].rearrange("p (j u w) -> p j u w", j=4, u=2), release
            source = wkv_in[n].bitcast(F32).rearrange("p (j w) -> p j w", j=4)[:, :, 256 * g : 256 * g + 256]
            copy(engine, split[(n, g)][0], source.rearrange("p j (w u) -> p j u w", u=2))

        def pickers():
            nc.vector.memset(gain_row[:], 0.0)
            nc.vector.memset(factors[:, :, 0], 1.0 / RANK)
            nc.vector.memset(pick[:], 0.0)
            low = identity[0:64, 0:64].unsqueeze(1).to_broadcast([64, 2, 64])
            high = identity[64:128, 64:128].unsqueeze(1).to_broadcast([64, 2, 64])
            nc.vector.tensor_copy(out=pick[0:64, 0, :].rearrange("p (a q) -> p a q", a=2), in_=low)
            nc.vector.tensor_copy(out=pick[64:128, 1, :].rearrange("p (a q) -> p a q", a=2), in_=high)
            nc.vector.tensor_scalar(out=pick[64:128, 2, :].rearrange("p (a q) -> p a q", a=2), in0=high, scalar1=-1.0, scalar2=None, op0=MULT)

        table = []

        def spread(bank, which):
            for e in range(2):
                nc.tensor.matmul(bank.rearrange("p (w e) -> p w e", e=2)[:, :, e], pick[:, which[e], :], angles[:], start=True, stop=True)

        def tables():
            spare = bank_tile("sin_spare")
            bank = bank_tile("table", 7)
            spread(spare[:, 0:256], (2, 1))
            spread(bank[:, 0:256], (0, 0))
            spread(bank[:, 256:512], (2, 1))
            copy("S", sin_pairs[:], spare[:, 0:256])
            table.append(bank)

        def temp():
            return placed("temp", [128, 1024], F32, TEMP, bufs=4)

        def rotate(j):
            pairs = dk[:, DK * j : DK * j + DK].rearrange("p (h w) -> p h w", w=HEAD)[:, :, 128:HEAD]
            by_cos = temp()[:].rearrange("p (h w) -> p h w", w=64)
            stage, release = stage_tile(-1)
            by_sin = stage[:].rearrange("p (h w) -> p h w", w=64)

            def product(engine, out, heads, row):
                engine.tensor_tensor(out=out[:, heads], in0=pairs[:, heads], in1=row.unsqueeze(1).to_broadcast([128, heads.stop - heads.start, 64]), op=MULT)

            product(nc.gpsimd, by_sin, slice(0, HELPED), sin_pairs[:, 64 * j : 64 * j + 64])
            product(nc.vector, by_cos, slice(0, HEADS), table[0][:, 64 * j : 64 * j + 64])
            product(nc.vector, by_sin, slice(HELPED, HEADS), table[0][:, 256 + 64 * j : 256 + 64 * j + 64])

            def add():
                nc.vector.tensor_tensor(
                    out=pairs.rearrange("p h (w e) -> p h w e", e=2),
                    in0=by_cos.rearrange("p h (w e) -> p h w e", e=2),
                    in1=by_sin.rearrange("p h (w e) -> p h w e", e=2)[:, :, :, ::-1],
                    op=ADD,
                )
                release()

            return add

        def spread_gain():
            bank = bank_tile("gain")
            nc.tensor.matmul(bank[:], ones[:], gain_row[:], start=True, stop=True)
            copy("S", gain[:], bank[:])

        def norm_factors():
            nc.vector.scalar_tensor_tensor(out=factors[:, :, 1], in0=rstd_col[:], scalar=1.0 / RANK, in1=rstd_col[:], op0=MULT, op1=MULT)

        def dh(j):
            bank = bank_tile("dh%d" % j, held[j % 2])
            for g in range(8):
                matmul_mx(bank[:], cols(dz2_mx, 1024 * j + 128 * g, 128), E5M2, cols(w2_mx, 512 * g, 512), E4M3, g == 0, g == 7)
            part = []
            c = c_in[:, RANK * j : RANK * j + RANK]
            one = slice(j, j + 1)

            def first():
                t = temp()
                part.extend([t[:, 0:RANK], t[:, RANK : 2 * RANK]])
                nc.vector.scalar_tensor_tensor(
                    out=part[0].rearrange("p (q j) -> p q j", j=4),
                    in0=bank[:].rearrange("p (j q) -> p q j", j=4),
                    scalar=rstd_col[:, one],
                    in1=gain[:].rearrange("p (q j) -> p q j", j=4),
                    op0=MULT,
                    op1=MULT,
                    accum_out=sums[:, j, 0:1],
                )

            def second():
                nc.vector.scalar_tensor_tensor(out=part[1], in0=c, scalar=mu_col[:, one], in1=part[0], op0=SUB, op1=MULT, accum_out=sums[:, j, 1:2])

            def third():
                nc.vector.tensor_tensor(out=means[:, j, :], in0=sums[:, j, :], in1=factors[:, j, :], op=MULT)

            def fourth():
                nc.vector.tensor_scalar(out=part[1], in0=c, scalar1=mu_col[:, one], scalar2=means[:, j, 1:2], op0=SUB, op1=MULT)

            def fifth():
                nc.vector.scalar_tensor_tensor(out=dc[:, RANK * j : RANK * j + RANK], in0=part[0], scalar=means[:, j, 0:1], in1=part[1], op0=SUB, op1=SUB)

            return [first, second, third, fourth, fifth]

        def tokens_beside(source, mx, fmt, engine, order):
            stage, release = stage_tile()
            copy(engine, stage[:].bitcast(BF16).rearrange(order, r=2, e=2, j=4), source.rearrange("p j (c r e) -> p c j r e", r=2, e=2))

            def finish():
                quantize(mx, fmt, stage[:])
                release()

            return finish

        def x_block(c, engine="V"):
            return tokens_beside(x_in[c // 2][:].rearrange("p (j w) -> p j w", j=4)[:, :, 512 * (c % 2) : 512 * (c % 2) + 512], cols(x_mx[c], 0, 512), E4M3, engine, "p (e c r j) -> p c j r e")

        def z_block(n, engine="V"):
            if n < 2:
                source = dk[:].rearrange("p (j w) -> p j w", j=4)[:, :, NOPE + 512 * n : NOPE + 512 * n + 512]
            else:
                source = dc[:].rearrange("p (j w) -> p j w", j=4)
            return tokens_beside(source, cols(token_mx, 512 * n, 512), E5M2, engine, "p (c r e j) -> p c j r e")

        made = []

        def out_tile(kib, width):
            made.append(kib)
            return placed("out%d" % len(made), [128, width], F32, kib)

        def out_1_bank(m, n):
            bank = bank_tile("al%d%d" % (m, n))
            matmul_mx(bank[:], cols(x_mx[m // 4], 128 * (m % 4), 128), E4M3, cols(token_mx, 512 * n, 512), E5M2, True, True)
            return bank

        def out_0_bank(n, j):
            bank = bank_tile("o%d%d" % (n, j))
            for g in range(3):
                left = cols(rope_mx, 256 * j + 128 * g, 128) if g < 2 else cols(late_mx["latent"], 128 * j, 128)
                matmul_mx(bank[:], left, E5M2, cols(wkv_mx[n], 512 * g, 512), E4M3, g == 0, g == 2)
            return bank

        def out_1_part(c, i, first, last, kib, engines):
            count = last - first
            t = out_tile(kib, 1024 * count)
            for e in range(2):
                for n in range(first, last):
                    place = count * e + n - first
                    copy(engines[place], t[:, 512 * place : 512 * place + 512], out_1_bank(4 * c + 2 * e + i, n)[:])
            nc.sync.dma_start(out=out_1_rows[:, c, i, :, 512 * first : 512 * last], in_=t[:].rearrange("p (e w) -> p e w", e=2))

        def out_1_row(c, i, e, kib, engines):
            t = out_tile(kib, WIDTH)
            for n in range(3):
                copy(engines[n], t[:, 512 * n : 512 * n + 512], out_1_bank(4 * c + 2 * e + i, n)[:])
            nc.sync.dma_start(out=out_1_rows[:, c, i, e, :], in_=t[:])

        def out_1_rest(c, i, kib, engines):
            t = out_tile(kib, 2048)
            for place, (e, n) in enumerate([(0, 2), (1, 0), (1, 1), (1, 2)]):
                copy(engines[place], t[:, 512 * place : 512 * place + 512], out_1_bank(4 * c + 2 * e + i, n)[:])
            nc.sync.dma_start(out=out_1_rows[:, c, i].rearrange("p e w -> p (e w)")[:, ROPE : 2 * WIDTH], in_=t[:])

        def out_1_early(c, kib):
            t = out_tile(kib, 2048)

            def step(i):
                for n in range(2):
                    copy("S", t[:, 1024 * i + 512 * n : 1024 * i + 512 * n + 512], out_1_bank(4 * c + i, n)[:])
                if i == 1:
                    nc.sync.dma_start(out=out_1_rows[:, c, :, 0, 0:ROPE], in_=t[:].rearrange("p (i w) -> p i w", i=2))

            return step

        def group_0(half, first, count, kib):
            t = out_tile(kib, 1024 * count)
            rows = t[:].rearrange("p (j w) -> p j w", j=count)

            def step(j, n, engine):
                side = rows[:, j - first, 512 * n : 512 * n + 512]
                copy(engine, side.rearrange("p (q j) -> p q j", j=4), out_0_bank(2 * half + n, j)[:].rearrange("p (j q) -> p q j", j=4))

            def store(start=0, stop=1024):
                nc.sync.dma_start(out=out_0_rows[:, first : first + count, 1024 * half + start : 1024 * half + stop], in_=rows[:, :, start:stop])

            return step, store

        def run(queue, count=1):
            for i in range(count):
                queue.pop(0)()

        ctx.enter_context(tc.manual_schedule())

        pickers()
        nc.scalar.dma_start(out=angles[0:64], in_=cos_rows)
        nc.scalar.dma_start(out=angles[64:128], in_=sin_rows)
        load_dk(0)
        nc.sync.dma_start(out=gain_row[0:1, :], in_=kvn_g.rearrange("(o w) -> o w", o=1))
        load_w(1, 0, 1)
        load_w(1, 1, 1)
        load_dk(1)
        load_w(1, 2, 1)
        load_w(1, 3, 1)
        load_dk(2)
        load_w(0, 0, 1)
        load_w(0, 1, 1)
        load_dk(3)
        load_w(0, 2, 1)
        load_w(0, 3, 1)
        load_grad_1(0, 1)
        load_grad_1(1, 1)
        load_grad_1(2, 2)

        tables()
        spread_gain()
        rotate(0)()
        run(w_run(1, 0), 4)
        q_w = w_run(1, 1)
        q_nope = [z_run(0, 0)]
        f_run(0)
        add = rotate(1)
        run(q_w)
        add()
        w_run(1, 2)
        run(q_w, 3)
        q_w.extend(w_run(1, 3))
        q_nope.append(z_run(1, 0))
        q_f = [f_run(1)]
        add = rotate(2)
        run(q_w)
        add()
        wk_run(0)
        run(q_w, 3)
        wk_run(1)
        q_nope.append(z_run(2, 0))
        f_run(2)
        load_x(0)
        nc.sync.dma_start(out=mu_col[:], in_=mu_rows)
        nc.sync.dma_start(out=rstd_col[:], in_=rstd_rows)
        nc.sync.dma_start(out=c_in[:], in_=c_lat_rows)
        load_x(1)
        add = rotate(3)
        ring.append(7)
        q_nope[0]()
        add()
        wk_run(2)
        wk_run(3)
        load_wkv(0, 1)
        q_nope[1]()
        q_t = [z_block(0)]
        q_v = [z_run(0, 1)]
        q_nope.append(z_run(3, 0))
        for g in range(4):
            wk_quantize(g)
        q_v.append(z_run(1, 1))
        q_v[0]()
        q_f.append(f_run(3))
        q_t[0]()
        q_t.append(z_block(1))
        q_v.append(z_run(2, 1))
        q_v[1]()
        q_v.append(z_run(3, 1))
        load_wkv(1, 3)
        q_t[1]()
        q_x = [x_block(0, "S"), x_block(1, "S")]
        q_nope[2]()
        norm_factors()
        q_v[2]()

        held.extend([ring.pop(0), ring.pop(0)])
        norm = [dh(0), dh(1)]
        norm[0][0]()
        q_x[0]()
        norm[0][1]()
        q_nope[3]()
        norm[0][2]()
        out_1_part(0, 0, 0, 2, 0, "SSSS")
        q_x.append(x_block(2, "S"))
        norm.append(dh(2))
        norm[1][0]()
        norm[0][3]()
        norm[1][1]()
        q_v[3]()
        norm[1][2]()
        out_1_part(0, 1, 0, 2, 8, "SSSS")
        norm.append(dh(3))
        norm[0][4]()
        q_x[1]()
        norm[1][3]()
        norm[2][0]()
        norm[1][4]()
        norm[2][1]()
        early = [out_1_early(1, 16), out_1_early(2, 220)]
        q_k = [k_run(0, 0)]
        early[0](0)
        q_x[2]()
        norm[2][2]()
        norm[3][0]()
        norm[2][3]()
        norm[3][1]()
        ring.extend(held)
        q_k.append(k_run(0, 1))
        early[0](1)
        norm[2][4]()
        norm[3][2]()
        run(q_k)
        norm[3][3]()
        q_k.append(k_run(0, 2))
        early[1](0)
        norm[3][4]()
        q_t2 = z_block(2)
        q_t2()
        q_d = d_run("VV")
        early[1](1)
        run(q_k)
        q_d()
        out_1_part(0, 0, 2, 3, 112, "SS")
        out_1_part(0, 1, 2, 3, 116, "SV")
        q_f[0]()
        q_f[1]()
        run(q_k)
        out_1_rest(1, 0, 120, "SSSS")
        left = [group_0(0, 0, 2, 128), group_0(0, 2, 2, 0)]
        q_k.append(k_run(1, 0, "VS"))
        out_1_rest(1, 1, 8, "VSVV")
        for j in range(2):
            left[0][0](j, 0, "S")
        q_x.append(x_block(3))
        out_1_rest(2, 0, 64, "SSVS")
        q_k.append(k_run(1, 1))
        q_x[3]()
        run(q_k)
        out_1_rest(2, 1, 16, "VSVV")
        for j in range(2, 4):
            left[1][0](j, 0, "S")
        k_split(2, 0)
        run(q_k)
        q_k.append(k_run(1, 2))
        k_split(2, 1)
        out_1_part(3, 0, 0, 3, 112, "SVSVSV")
        run(q_k)
        q_k.extend([k_run(2, 0), k_run(2, 1)])
        k_split(2, 2)
        k_split(3, 0)
        for j in range(2):
            left[0][0](j, 1, "SV"[j])
        left[0][1]()
        q_k.extend([k_run(2, 2), k_run(3, 0)])
        k_split(3, 1)
        k_split(3, 2)
        out_1_row(3, 1, 0, 136, "VVS")
        out_1_row(3, 1, 1, 144, "VSV")
        q_k.extend([k_run(3, 1), k_run(3, 2)])
        run(q_k, 3)
        for j in range(2, 4):
            left[1][0](j, 1, "S")
        left[1][1]()
        run(q_k, 3)
        right = [group_0(1, j, 1, kib) for j, kib in enumerate((8, 12, 64, 68))]
        for j in range(2):
            right[j][0](j, 0, "S")
        for j in range(2):
            right[j][0](j, 1, "SV"[j])
            right[j][1]()
        for n in range(2):
            right[2][0](2, n, "SV"[n])
        right[2][1]()
        for n in range(2):
            right[3][0](3, n, "SV"[n])
            right[3][1](512 * n, 512 * n + 512)
